import numpy as np
import ml_dtypes


def mxq(x, axis, fmt="e4m3"):
    dtype, down = {"e4m3": (ml_dtypes.float8_e4m3fn, 7), "e5m2": (ml_dtypes.float8_e5m2, 14)}[fmt]
    v = np.moveaxis(np.asarray(x, np.float32).astype(ml_dtypes.bfloat16).astype(np.float64), axis, -1)
    blocks = v.reshape(v.shape[:-1] + (-1, 32))
    amax = np.abs(blocks).max(-1, keepdims=True)
    byte = np.maximum(np.where(amax > 0, np.frexp(amax)[1] - 1 + 127, 0) - down, 1)
    scale = np.exp2(byte - 127.0)
    codes = (blocks / scale).astype(np.float32).astype(dtype).astype(np.float64)
    return np.moveaxis((codes * scale).reshape(v.shape), -1, axis)


WIDE = False


def mx_kscale(k):
    if not WIDE:
        return np.ones(k)
    levels = np.array([10, -10, 5, -5, 0])
    a = np.random.permutation(np.resize(levels, k // 512 * 4)).reshape(k // 512, 4)
    idx = np.arange(k)
    return np.exp2(a[idx // 512, idx % 128 // 32])


BF16 = ml_dtypes.bfloat16


def bf(x):
    return np.asarray(x, np.float32).astype(BF16)


def f64(x):
    return np.asarray(x).astype(np.float64)


B, H, W, D, C, L = 1, 16, 16, 16, 512, 16
G = C // L
LC = C // G
H1, W1 = H // L, W // L
L2 = L * L


def setup_inputs():
    s = mx_kscale(C)
    sn = (s / s.max()).reshape(L, G)
    x = np.random.standard_normal((B, H1, L, W, D, LC, G)) * sn[:, None, None, None, :]
    wsc = 1.0 / np.sqrt(C)
    return {"x": bf(x.reshape(B, H, W, D, C)),
            "W_h": bf(np.random.standard_normal((C, C)) * 0.6 * wsc / sn.reshape(C)[:, None]), "b_h": bf(np.random.standard_normal(C) * 0.2),
            "W_w": bf(np.random.standard_normal((C, C)) * 0.6 * wsc), "b_w": bf(np.random.standard_normal(C) * 0.2),
            "W_c": bf(np.random.standard_normal((C, C)) * 0.6 * wsc), "b_c": bf(np.random.standard_normal(C) * 0.2),
            "W_attn": bf(np.random.standard_normal((L2, L2)) * 0.5 / np.sqrt(L2)), "b_attn": bf(np.random.standard_normal(L2) * 0.2),
            "W_1": bf(np.random.standard_normal((C, C)) * 0.8 * wsc), "b_1": bf(np.random.standard_normal(C) * 0.2)}


def reference(x, W_h, b_h, W_w, b_w, W_c, b_c, W_attn, b_attn, W_1, b_1):
    x = f64(x)
    xa = x.reshape(B, H1, L, W1, L, D, C).transpose(0, 1, 3, 5, 6, 2, 4).reshape(B, H1, W1, D, C, L2)
    xa = xa @ f64(W_attn) + f64(b_attn)
    x_att = xa.reshape(B, H1, W1, D, C, L, L).transpose(0, 1, 5, 2, 6, 3, 4).reshape(B, H, W, D, C)
    xh = x.reshape(B, H1, L, W, D, LC, G).transpose(0, 1, 3, 5, 4, 2, 6).reshape(B, H1 * W, LC, D, L * G)
    xh = (mxq(xh, 4, "e4m3") @ mxq(f64(W_h), 0, "e4m3")) + f64(b_h)
    x_h = xh.reshape(B, H1, W, LC, D, L, G).transpose(0, 1, 5, 2, 4, 3, 6).reshape(B, H, W, D, C)
    xw = x.reshape(B, H, W1, L, D, LC, G).transpose(0, 1, 2, 5, 4, 3, 6).reshape(B, H * W1, LC, D, L * G)
    xw = (mxq(xw, 4, "e4m3") @ mxq(f64(W_w), 0, "e4m3")) + f64(b_w)
    x_w = xw.reshape(B, H, W1, LC, D, L, G).transpose(0, 1, 2, 5, 4, 3, 6).reshape(B, H, W, D, C)
    x_c = (mxq(x, 4, "e4m3") @ mxq(f64(W_c), 0, "e4m3")) + f64(b_c)
    hid = (1.0 + x_att) * (x_h + x_w + x_c)
    return x + ((mxq(hid, 4, "e4m3") @ mxq(f64(W_1), 0, "e4m3")) + f64(b_1))

@@ -1,0 +1,341 @@
+from contextlib import ExitStack
+
+import concourse.mybir as mybir
+from concourse.masks import make_identity
+
+F32 = mybir.dt.float32
+BF16 = mybir.dt.bfloat16
+U32 = mybir.dt.uint32
+U8 = mybir.dt.uint8
+FP8X4 = mybir.dt.float8_e4m3fn_x4
+ADD = mybir.AluOpType.add
+MULT = mybir.AluOpType.mult
+
+P = 128
+C = 512
+FLOPS = 4 * 2 * 4096 * 512 * 512 + 2 * 8192 * 256 * 256
+
+
+def tile_mlpp_pa_kernel(tc, x, W_h, b_h, W_w, b_w, W_c, b_c, W_attn, b_attn, W_1, b_1, out):
+    nc = tc.nc
+    with ExitStack() as ctx:
+        consts = ctx.enter_context(tc.tile_pool(name="consts", bufs=1))
+        xsp = ctx.enter_context(tc.tile_pool(name="xsp", bufs=2))
+        one = ctx.enter_context(tc.tile_pool(name="one", bufs=1))
+        two = ctx.enter_context(tc.tile_pool(name="two", bufs=2))
+        three = ctx.enter_context(tc.tile_pool(name="three", bufs=3))
+        ps_tp = ctx.enter_context(tc.psum_pool(name="ps_tp", bufs=3))
+        ps_mx = ctx.enter_context(tc.psum_pool(name="ps_mx", bufs=3))
+        ps_at = ctx.enter_context(tc.psum_pool(name="ps_at", bufs=2))
+
+        xnv = x.rearrange("b (k h) w d c -> k (b h w) (d c)", k=2)
+        x1v = x.rearrange("b h w (a e) c -> (b w a) h e c", e=2)
+        x2v = x.rearrange("b h w (a e) c -> (b h) w a e c", e=2)
+        outv = out.rearrange("b (k h) w d c -> k (b h w) d c", k=2)
+
+        ident_f = consts.tile([P, P], F32, tag="ident_f")
+        make_identity(nc, ident_f[:])
+        ident_b = consts.tile([P, P], BF16, tag="ident_b")
+        make_identity(nc, ident_b[:])
+
+        wraw = one.tile([P, 8192], BF16, tag="s2", align_bytes=64)
+        wrv = wraw[:].rearrange("p (i t n) -> p i t n", i=4, t=4, n=C)
+        wg = two.tile([P, 8192], BF16, tag="a", align_bytes=64)
+        wgv = wg[:].rearrange("p (i n t) -> p i n t", i=4, n=C, t=4)
+        wcodes = consts.tile([P, 2048], U32, tag="wcodes", align_bytes=64)
+        wscl = consts.tile([P, 2048], U8, tag="wscl", align_bytes=64)
+        for i, w_ap in enumerate((W_h, W_w, W_c)):
+            for u in range(2):
+                nc.scalar.dma_start(
+                    out=wrv[:, i, 2 * u : 2 * u + 2, :],
+                    in_=w_ap[256 * u : 256 * u + 256, :].rearrange("(q e) n -> q e n", e=2),
+                )
+        nc.scalar.dma_start(out=wrv[:, 3, :, :], in_=W_1.rearrange("(t p) n -> p t n", p=P))
+
+        def weight_prep(i, eng_copy):
+            eng_copy(out=wgv[:, i], in_=wrv[:, i].rearrange("p t n -> p n t"))
+
+        def weight_quant(i):
+            nc.vector.quantize_mx(
+                out=wcodes[:, i * C : (i + 1) * C].bitcast(FP8X4),
+                scales=wscl[:, i * C : (i + 1) * C],
+                in_=wg[:, i * 2048 : (i + 1) * 2048],
+            )
+
+        weight_prep(0, nc.vector.tensor_copy)
+        weight_prep(1, nc.vector.tensor_copy)
+        weight_prep(2, nc.scalar.copy)
+        weight_prep(3, nc.scalar.copy)
+        for i in range(4):
+            weight_quant(i)
+
+        def wslice(i, c0, n):
+            return (
+                wcodes[:, i * C + c0 : i * C + c0 + n].bitcast(FP8X4),
+                wscl[:, i * C + c0 : i * C + c0 + n],
+            )
+
+        wattn = consts.tile([P, 2, 256], BF16, tag="wattn")
+        nc.scalar.dma_start(out=wattn[:], in_=W_attn.rearrange("(k p) n -> p k n", p=P))
+        b1bc = consts.tile([P, C], BF16, tag="b1bc")
+        nc.scalar.dma_start(out=b1bc[:], in_=b_1.partition_broadcast(P))
+        bcbc = consts.tile([P, C], BF16, tag="bcbc")
+        nc.scalar.dma_start(out=bcbc[:], in_=b_c.partition_broadcast(P))
+        tb = consts.tile([P, 32], BF16, tag="tb")
+        nc.vector.memset(tb[:], 0.0)
+        nc.scalar.dma_start(out=tb[0:16, :], in_=b_w.rearrange("(w g) -> w g", g=32))
+        nc.scalar.dma_start(out=tb[16:32, :], in_=b_h.rearrange("(h g) -> h g", g=32))
+        tba = consts.tile([P, P], BF16, tag="tba")
+        nc.vector.memset(tba[:], 0.0)
+        nc.scalar.dma_start(out=tba[0:2, :], in_=b_attn.rearrange("(k p) -> k p", p=P))
+
+        def input_stage(which, dlo):
+            rl = one.tile([P, 8192], BF16, tag="rl")
+            rl4 = rl[:].rearrange("p (l y g) -> p l y g", l=16, y=16, g=32)
+            for q in range(2):
+                xs = xsp.tile([P, 8, C], BF16, tag="xs")
+                if which == 0:
+                    nc.sync.dma_start(out=xs[:], in_=x1v[:, 8 * q : 8 * q + 8, dlo, :])
+                else:
+                    for a8 in range(8):
+                        nc.sync.dma_start(
+                            out=xs[16 * a8 : 16 * a8 + 16, :, :], in_=x2v[:, 8 * q : 8 * q + 8, a8, dlo, :]
+                        )
+                nc.vector.tensor_copy(
+                    out=rl4[:, :, 8 * q : 8 * q + 8, :],
+                    in_=xs[:].rearrange("p y (l g) -> p l y g", l=16, g=32),
+                )
+            rlw = rl[:].bitcast(F32)
+            gr = two.tile([P, 8192], BF16, tag="gr", align_bytes=64)
+            grw = gr[:].bitcast(F32).rearrange("p (y l a u) -> p y l a u", y=16, l=16, a=8, u=2)
+            for lp in range(8):
+                pt = ps_tp.tile([P, C], F32, tag="tp")
+                for li in range(2):
+                    for u in range(2):
+                        w0 = (2 * lp + li) * 256 + u * P
+                        s0 = (2 * li + u) * P
+                        nc.tensor.transpose(pt[:, s0 : s0 + P], rlw[:, w0 : w0 + P], ident_f[:])
+                for li in range(2):
+                    half_bank = pt[:, li * 256 : (li + 1) * 256]
+                    if which == 0:
+                        src = half_bank.rearrange("p (u y a) -> p y a u", u=2, y=16, a=8)
+                    else:
+                        src = half_bank.rearrange("p (u a y) -> p y a u", u=2, y=16, a=8)
+                    nc.scalar.copy(out=grw[:, :, 2 * lp + li, :, :], in_=src)
+            if which == 0:
+                codes = one.tile([P, 2048], U32, tag="ch", align_bytes=64)
+                scl = one.tile([P, 2048], U8, tag="sh", align_bytes=64)
+            else:
+                codes = one.tile([P, 2048], U32, tag="cw", align_bytes=64)
+                scl = one.tile([P, 2048], U8, tag="sw", align_bytes=64)
+            for qn in range(2):
+                nc.vector.quantize_mx(
+                    out=codes[:, qn * 1024 : (qn + 1) * 1024].bitcast(FP8X4),
+                    scales=scl[:, qn * 1024 : (qn + 1) * 1024],
+                    in_=gr[:, qn * 4096 : (qn + 1) * 4096],
+                )
+            return codes, scl
+
+        ch0 = input_stage(0, 0)
+        cw0 = input_stage(1, 0)
+
+        xn = []
+        for k in range(2):
+            xnk = consts.tile([P, 8192], BF16, name="xn%d" % k, tag="xn%d" % k)
+            for j in range(2):
+                nc.sync.dma_start(out=xnk[:, j * 4096 : (j + 1) * 4096], in_=xnv[k][:, j * 4096 : (j + 1) * 4096])
+            xn.append(xnk)
+
+        tbx = consts.tile([P, 16, 32], BF16, tag="tbx")
+        nc.vector.tensor_copy(out=tbx[:], in_=tb[:].unsqueeze(1).to_broadcast([P, 16, 32]))
+        selw = consts.tile([P, 8, 16], BF16, tag="selw")
+        nc.vector.tensor_copy(out=selw[:], in_=ident_b[:, 0:16].unsqueeze(1).to_broadcast([P, 8, 16]))
+        bias_n = consts.tile([P, 2, C], F32, tag="bias_n")
+        for hh in range(2):
+            sel = consts.tile([P, 8, 16], BF16, name="sel%d" % hh, tag="sel%d" % hh)
+            nc.vector.tensor_tensor(
+                out=sel[:],
+                in0=selw[:],
+                in1=ident_b[:, 16 + 8 * hh : 24 + 8 * hh].unsqueeze(2).to_broadcast([P, 8, 16]),
+                op=ADD,
+            )
+            pb = ps_at.tile([P, C], F32, tag="at")
+            nc.tensor.matmul(
+                out=pb[:],
+                lhsT=sel[:].rearrange("p a w -> p (a w)"),
+                rhs=tbx[:].rearrange("p l g -> p (l g)"),
+                start=True,
+                stop=True,
+            )
+            nc.vector.tensor_tensor(out=bias_n[:, hh, :], in0=pb[:], in1=bcbc[:], op=ADD)
+        pta = ps_tp.tile([P, P], BF16, tag="tp")
+        nc.tensor.transpose(pta[:], tba[:], ident_b[:])
+        ap1 = consts.tile([P, 2], F32, tag="ap1")
+        nc.vector.tensor_scalar_add(out=ap1[:], in0=pta[:, 0:2], scalar1=1.0)
+
+        def xc_stage(dlo, hh):
+            cc = two.tile([P, 1024], U32, tag="cc", align_bytes=64)
+            sc = two.tile([P, 1024], U8, tag="sc", align_bytes=64)
+            xw32 = xn[hh][:].bitcast(F32)
+            for half in range(2):
+                gc = one.tile([P, 2048], BF16, tag="gc", align_bytes=64)
+                gcw = gc[:].bitcast(F32)
+                for pr in range(2):
+                    pt = ps_tp.tile([P, C], F32, tag="tp")
+                    for i in range(2):
+                        d = 2 * (half * 4 + pr * 2 + i) + dlo
+                        for u in range(2):
+                            s0 = (2 * i + u) * P
+                            nc.tensor.transpose(
+                                pt[:, s0 : s0 + P], xw32[:, d * 256 + u * P : d * 256 + (u + 1) * P], ident_f[:]
+                            )
+                    nc.scalar.copy(
+                        out=gcw[:, pr * C : (pr + 1) * C].rearrange("p (i r u) -> p i r u", i=2, r=P, u=2),
+                        in_=pt[:].rearrange("p (i u r) -> p i r u", i=2, u=2, r=P),
+                    )
+                nc.vector.quantize_mx(
+                    out=cc[:, half * C : (half + 1) * C].bitcast(FP8X4),
+                    scales=sc[:, half * C : (half + 1) * C],
+                    in_=gc[:],
+                )
+            return cc, sc
+
+        def beta(hh, chs, cws):
+            ch, sh = chs
+            cw, sw = cws
+            s2 = one.tile([P, 4096], F32, tag="s2", align_bytes=64)
+            s2v = s2[:].rearrange("p (g h w) -> p g h w", g=32, h=8, w=16)
+            for hb in range(2):
+                rc, rs = wslice(0, hh * 256 + hb * P, P)
+                for wb in range(4):
+                    ph = ps_mx.tile([P, C], F32, tag="mx")
+                    for wi in range(4):
+                        w = 4 * wb + wi
+                        nc.tensor.matmul_mx(
+                            out=ph[:, wi * P : (wi + 1) * P],
+                            lhsT=ch[:, w * P : (w + 1) * P].bitcast(FP8X4),
+                            lhsT_scale=sh[:, w * P : (w + 1) * P],
+                            rhs=rc,
+                            rhs_scale=rs,
+                            start=True,
+                            stop=True,
+                        )
+                    nc.scalar.copy(
+                        out=s2v[:, :, 4 * hb : 4 * hb + 4, 4 * wb : 4 * wb + 4],
+                        in_=ph[:].rearrange("p (w h g) -> p g h w", w=4, h=4, g=32),
+                    )
+            rc, rs = wslice(1, 0, C)
+            for h8 in range(8):
+                h = 8 * hh + h8
+                pw = ps_mx.tile([P, C], F32, tag="mx")
+                nc.tensor.matmul_mx(
+                    out=pw[:],
+                    lhsT=cw[:, h * P : (h + 1) * P].bitcast(FP8X4),
+                    lhsT_scale=sw[:, h * P : (h + 1) * P],
+                    rhs=rc,
+                    rhs_scale=rs,
+                    start=True,
+                    stop=True,
+                )
+                nc.vector.tensor_tensor(
+                    out=s2v[:, :, h8, :],
+                    in0=pw[:].rearrange("p (w g) -> p g w", w=16, g=32),
+                    in1=s2v[:, :, h8, :],
+                    op=ADD,
+                )
+            a = two.tile([P, 4096], F32, tag="a", align_bytes=64)
+            av = a[:].rearrange("p (a l g) -> p a l g", a=8, l=16, g=32)
+            for gb in range(8):
+                pst = ps_tp.tile([P, C], F32, tag="tp")
+                for gi in range(4):
+                    g = 4 * gb + gi
+                    nc.tensor.transpose(pst[:, gi * P : (gi + 1) * P], s2[:, g * P : (g + 1) * P], ident_f[:])
+                nc.scalar.copy(
+                    out=av[:, :, :, 4 * gb : 4 * gb + 4],
+                    in_=pst[:].rearrange("p (g l a) -> p a l g", g=4, l=16, a=8),
+                )
+            for d8 in range(8):
+                nc.gpsimd.tensor_tensor(
+                    out=a[:, d8 * C : (d8 + 1) * C], in0=a[:, d8 * C : (d8 + 1) * C], in1=bias_n[:, hh, :], op=ADD
+                )
+            return a
+
+        def gamma(dlo, hh, a, ccs):
+            cc, sc = ccs
+            wc_c, wc_s = wslice(2, 0, C)
+            w1_c, w1_s = wslice(3, 0, C)
+            for half in range(2):
+                ghid = one.tile([P, 2048], BF16, tag="ghid", align_bytes=64)
+                for pr in range(2):
+                    hidn = three.tile([P, 2, C], BF16, tag="hidn")
+                    for i in range(2):
+                        d8 = half * 4 + pr * 2 + i
+                        d = 2 * d8 + dlo
+                        pc = ps_mx.tile([P, C], F32, tag="mx")
+                        nc.tensor.matmul_mx(
+                            out=pc[:],
+                            lhsT=cc[:, d8 * P : (d8 + 1) * P].bitcast(FP8X4),
+                            lhsT_scale=sc[:, d8 * P : (d8 + 1) * P],
+                            rhs=wc_c,
+                            rhs_scale=wc_s,
+                            start=True,
+                            stop=True,
+                        )
+                        pa = ps_at.tile([P, C], F32, tag="at")
+                        for k in range(2):
+                            nc.tensor.matmul(
+                                out=pa[:],
+                                lhsT=wattn[:, k, hh * P : (hh + 1) * P],
+                                rhs=xn[k][:, d * C : (d + 1) * C],
+                                start=(k == 0),
+                                stop=(k == 1),
+                            )
+                        bsum = two.tile([P, C], F32, tag="bsum")
+                        nc.vector.tensor_tensor(out=bsum[:], in0=pc[:], in1=a[:, d8 * C : (d8 + 1) * C], op=ADD)
+                        nc.vector.scalar_tensor_tensor(
+                            out=hidn[:, i, :], in0=pa[:], scalar=ap1[:, hh : hh + 1], in1=bsum[:], op0=ADD, op1=MULT
+                        )
+                    pht = ps_tp.tile([P, 1024], BF16, tag="tp")
+                    for i in range(2):
+                        for t in range(4):
+                            s0 = (4 * i + t) * P
+                            nc.tensor.transpose(pht[:, s0 : s0 + P], hidn[:, i, t * P : (t + 1) * P], ident_b[:])
+                    nc.scalar.copy(
+                        out=ghid[:, pr * 1024 : (pr + 1) * 1024].rearrange("p (i r t) -> p i r t", i=2, r=P, t=4),
+                        in_=pht[:].rearrange("p (i t r) -> p i r t", i=2, t=4, r=P),
+                    )
+                chid = two.tile([P, C], U32, tag="chid", align_bytes=64)
+                shid = two.tile([P, C], U8, tag="shid", align_bytes=64)
+                nc.vector.quantize_mx(out=chid[:].bitcast(FP8X4), scales=shid[:], in_=ghid[:])
+                for j in range(4):
+                    d = 2 * (half * 4 + j) + dlo
+                    xpb = three.tile([P, C], F32, tag="xpb")
+                    nc.gpsimd.tensor_tensor(out=xpb[:], in0=xn[hh][:, d * C : (d + 1) * C], in1=b1bc[:], op=ADD)
+                    pf = ps_mx.tile([P, C], F32, tag="mx")
+                    nc.tensor.matmul_mx(
+                        out=pf[:],
+                        lhsT=chid[:, j * P : (j + 1) * P].bitcast(FP8X4),
+                        lhsT_scale=shid[:, j * P : (j + 1) * P],
+                        rhs=w1_c,
+                        rhs_scale=w1_s,
+                        start=True,
+                        stop=True,
+                    )
+                    o = three.tile([P, C], F32, tag="o")
+                    nc.vector.tensor_tensor(out=o[:], in0=pf[:], in1=xpb[:], op=ADD)
+                    nc.sync.dma_start(out=outv[hh][:, d, :], in_=o[:])
+
+        cc00 = xc_stage(0, 0)
+        a00 = beta(0, ch0, cw0)
+        cc01 = xc_stage(0, 1)
+        a01 = beta(1, ch0, cw0)
+        ch1 = input_stage(0, 1)
+        cw1 = input_stage(1, 1)
+        gamma(0, 0, a00, cc00)
+        cc10 = xc_stage(1, 0)
+        a10 = beta(0, ch1, cw1)
+        gamma(0, 1, a01, cc01)
+        cc11 = xc_stage(1, 1)
+        a11 = beta(1, ch1, cw1)
+        gamma(1, 0, a10, cc10)
+        gamma(1, 1, a11, cc11)

@@ -24,33 +24,67 @@ def tile_mlpp_pa_kernel(tc, x, W_h, b_h, W_w, b_w, W_c, b_c, W_attn, b_attn, W_1
         one = ctx.enter_context(tc.tile_pool(name="one", bufs=1))
         two = ctx.enter_context(tc.tile_pool(name="two", bufs=2))
         three = ctx.enter_context(tc.tile_pool(name="three", bufs=3))
-        ps_tp = ctx.enter_context(tc.psum_pool(name="ps_tp", bufs=3))
-        ps_mx = ctx.enter_context(tc.psum_pool(name="ps_mx", bufs=3))
-        ps_at = ctx.enter_context(tc.psum_pool(name="ps_at", bufs=2))
+        ps1 = ctx.enter_context(tc.psum_pool(name="ps1", bufs=1))
+        ps2 = ctx.enter_context(tc.psum_pool(name="ps2", bufs=2))
+
+        def bank(tag, dtype=F32, cols=C):
+            if tag in ("pc", "pf"):
+                t = ps1.tile([P, cols], dtype, name="bk_" + tag, tag=tag)
+            else:
+                t = ps2.tile([P, cols], dtype, name="bk_" + tag, tag=tag)
+            return t
 
         xnv = x.rearrange("b (k h) w d c -> k (b h w) (d c)", k=2)
         x1v = x.rearrange("b h w (a e) c -> (b w a) h e c", e=2)
         x2v = x.rearrange("b h w (a e) c -> (b h) w a e c", e=2)
         outv = out.rearrange("b (k h) w d c -> k (b h w) d c", k=2)
 
+        st = {}
+
         ident_f = consts.tile([P, P], F32, tag="ident_f")
         make_identity(nc, ident_f[:])
         ident_b = consts.tile([P, P], BF16, tag="ident_b")
         make_identity(nc, ident_b[:])
 
-        wraw = one.tile([P, 8192], BF16, tag="s2", align_bytes=64)
+        def load_x2_first():
+            xbig = two.tile([P, 16, C], BF16, tag="xn", align_bytes=64)
+            for q in range(2):
+                for a8 in range(8):
+                    nc.sync.dma_start(
+                        out=xbig[16 * a8 : 16 * a8 + 16, 8 * q : 8 * q + 8, :], in_=x2v[:, 8 * q : 8 * q + 8, a8, 0, :]
+                    )
+                st["xs", 1, 0, q] = xbig[:, 8 * q : 8 * q + 8, :]
+
+        def load_xs(which, dlo, q):
+            xs = xsp.tile([P, 8, C], BF16, tag="xs")
+            if which == 0:
+                nc.sync.dma_start(out=xs[:], in_=x1v[:, 8 * q : 8 * q + 8, dlo, :])
+            else:
+                for a8 in range(8):
+                    nc.sync.dma_start(out=xs[16 * a8 : 16 * a8 + 16, :, :], in_=x2v[:, 8 * q : 8 * q + 8, a8, dlo, :])
+            st["xs", which, dlo, q] = xs[:]
+
+        wraw = two.tile([P, 8192], BF16, tag="xn", align_bytes=64)
         wrv = wraw[:].rearrange("p (i t n) -> p i t n", i=4, t=4, n=C)
         wg = two.tile([P, 8192], BF16, tag="a", align_bytes=64)
         wgv = wg[:].rearrange("p (i n t) -> p i n t", i=4, n=C, t=4)
         wcodes = consts.tile([P, 2048], U32, tag="wcodes", align_bytes=64)
         wscl = consts.tile([P, 2048], U8, tag="wscl", align_bytes=64)
-        for i, w_ap in enumerate((W_h, W_w, W_c)):
+
+        def load_w(i, w_ap):
             for u in range(2):
-                nc.scalar.dma_start(
+                nc.sync.dma_start(
                     out=wrv[:, i, 2 * u : 2 * u + 2, :],
                     in_=w_ap[256 * u : 256 * u + 256, :].rearrange("(q e) n -> q e n", e=2),
                 )
-        nc.scalar.dma_start(out=wrv[:, 3, :, :], in_=W_1.rearrange("(t p) n -> p t n", p=P))
+
+        load_xs(0, 0, 0)
+        load_xs(0, 0, 1)
+        load_x2_first()
+        load_w(0, W_h)
+        load_w(1, W_w)
+        load_w(2, W_c)
+        nc.sync.dma_start(out=wrv[:, 3, :, :], in_=W_1.rearrange("(t p) n -> p t n", p=P))
 
         def weight_prep(i, eng_copy):
             eng_copy(out=wgv[:, i], in_=wrv[:, i].rearrange("p t n -> p n t"))
@@ -61,13 +95,6 @@ def tile_mlpp_pa_kernel(tc, x, W_h, b_h, W_w, b_w, W_c, b_c, W_attn, b_attn, W_1
                 scales=wscl[:, i * C : (i + 1) * C],
                 in_=wg[:, i * 2048 : (i + 1) * 2048],
             )
-
-        weight_prep(0, nc.vector.tensor_copy)
-        weight_prep(1, nc.vector.tensor_copy)
-        weight_prep(2, nc.scalar.copy)
-        weight_prep(3, nc.scalar.copy)
-        for i in range(4):
-            weight_quant(i)
 
         def wslice(i, c0, n):
             return (
@@ -89,62 +116,340 @@ def tile_mlpp_pa_kernel(tc, x, W_h, b_h, W_w, b_w, W_c, b_c, W_attn, b_attn, W_1
         nc.vector.memset(tba[:], 0.0)
         nc.scalar.dma_start(out=tba[0:2, :], in_=b_attn.rearrange("(k p) -> k p", p=P))
 
-        def input_stage(which, dlo):
-            rl = one.tile([P, 8192], BF16, tag="rl")
+        def in_relayout(which, dlo, q):
+            if q == 0:
+                rl = one.tile([P, 8192], BF16, tag="rl")
+                st["rl", which, dlo] = rl
+            rl = st["rl", which, dlo]
             rl4 = rl[:].rearrange("p (l y g) -> p l y g", l=16, y=16, g=32)
-            for q in range(2):
-                xs = xsp.tile([P, 8, C], BF16, tag="xs")
-                if which == 0:
-                    nc.sync.dma_start(out=xs[:], in_=x1v[:, 8 * q : 8 * q + 8, dlo, :])
-                else:
-                    for a8 in range(8):
-                        nc.sync.dma_start(
-                            out=xs[16 * a8 : 16 * a8 + 16, :, :], in_=x2v[:, 8 * q : 8 * q + 8, a8, dlo, :]
-                        )
-                nc.vector.tensor_copy(
-                    out=rl4[:, :, 8 * q : 8 * q + 8, :],
-                    in_=xs[:].rearrange("p y (l g) -> p l y g", l=16, g=32),
-                )
-            rlw = rl[:].bitcast(F32)
-            gr = two.tile([P, 8192], BF16, tag="gr", align_bytes=64)
-            grw = gr[:].bitcast(F32).rearrange("p (y l a u) -> p y l a u", y=16, l=16, a=8, u=2)
-            for lp in range(8):
-                pt = ps_tp.tile([P, C], F32, tag="tp")
-                for li in range(2):
-                    for u in range(2):
-                        w0 = (2 * lp + li) * 256 + u * P
-                        s0 = (2 * li + u) * P
-                        nc.tensor.transpose(pt[:, s0 : s0 + P], rlw[:, w0 : w0 + P], ident_f[:])
-                for li in range(2):
-                    half_bank = pt[:, li * 256 : (li + 1) * 256]
-                    if which == 0:
-                        src = half_bank.rearrange("p (u y a) -> p y a u", u=2, y=16, a=8)
-                    else:
-                        src = half_bank.rearrange("p (u a y) -> p y a u", u=2, y=16, a=8)
-                    nc.scalar.copy(out=grw[:, :, 2 * lp + li, :, :], in_=src)
-            if which == 0:
-                codes = one.tile([P, 2048], U32, tag="ch", align_bytes=64)
-                scl = one.tile([P, 2048], U8, tag="sh", align_bytes=64)
-            else:
-                codes = one.tile([P, 2048], U32, tag="cw", align_bytes=64)
-                scl = one.tile([P, 2048], U8, tag="sw", align_bytes=64)
-            for qn in range(2):
-                nc.vector.quantize_mx(
-                    out=codes[:, qn * 1024 : (qn + 1) * 1024].bitcast(FP8X4),
-                    scales=scl[:, qn * 1024 : (qn + 1) * 1024],
-                    in_=gr[:, qn * 4096 : (qn + 1) * 4096],
-                )
-            return codes, scl
+            xs = st["xs", which, dlo, q]
+            nc.vector.tensor_copy(
+                out=rl4[:, :, 8 * q : 8 * q + 8, :], in_=xs.rearrange("p y (l g) -> p l y g", l=16, g=32)
+            )
 
-        ch0 = input_stage(0, 0)
-        cw0 = input_stage(1, 0)
+        def in_transpose(which, dlo, lp, tag):
+            rlw = st["rl", which, dlo][:].bitcast(F32)
+            pt = bank(tag)
+            for li in range(2):
+                for u in range(2):
+                    w0 = (2 * lp + li) * 256 + u * P
+                    s0 = (2 * li + u) * P
+                    nc.tensor.transpose(pt[:, s0 : s0 + P], rlw[:, w0 : w0 + P], ident_f[:])
+            st["pt", which, dlo, lp] = pt
+
+        def in_evac(which, dlo, lp, copies):
+            if lp == 0:
+                gr = two.tile([P, 8192], BF16, tag="gr", align_bytes=64)
+                st["gr", which, dlo] = gr
+            gr = st["gr", which, dlo]
+            grw = gr[:].bitcast(F32).rearrange("p (y l a u) -> p y l a u", y=16, l=16, a=8, u=2)
+            pt = st["pt", which, dlo, lp]
+            for li in range(2):
+                half_bank = pt[:, li * 256 : (li + 1) * 256]
+                if which == 0:
+                    src = half_bank.rearrange("p (u y a) -> p y a u", u=2, y=16, a=8)
+                else:
+                    src = half_bank.rearrange("p (u a y) -> p y a u", u=2, y=16, a=8)
+                copies[li](out=grw[:, :, 2 * lp + li, :, :], in_=src)
+
+        def in_quant(which, dlo, qn):
+            if qn == 0:
+                if which == 0:
+                    codes = one.tile([P, 2048], U32, tag="ch", align_bytes=64)
+                    scl = one.tile([P, 2048], U8, tag="sh", align_bytes=64)
+                else:
+                    codes = one.tile([P, 2048], U32, tag="cw", align_bytes=64)
+                    scl = one.tile([P, 2048], U8, tag="sw", align_bytes=64)
+                st["codes", which, dlo] = (codes, scl)
+            codes, scl = st["codes", which, dlo]
+            nc.vector.quantize_mx(
+                out=codes[:, qn * 1024 : (qn + 1) * 1024].bitcast(FP8X4),
+                scales=scl[:, qn * 1024 : (qn + 1) * 1024],
+                in_=st["gr", which, dlo][:, qn * 4096 : (qn + 1) * 4096],
+            )
+
+        def input_steps(which, dlo, tags, copies):
+            steps = []
+            steps.append(lambda: in_relayout(which, dlo, 0))
+            steps.append(lambda: in_relayout(which, dlo, 1))
+            steps.append(lambda: in_transpose(which, dlo, 0, tags[0]))
+            for lp in range(1, 8):
+                steps.append(lambda lp=lp: (in_transpose(which, dlo, lp, tags[lp % len(tags)]), in_evac(which, dlo, lp - 1, copies)))
+            steps.append(lambda: in_evac(which, dlo, 7, copies))
+            steps.append(lambda: in_quant(which, dlo, 0))
+            steps.append(lambda: in_quant(which, dlo, 1))
+            return steps
 
         xn = []
-        for k in range(2):
-            xnk = consts.tile([P, 8192], BF16, name="xn%d" % k, tag="xn%d" % k)
-            for j in range(2):
-                nc.sync.dma_start(out=xnk[:, j * 4096 : (j + 1) * 4096], in_=xnv[k][:, j * 4096 : (j + 1) * 4096])
-            xn.append(xnk)
+
+        def load_xn():
+            for k in range(2):
+                xnk = two.tile([P, 8192], BF16, name="xn%d" % k, tag="xn", align_bytes=64)
+                for j in range(2):
+                    nc.sync.dma_start(out=xnk[:, j * 4096 : (j + 1) * 4096], in_=xnv[k][:, j * 4096 : (j + 1) * 4096])
+                xn.append(xnk)
+
+        def xc_transpose(s, pr4, tag):
+            dlo, hh = s // 2, s % 2
+            xw32 = xn[hh][:].bitcast(F32)
+            pt = bank(tag)
+            for i in range(2):
+                d = 2 * (pr4 * 2 + i) + dlo
+                for u in range(2):
+                    s0 = (2 * i + u) * P
+                    nc.tensor.transpose(pt[:, s0 : s0 + P], xw32[:, d * 256 + u * P : d * 256 + (u + 1) * P], ident_f[:])
+            st["pxc", s, pr4] = pt
+
+        def xc_evac(s, pr4, copy):
+            if pr4 % 2 == 0:
+                gc = one.tile([P, 2048], BF16, tag="gc", align_bytes=64)
+                st["gc", s, pr4 // 2] = gc
+            gcw = st["gc", s, pr4 // 2][:].bitcast(F32)
+            pr = pr4 % 2
+            copy(
+                out=gcw[:, pr * C : (pr + 1) * C].rearrange("p (i r u) -> p i r u", i=2, r=P, u=2),
+                in_=st["pxc", s, pr4][:].rearrange("p (i u r) -> p i r u", i=2, u=2, r=P),
+            )
+
+        def xc_quant(s, half):
+            if half == 0:
+                cc = two.tile([P, 1024], U32, tag="cc", align_bytes=64)
+                sc = two.tile([P, 1024], U8, tag="sc", align_bytes=64)
+                st["cc", s] = (cc, sc)
+            cc, sc = st["cc", s]
+            nc.vector.quantize_mx(
+                out=cc[:, half * C : (half + 1) * C].bitcast(FP8X4),
+                scales=sc[:, half * C : (half + 1) * C],
+                in_=st["gc", s, half][:],
+            )
+
+        def xc_steps(s, tags, copy):
+            steps = []
+            steps.append(lambda: xc_transpose(s, 0, tags[0]))
+            steps.append(lambda: (xc_transpose(s, 1, tags[1 % len(tags)]), xc_evac(s, 0, copy)))
+            steps.append(lambda: xc_evac(s, 1, copy))
+            steps.append(lambda: (xc_transpose(s, 2, tags[0]), xc_quant(s, 0)))
+            steps.append(lambda: (xc_transpose(s, 3, tags[1 % len(tags)]), xc_evac(s, 2, copy)))
+            steps.append(lambda: xc_evac(s, 3, copy))
+            steps.append(lambda: xc_quant(s, 1))
+            return steps
+
+        def b_xh(s, k, tag):
+            dlo, hh = s // 2, s % 2
+            ch, sh = st["codes", 0, dlo]
+            hb, wb = k // 4, k % 4
+            rc, rs = wslice(0, hh * 256 + hb * P, P)
+            ph = bank(tag)
+            for wi in range(4):
+                w = 4 * wb + wi
+                nc.tensor.matmul_mx(
+                    out=ph[:, wi * P : (wi + 1) * P],
+                    lhsT=ch[:, w * P : (w + 1) * P].bitcast(FP8X4),
+                    lhsT_scale=sh[:, w * P : (w + 1) * P],
+                    rhs=rc,
+                    rhs_scale=rs,
+                    start=True,
+                    stop=True,
+                )
+            st["ph", s, k] = ph
+
+        def b_xh_evac(s, k, copy):
+            if k == 0:
+                s2 = one.tile([P, 4096], F32, tag="s2", align_bytes=64)
+                st["s2", s] = s2
+            s2v = st["s2", s][:].rearrange("p (g h w) -> p g h w", g=32, h=8, w=16)
+            hb, wb = k // 4, k % 4
+            copy(
+                out=s2v[:, :, 4 * hb : 4 * hb + 4, 4 * wb : 4 * wb + 4],
+                in_=st["ph", s, k][:].rearrange("p (w h g) -> p g h w", w=4, h=4, g=32),
+            )
+
+        def b_xw(s, h8, tag):
+            dlo, hh = s // 2, s % 2
+            cw, sw = st["codes", 1, dlo]
+            rc, rs = wslice(1, 0, C)
+            h = 8 * hh + h8
+            pw = bank(tag)
+            nc.tensor.matmul_mx(
+                out=pw[:],
+                lhsT=cw[:, h * P : (h + 1) * P].bitcast(FP8X4),
+                lhsT_scale=sw[:, h * P : (h + 1) * P],
+                rhs=rc,
+                rhs_scale=rs,
+                start=True,
+                stop=True,
+            )
+            st["pw", s, h8] = pw
+
+        def b_add(s, h8):
+            s2v = st["s2", s][:].rearrange("p (g h w) -> p g h w", g=32, h=8, w=16)
+            nc.vector.tensor_tensor(
+                out=s2v[:, :, h8, :],
+                in0=st["pw", s, h8][:].rearrange("p (w g) -> p g w", w=16, g=32),
+                in1=s2v[:, :, h8, :],
+                op=ADD,
+            )
+
+        def b_t(s, gb, tag):
+            s2 = st["s2", s]
+            pst = bank(tag)
+            for gi in range(4):
+                g = 4 * gb + gi
+                nc.tensor.transpose(pst[:, gi * P : (gi + 1) * P], s2[:, g * P : (g + 1) * P], ident_f[:])
+            st["pst", s, gb] = pst
+
+        def b_t_evac(s, gb, copy):
+            if gb == 0:
+                a = two.tile([P, 4096], F32, tag="a", align_bytes=64)
+                st["a", s] = a
+            av = st["a", s][:].rearrange("p (a l g) -> p a l g", a=8, l=16, g=32)
+            copy(
+                out=av[:, :, :, 4 * gb : 4 * gb + 4],
+                in_=st["pst", s, gb][:].rearrange("p (g l a) -> p a l g", g=4, l=16, a=8),
+            )
+
+        def b_bias(s, d8):
+            a = st["a", s]
+            nc.gpsimd.tensor_tensor(
+                out=a[:, d8 * C : (d8 + 1) * C], in0=a[:, d8 * C : (d8 + 1) * C], in1=bias_n[:, s % 2, :], op=ADD
+            )
+
+        def beta_steps(s, mtags, ttags, copies):
+            steps = []
+            nm, nt, ncp = len(mtags), len(ttags), len(copies)
+            steps.append(lambda: b_xh(s, 0, mtags[0]))
+            for k in range(1, 8):
+                steps.append(lambda k=k: (b_xh(s, k, mtags[k % nm]), b_xh_evac(s, k - 1, copies[((k - 1) // 2) % ncp])))
+            steps.append(lambda: (b_xw(s, 0, mtags[0]), b_xh_evac(s, 7, copies[3 % ncp])))
+            for h8 in range(1, 8):
+                steps.append(lambda h8=h8: (b_xw(s, h8, mtags[h8 % nm]), b_add(s, h8 - 1)))
+            steps.append(lambda: b_add(s, 7))
+            steps.append(lambda: b_t(s, 0, ttags[0]))
+            for gb in range(1, 8):
+                steps.append(lambda gb=gb: (b_t(s, gb, ttags[gb % nt]), b_t_evac(s, gb - 1, copies[((gb - 1) // 2) % ncp])))
+            steps.append(lambda: b_t_evac(s, 7, copies[3 % ncp]))
+            for d8 in range(8):
+                steps.append(lambda d8=d8: b_bias(s, d8))
+            return steps
+
+        def where(n):
+            s = n // 8
+            return s, s // 2, s % 2, n % 8
+
+        def pe1(n):
+            s, dlo, hh, d8 = where(n)
+            d = 2 * d8 + dlo
+            cc, sc = st["cc", s]
+            rc, rs = wslice(2, 0, C)
+            pc = bank("pc")
+            nc.tensor.matmul_mx(
+                out=pc[:],
+                lhsT=cc[:, d8 * P : (d8 + 1) * P].bitcast(FP8X4),
+                lhsT_scale=sc[:, d8 * P : (d8 + 1) * P],
+                rhs=rc,
+                rhs_scale=rs,
+                start=True,
+                stop=True,
+            )
+            pa = bank("pa")
+            for k in range(2):
+                nc.tensor.matmul(
+                    out=pa[:],
+                    lhsT=wattn[:, k, hh * P : (hh + 1) * P],
+                    rhs=xn[k][:, d * C : (d + 1) * C],
+                    start=(k == 0),
+                    stop=(k == 1),
+                )
+            st["pc", n] = pc
+            st["pa", n] = pa
+
+        def v1(n):
+            s, dlo, hh, d8 = where(n)
+            if n % 2 == 0:
+                hidn = two.tile([P, 2, C], BF16, tag="hidn")
+                st["hidn", n // 2] = hidn
+            hidn = st["hidn", n // 2]
+            bsum = two.tile([P, C], F32, tag="bsum")
+            nc.vector.tensor_tensor(out=bsum[:], in0=st["pc", n][:], in1=st["a", s][:, d8 * C : (d8 + 1) * C], op=ADD)
+            nc.vector.scalar_tensor_tensor(
+                out=hidn[:, n % 2, :], in0=st["pa", n][:], scalar=ap1[:, hh : hh + 1], in1=bsum[:], op0=ADD, op1=MULT
+            )
+
+        def pe2(j):
+            hidn = st["hidn", j]
+            pht = bank("tp", BF16, 1024)
+            for i in range(2):
+                for t in range(4):
+                    s0 = (4 * i + t) * P
+                    nc.tensor.transpose(pht[:, s0 : s0 + P], hidn[:, i, t * P : (t + 1) * P], ident_b[:])
+            st["pht", j] = pht
+
+        def s2c(j):
+            if j % 2 == 0:
+                ghid = two.tile([P, 2048], BF16, tag="ghid", align_bytes=64)
+                st["ghid", j // 2] = ghid
+            ghid = st["ghid", j // 2]
+            pr = j % 2
+            nc.scalar.copy(
+                out=ghid[:, pr * 1024 : (pr + 1) * 1024].rearrange("p (i r t) -> p i r t", i=2, r=P, t=4),
+                in_=st["pht", j][:].rearrange("p (i t r) -> p i r t", i=2, t=4, r=P),
+            )
+
+        def qh(m):
+            chid = two.tile([P, C], U32, tag="chid", align_bytes=64)
+            shid = two.tile([P, C], U8, tag="shid", align_bytes=64)
+            nc.vector.quantize_mx(out=chid[:].bitcast(FP8X4), scales=shid[:], in_=st["ghid", m][:])
+            st["chid", m] = (chid, shid)
+
+        def gx(n):
+            s, dlo, hh, d8 = where(n)
+            d = 2 * d8 + dlo
+            xpb = three.tile([P, C], F32, tag="xpb")
+            nc.gpsimd.tensor_tensor(out=xpb[:], in0=xn[hh][:, d * C : (d + 1) * C], in1=b1bc[:], op=ADD)
+            st["xpb", n] = xpb
+
+        def pe3(n):
+            chid, shid = st["chid", n // 4]
+            j = n % 4
+            rc, rs = wslice(3, 0, C)
+            pf = bank("pf")
+            nc.tensor.matmul_mx(
+                out=pf[:],
+                lhsT=chid[:, j * P : (j + 1) * P].bitcast(FP8X4),
+                lhsT_scale=shid[:, j * P : (j + 1) * P],
+                rhs=rc,
+                rhs_scale=rs,
+                start=True,
+                stop=True,
+            )
+            st["pf", n] = pf
+
+        def v3(n):
+            s, dlo, hh, d8 = where(n)
+            d = 2 * d8 + dlo
+            o = three.tile([P, C], F32, tag="o")
+            nc.vector.tensor_tensor(out=o[:], in0=st["pf", n][:], in1=st["xpb", n][:], op=ADD)
+            nc.sync.dma_start(out=outv[hh][:, d, :], in_=o[:])
+
+        sc_copy = nc.scalar.copy
+        ve_copy = nc.vector.tensor_copy
+        alltags = ("tp", "sd", "pa", "tp", "sd", "pa")
+
+        def run(steps):
+            for f in steps:
+                f()
+
+        weight_prep(0, ve_copy)
+        weight_prep(1, sc_copy)
+        weight_quant(0)
+        ih = input_steps(0, 0, alltags, (sc_copy, ve_copy))
+        run(ih[:2])
+        load_xs(0, 1, 0)
+        load_xs(0, 1, 1)
+        weight_quant(1)
+        run(ih[2:])
+        weight_prep(2, sc_copy)
+        weight_prep(3, sc_copy)
 
         tbx = consts.tile([P, 16, 32], BF16, tag="tbx")
         nc.vector.tensor_copy(out=tbx[:], in_=tb[:].unsqueeze(1).to_broadcast([P, 16, 32]))
@@ -159,7 +464,7 @@ def tile_mlpp_pa_kernel(tc, x, W_h, b_h, W_w, b_w, W_c, b_c, W_attn, b_attn, W_1
                 in1=ident_b[:, 16 + 8 * hh : 24 + 8 * hh].unsqueeze(2).to_broadcast([P, 8, 16]),
                 op=ADD,
             )
-            pb = ps_at.tile([P, C], F32, tag="at")
+            pb = bank("pa")
             nc.tensor.matmul(
                 out=pb[:],
                 lhsT=sel[:].rearrange("p a w -> p (a w)"),
@@ -168,174 +473,59 @@ def tile_mlpp_pa_kernel(tc, x, W_h, b_h, W_w, b_w, W_c, b_c, W_attn, b_attn, W_1
                 stop=True,
             )
             nc.vector.tensor_tensor(out=bias_n[:, hh, :], in0=pb[:], in1=bcbc[:], op=ADD)
-        pta = ps_tp.tile([P, P], BF16, tag="tp")
+        pta = bank("tp", BF16, P)
         nc.tensor.transpose(pta[:], tba[:], ident_b[:])
         ap1 = consts.tile([P, 2], F32, tag="ap1")
         nc.vector.tensor_scalar_add(out=ap1[:], in0=pta[:, 0:2], scalar1=1.0)
 
-        def xc_stage(dlo, hh):
-            cc = two.tile([P, 1024], U32, tag="cc", align_bytes=64)
-            sc = two.tile([P, 1024], U8, tag="sc", align_bytes=64)
-            xw32 = xn[hh][:].bitcast(F32)
-            for half in range(2):
-                gc = one.tile([P, 2048], BF16, tag="gc", align_bytes=64)
-                gcw = gc[:].bitcast(F32)
-                for pr in range(2):
-                    pt = ps_tp.tile([P, C], F32, tag="tp")
-                    for i in range(2):
-                        d = 2 * (half * 4 + pr * 2 + i) + dlo
-                        for u in range(2):
-                            s0 = (2 * i + u) * P
-                            nc.tensor.transpose(
-                                pt[:, s0 : s0 + P], xw32[:, d * 256 + u * P : d * 256 + (u + 1) * P], ident_f[:]
-                            )
-                    nc.scalar.copy(
-                        out=gcw[:, pr * C : (pr + 1) * C].rearrange("p (i r u) -> p i r u", i=2, r=P, u=2),
-                        in_=pt[:].rearrange("p (i u r) -> p i r u", i=2, u=2, r=P),
-                    )
-                nc.vector.quantize_mx(
-                    out=cc[:, half * C : (half + 1) * C].bitcast(FP8X4),
-                    scales=sc[:, half * C : (half + 1) * C],
-                    in_=gc[:],
-                )
-            return cc, sc
+        b0 = beta_steps(0, ("sd", "pa", "tp"), ("tp", "sd", "pa"), (sc_copy, ve_copy))
+        iw = input_steps(1, 0, alltags, (sc_copy, ve_copy))
+        run(iw[:2])
+        load_xn()
+        run(b0[:8])
+        run(iw[2:])
+        weight_quant(2)
+        weight_quant(3)
+        run(b0[8:])
+        run(xc_steps(0, ("tp", "sd"), sc_copy))
 
-        def beta(hh, chs, cws):
-            ch, sh = chs
-            cw, sw = cws
-            s2 = one.tile([P, 4096], F32, tag="s2", align_bytes=64)
-            s2v = s2[:].rearrange("p (g h w) -> p g h w", g=32, h=8, w=16)
-            for hb in range(2):
-                rc, rs = wslice(0, hh * 256 + hb * P, P)
-                for wb in range(4):
-                    ph = ps_mx.tile([P, C], F32, tag="mx")
-                    for wi in range(4):
-                        w = 4 * wb + wi
-                        nc.tensor.matmul_mx(
-                            out=ph[:, wi * P : (wi + 1) * P],
-                            lhsT=ch[:, w * P : (w + 1) * P].bitcast(FP8X4),
-                            lhsT_scale=sh[:, w * P : (w + 1) * P],
-                            rhs=rc,
-                            rhs_scale=rs,
-                            start=True,
-                            stop=True,
-                        )
-                    nc.scalar.copy(
-                        out=s2v[:, :, 4 * hb : 4 * hb + 4, 4 * wb : 4 * wb + 4],
-                        in_=ph[:].rearrange("p (w h g) -> p g h w", w=4, h=4, g=32),
-                    )
-            rc, rs = wslice(1, 0, C)
-            for h8 in range(8):
-                h = 8 * hh + h8
-                pw = ps_mx.tile([P, C], F32, tag="mx")
-                nc.tensor.matmul_mx(
-                    out=pw[:],
-                    lhsT=cw[:, h * P : (h + 1) * P].bitcast(FP8X4),
-                    lhsT_scale=sw[:, h * P : (h + 1) * P],
-                    rhs=rc,
-                    rhs_scale=rs,
-                    start=True,
-                    stop=True,
-                )
-                nc.vector.tensor_tensor(
-                    out=s2v[:, :, h8, :],
-                    in0=pw[:].rearrange("p (w g) -> p g w", w=16, g=32),
-                    in1=s2v[:, :, h8, :],
-                    op=ADD,
-                )
-            a = two.tile([P, 4096], F32, tag="a", align_bytes=64)
-            av = a[:].rearrange("p (a l g) -> p a l g", a=8, l=16, g=32)
-            for gb in range(8):
-                pst = ps_tp.tile([P, C], F32, tag="tp")
-                for gi in range(4):
-                    g = 4 * gb + gi
-                    nc.tensor.transpose(pst[:, gi * P : (gi + 1) * P], s2[:, g * P : (g + 1) * P], ident_f[:])
-                nc.scalar.copy(
-                    out=av[:, :, :, 4 * gb : 4 * gb + 4],
-                    in_=pst[:].rearrange("p (g l a) -> p a l g", g=4, l=16, a=8),
-                )
-            for d8 in range(8):
-                nc.gpsimd.tensor_tensor(
-                    out=a[:, d8 * C : (d8 + 1) * C], in0=a[:, d8 * C : (d8 + 1) * C], in1=bias_n[:, hh, :], op=ADD
-                )
-            return a
+        side = {}
+        side[0] = (
+            xc_steps(1, ("tp",), sc_copy)
+            + beta_steps(1, ("sd",), ("tp",), (sc_copy,))
+            + input_steps(0, 1, ("tp",), (sc_copy, sc_copy))[:2]
+            + [lambda: (load_xs(1, 1, 0), load_xs(1, 1, 1))]
+            + input_steps(0, 1, ("tp",), (sc_copy, sc_copy))[2:]
+        )
+        side[1] = (
+            input_steps(1, 1, ("tp",), (sc_copy, sc_copy))
+            + xc_steps(2, ("tp",), sc_copy)
+            + beta_steps(2, ("sd",), ("tp",), (sc_copy,))
+        )
+        side[2] = xc_steps(3, ("tp",), sc_copy) + beta_steps(3, ("sd",), ("tp",), (sc_copy,))
+        side[3] = []
 
-        def gamma(dlo, hh, a, ccs):
-            cc, sc = ccs
-            wc_c, wc_s = wslice(2, 0, C)
-            w1_c, w1_s = wslice(3, 0, C)
-            for half in range(2):
-                ghid = one.tile([P, 2048], BF16, tag="ghid", align_bytes=64)
-                for pr in range(2):
-                    hidn = three.tile([P, 2, C], BF16, tag="hidn")
-                    for i in range(2):
-                        d8 = half * 4 + pr * 2 + i
-                        d = 2 * d8 + dlo
-                        pc = ps_mx.tile([P, C], F32, tag="mx")
-                        nc.tensor.matmul_mx(
-                            out=pc[:],
-                            lhsT=cc[:, d8 * P : (d8 + 1) * P].bitcast(FP8X4),
-                            lhsT_scale=sc[:, d8 * P : (d8 + 1) * P],
-                            rhs=wc_c,
-                            rhs_scale=wc_s,
-                            start=True,
-                            stop=True,
-                        )
-                        pa = ps_at.tile([P, C], F32, tag="at")
-                        for k in range(2):
-                            nc.tensor.matmul(
-                                out=pa[:],
-                                lhsT=wattn[:, k, hh * P : (hh + 1) * P],
-                                rhs=xn[k][:, d * C : (d + 1) * C],
-                                start=(k == 0),
-                                stop=(k == 1),
-                            )
-                        bsum = two.tile([P, C], F32, tag="bsum")
-                        nc.vector.tensor_tensor(out=bsum[:], in0=pc[:], in1=a[:, d8 * C : (d8 + 1) * C], op=ADD)
-                        nc.vector.scalar_tensor_tensor(
-                            out=hidn[:, i, :], in0=pa[:], scalar=ap1[:, hh : hh + 1], in1=bsum[:], op0=ADD, op1=MULT
-                        )
-                    pht = ps_tp.tile([P, 1024], BF16, tag="tp")
-                    for i in range(2):
-                        for t in range(4):
-                            s0 = (4 * i + t) * P
-                            nc.tensor.transpose(pht[:, s0 : s0 + P], hidn[:, i, t * P : (t + 1) * P], ident_b[:])
-                    nc.scalar.copy(
-                        out=ghid[:, pr * 1024 : (pr + 1) * 1024].rearrange("p (i r t) -> p i r t", i=2, r=P, t=4),
-                        in_=pht[:].rearrange("p (i t r) -> p i r t", i=2, t=4, r=P),
-                    )
-                chid = two.tile([P, C], U32, tag="chid", align_bytes=64)
-                shid = two.tile([P, C], U8, tag="shid", align_bytes=64)
-                nc.vector.quantize_mx(out=chid[:].bitcast(FP8X4), scales=shid[:], in_=ghid[:])
-                for j in range(4):
-                    d = 2 * (half * 4 + j) + dlo
-                    xpb = three.tile([P, C], F32, tag="xpb")
-                    nc.gpsimd.tensor_tensor(out=xpb[:], in0=xn[hh][:, d * C : (d + 1) * C], in1=b1bc[:], op=ADD)
-                    pf = ps_mx.tile([P, C], F32, tag="mx")
-                    nc.tensor.matmul_mx(
-                        out=pf[:],
-                        lhsT=chid[:, j * P : (j + 1) * P].bitcast(FP8X4),
-                        lhsT_scale=shid[:, j * P : (j + 1) * P],
-                        rhs=w1_c,
-                        rhs_scale=w1_s,
-                        start=True,
-                        stop=True,
-                    )
-                    o = three.tile([P, C], F32, tag="o")
-                    nc.vector.tensor_tensor(out=o[:], in0=pf[:], in1=xpb[:], op=ADD)
-                    nc.sync.dma_start(out=outv[hh][:, d, :], in_=o[:])
-
-        cc00 = xc_stage(0, 0)
-        a00 = beta(0, ch0, cw0)
-        cc01 = xc_stage(0, 1)
-        a01 = beta(1, ch0, cw0)
-        ch1 = input_stage(0, 1)
-        cw1 = input_stage(1, 1)
-        gamma(0, 0, a00, cc00)
-        cc10 = xc_stage(1, 0)
-        a10 = beta(0, ch1, cw1)
-        gamma(0, 1, a01, cc01)
-        cc11 = xc_stage(1, 1)
-        a11 = beta(1, ch1, cw1)
-        gamma(1, 0, a10, cc10)
-        gamma(1, 1, a11, cc11)
+        NT = 32
+        pe1(0)
+        done = {0: 0, 1: 0, 2: 0, 3: 0}
+        for n in range(NT + 8):
+            if n + 1 < NT:
+                pe1(n + 1)
+            if n < NT:
+                v1(n)
+            if 0 <= n - 5 < NT:
+                gx(n - 5)
+            if n >= 2 and n % 2 == 0 and (n - 2) // 2 < NT // 2:
+                pe2((n - 2) // 2)
+                s2c((n - 2) // 2)
+            if n >= 5 and (n - 5) % 4 == 0 and (n - 5) // 4 < NT // 4:
+                qh((n - 5) // 4)
+            if 0 <= n - 6 < NT:
+                pe3(n - 6)
+            if 0 <= n - 7 < NT:
+                v3(n - 7)
+            if n < NT:
+                w = n // 8
+                upto = ((n % 8 + 1) * len(side[w]) + 7) // 8
+                run(side[w][done[w] : upto])
+                done[w] = upto

@@ -19,19 +19,20 @@ FLOPS = 4 * 2 * 4096 * 512 * 512 + 2 * 8192 * 256 * 256
 def tile_mlpp_pa_kernel(tc, x, W_h, b_h, W_w, b_w, W_c, b_c, W_attn, b_attn, W_1, b_1, out):
     nc = tc.nc
     with ExitStack() as ctx:
+        ctx.enter_context(tc.manual_schedule())
         consts = ctx.enter_context(tc.tile_pool(name="consts", bufs=1))
         xsp = ctx.enter_context(tc.tile_pool(name="xsp", bufs=2))
         one = ctx.enter_context(tc.tile_pool(name="one", bufs=1))
         two = ctx.enter_context(tc.tile_pool(name="two", bufs=2))
         three = ctx.enter_context(tc.tile_pool(name="three", bufs=3))
         ps1 = ctx.enter_context(tc.psum_pool(name="ps1", bufs=1))
-        ps2 = ctx.enter_context(tc.psum_pool(name="ps2", bufs=2))
+        ps5 = ctx.enter_context(tc.psum_pool(name="ps5", bufs=5))
 
         def bank(tag, dtype=F32, cols=C):
-            if tag in ("pc", "pf"):
-                t = ps1.tile([P, cols], dtype, name="bk_" + tag, tag=tag)
+            if tag == "ss":
+                t = ps5.tile([P, cols], dtype, name="bk_ss", tag="ss")
             else:
-                t = ps2.tile([P, cols], dtype, name="bk_" + tag, tag=tag)
+                t = ps1.tile([P, cols], dtype, name="bk_" + tag, tag=tag)
             return t
 
         xnv = x.rearrange("b (k h) w d c -> k (b h w) (d c)", k=2)
@@ -64,7 +65,7 @@ def tile_mlpp_pa_kernel(tc, x, W_h, b_h, W_w, b_w, W_c, b_c, W_attn, b_attn, W_1
                     nc.sync.dma_start(out=xs[16 * a8 : 16 * a8 + 16, :, :], in_=x2v[:, 8 * q : 8 * q + 8, a8, dlo, :])
             st["xs", which, dlo, q] = xs[:]
 
-        wraw = two.tile([P, 8192], BF16, tag="xn", align_bytes=64)
+        wraw = two.tile([P, 8192], BF16, tag="a", align_bytes=64)
         wrv = wraw[:].rearrange("p (i t n) -> p i t n", i=4, t=4, n=C)
         wg = two.tile([P, 8192], BF16, tag="a", align_bytes=64)
         wgv = wg[:].rearrange("p (i n t) -> p i n t", i=4, n=C, t=4)
@@ -80,11 +81,9 @@ def tile_mlpp_pa_kernel(tc, x, W_h, b_h, W_w, b_w, W_c, b_c, W_attn, b_attn, W_1
 
         load_xs(0, 0, 0)
         load_xs(0, 0, 1)
-        load_x2_first()
         load_w(0, W_h)
+        load_x2_first()
         load_w(1, W_w)
-        load_w(2, W_c)
-        nc.sync.dma_start(out=wrv[:, 3, :, :], in_=W_1.rearrange("(t p) n -> p t n", p=P))
 
         def weight_prep(i, eng_copy):
             eng_copy(out=wgv[:, i], in_=wrv[:, i].rearrange("p t n -> p n t"))
@@ -139,7 +138,7 @@ def tile_mlpp_pa_kernel(tc, x, W_h, b_h, W_w, b_w, W_c, b_c, W_attn, b_attn, W_1
 
         def in_evac(which, dlo, lp, copies):
             if lp == 0:
-                gr = two.tile([P, 8192], BF16, tag="gr", align_bytes=64)
+                gr = one.tile([P, 8192], BF16, tag="gr", align_bytes=64)
                 st["gr", which, dlo] = gr
             gr = st["gr", which, dlo]
             grw = gr[:].bitcast(F32).rearrange("p (y l a u) -> p y l a u", y=16, l=16, a=8, u=2)
@@ -182,12 +181,11 @@ def tile_mlpp_pa_kernel(tc, x, W_h, b_h, W_w, b_w, W_c, b_c, W_attn, b_attn, W_1
 
         xn = []
 
-        def load_xn():
-            for k in range(2):
-                xnk = two.tile([P, 8192], BF16, name="xn%d" % k, tag="xn", align_bytes=64)
-                for j in range(2):
-                    nc.sync.dma_start(out=xnk[:, j * 4096 : (j + 1) * 4096], in_=xnv[k][:, j * 4096 : (j + 1) * 4096])
-                xn.append(xnk)
+        def load_xn(k):
+            xnk = two.tile([P, 8192], BF16, name="xn%d" % k, tag="xn", align_bytes=64)
+            for j in range(2):
+                nc.sync.dma_start(out=xnk[:, j * 4096 : (j + 1) * 4096], in_=xnv[k][:, j * 4096 : (j + 1) * 4096])
+            xn.append(xnk)
 
         def xc_transpose(s, pr4, tag):
             dlo, hh = s // 2, s % 2
@@ -255,7 +253,7 @@ def tile_mlpp_pa_kernel(tc, x, W_h, b_h, W_w, b_w, W_c, b_c, W_attn, b_attn, W_1
 
         def b_xh_evac(s, k, copy):
             if k == 0:
-                s2 = one.tile([P, 4096], F32, tag="s2", align_bytes=64)
+                s2 = two.tile([P, 4096], F32, tag="s2", align_bytes=64)
                 st["s2", s] = s2
             s2v = st["s2", s][:].rearrange("p (g h w) -> p g h w", g=32, h=8, w=16)
             hb, wb = k // 4, k % 4
@@ -377,7 +375,7 @@ def tile_mlpp_pa_kernel(tc, x, W_h, b_h, W_w, b_w, W_c, b_c, W_attn, b_attn, W_1
 
         def pe2(j):
             hidn = st["hidn", j]
-            pht = bank("tp", BF16, 1024)
+            pht = bank("ss", BF16, 1024)
             for i in range(2):
                 for t in range(4):
                     s0 = (4 * i + t) * P
@@ -408,11 +406,11 @@ def tile_mlpp_pa_kernel(tc, x, W_h, b_h, W_w, b_w, W_c, b_c, W_attn, b_attn, W_1
             nc.gpsimd.tensor_tensor(out=xpb[:], in0=xn[hh][:, d * C : (d + 1) * C], in1=b1bc[:], op=ADD)
             st["xpb", n] = xpb
 
-        def pe3(n):
+        def pe3(n, tag="pf"):
             chid, shid = st["chid", n // 4]
             j = n % 4
             rc, rs = wslice(3, 0, C)
-            pf = bank("pf")
+            pf = bank(tag)
             nc.tensor.matmul_mx(
                 out=pf[:],
                 lhsT=chid[:, j * P : (j + 1) * P].bitcast(FP8X4),
@@ -433,23 +431,18 @@ def tile_mlpp_pa_kernel(tc, x, W_h, b_h, W_w, b_w, W_c, b_c, W_attn, b_attn, W_1
 
         sc_copy = nc.scalar.copy
         ve_copy = nc.vector.tensor_copy
-        alltags = ("tp", "sd", "pa", "tp", "sd", "pa")
+        both = (sc_copy, ve_copy)
+        only_s = (sc_copy, sc_copy)
+        rot = {"n": 0}
+        ring = ("ss", "ss", "ss", "ss", "ss", "pc", "pa", "pf")
 
-        def run(steps):
-            for f in steps:
-                f()
+        def ptag():
+            rot["n"] += 1
+            return ring[(rot["n"] - 1) % len(ring)]
 
-        weight_prep(0, ve_copy)
-        weight_prep(1, sc_copy)
-        weight_quant(0)
-        ih = input_steps(0, 0, alltags, (sc_copy, ve_copy))
-        run(ih[:2])
-        load_xs(0, 1, 0)
-        load_xs(0, 1, 1)
-        weight_quant(1)
-        run(ih[2:])
-        weight_prep(2, sc_copy)
-        weight_prep(3, sc_copy)
+        load_xn(0)
+        load_w(2, W_c)
+        nc.sync.dma_start(out=wrv[:, 3, :, :], in_=W_1.rearrange("(t p) n -> p t n", p=P))
 
         tbx = consts.tile([P, 16, 32], BF16, tag="tbx")
         nc.vector.tensor_copy(out=tbx[:], in_=tb[:].unsqueeze(1).to_broadcast([P, 16, 32]))
@@ -464,7 +457,7 @@ def tile_mlpp_pa_kernel(tc, x, W_h, b_h, W_w, b_w, W_c, b_c, W_attn, b_attn, W_1
                 in1=ident_b[:, 16 + 8 * hh : 24 + 8 * hh].unsqueeze(2).to_broadcast([P, 8, 16]),
                 op=ADD,
             )
-            pb = bank("pa")
+            pb = bank(ptag())
             nc.tensor.matmul(
                 out=pb[:],
                 lhsT=sel[:].rearrange("p a w -> p (a w)"),
@@ -473,59 +466,221 @@ def tile_mlpp_pa_kernel(tc, x, W_h, b_h, W_w, b_w, W_c, b_c, W_attn, b_attn, W_1
                 stop=True,
             )
             nc.vector.tensor_tensor(out=bias_n[:, hh, :], in0=pb[:], in1=bcbc[:], op=ADD)
-        pta = bank("tp", BF16, P)
+        pta = bank(ptag(), BF16, P)
         nc.tensor.transpose(pta[:], tba[:], ident_b[:])
         ap1 = consts.tile([P, 2], F32, tag="ap1")
         nc.vector.tensor_scalar_add(out=ap1[:], in0=pta[:, 0:2], scalar1=1.0)
 
-        b0 = beta_steps(0, ("sd", "pa", "tp"), ("tp", "sd", "pa"), (sc_copy, ve_copy))
-        iw = input_steps(1, 0, alltags, (sc_copy, ve_copy))
-        run(iw[:2])
-        load_xn()
-        run(b0[:8])
-        run(iw[2:])
+        in_relayout(0, 0, 0)
+        in_relayout(0, 0, 1)
+        load_xs(0, 1, 0)
+        load_xs(0, 1, 1)
+        for lp in range(8):
+            in_transpose(0, 0, lp, ptag())
+            if lp >= 1:
+                in_evac(0, 0, lp - 1, both)
+        in_evac(0, 0, 7, both)
+        weight_prep(0, ve_copy)
+        in_quant(0, 0, 0)
+        weight_quant(0)
+        in_quant(0, 0, 1)
+        weight_prep(1, sc_copy)
+        in_relayout(1, 0, 0)
+        in_relayout(1, 0, 1)
+        load_xn(1)
+        weight_quant(1)
+        for s in range(2):
+            for k in range(8):
+                b_xh(s, k, ptag())
+                b_xh_evac(s, k, both[(k // 2) % 2])
+        for lp in range(8):
+            in_transpose(1, 0, lp, ptag())
+            if lp >= 1:
+                in_evac(1, 0, lp - 1, both)
+        in_evac(1, 0, 7, both)
+        in_quant(1, 0, 0)
+        in_quant(1, 0, 1)
+        weight_prep(2, sc_copy)
+        weight_prep(3, sc_copy)
+
+        for h8 in range(8):
+            b_xw(0, h8, ptag())
+        for h8 in range(8):
+            b_add(0, h8)
+            if h8 < 4:
+                b_xw(1, h8, ptag())
         weight_quant(2)
         weight_quant(3)
-        run(b0[8:])
-        run(xc_steps(0, ("tp", "sd"), sc_copy))
+        for gb in range(8):
+            b_t(0, gb, ptag())
+            b_t_evac(0, gb, sc_copy)
+            if gb < 4:
+                b_add(1, gb)
+        for d8 in range(8):
+            b_bias(0, d8)
+        for h8 in range(4, 8):
+            b_xw(1, h8, ptag())
+            b_add(1, h8)
+        for f in xc_steps(0, ("ss",), sc_copy):
+            f()
 
-        side = {}
-        side[0] = (
-            xc_steps(1, ("tp",), sc_copy)
-            + beta_steps(1, ("sd",), ("tp",), (sc_copy,))
-            + input_steps(0, 1, ("tp",), (sc_copy, sc_copy))[:2]
-            + [lambda: (load_xs(1, 1, 0), load_xs(1, 1, 1))]
-            + input_steps(0, 1, ("tp",), (sc_copy, sc_copy))[2:]
-        )
-        side[1] = (
-            input_steps(1, 1, ("tp",), (sc_copy, sc_copy))
-            + xc_steps(2, ("tp",), sc_copy)
-            + beta_steps(2, ("sd",), ("tp",), (sc_copy,))
-        )
-        side[2] = xc_steps(3, ("tp",), sc_copy) + beta_steps(3, ("sd",), ("tp",), (sc_copy,))
-        side[3] = []
+        def t_jobs(s):
+            jobs = [
+                ("T", lambda gb=gb: b_t(s, gb, "ss"), lambda gb=gb: b_t_evac(s, gb, sc_copy), ("add", s), None)
+                for gb in range(8)
+            ]
+            jobs.append(("G", lambda: [b_bias(s, d8) for d8 in range(8)], None, None, ("a", s)))
+            return jobs
 
+        def i_jobs(which):
+            jobs = [("V", lambda q=q: in_relayout(which, 1, q), 2, None, None) for q in range(2)]
+            if which == 0:
+                jobs.append(("G", lambda: (load_xs(1, 1, 0), load_xs(1, 1, 1)), None, None, None))
+            jobs += [
+                ("T", lambda lp=lp: in_transpose(which, 1, lp, "ss"), lambda lp=lp: in_evac(which, 1, lp, only_s), None, None)
+                for lp in range(8)
+            ]
+            jobs.append(("V", lambda: in_quant(which, 1, 0), 2, None, ("q0", which)))
+            jobs.append(("V", lambda: in_quant(which, 1, 1), 2, None, ("q1", which)))
+            return jobs
+
+        def ic_jobs(s):
+            jobs = []
+            for half in range(2):
+                for pr in range(2):
+                    jobs.append(
+                        (
+                            "T",
+                            lambda q=2 * half + pr: xc_transpose(s, q, "ss"),
+                            lambda q=2 * half + pr: xc_evac(s, q, sc_copy),
+                            ("tile", 8 * s - 9),
+                            None,
+                        )
+                    )
+                jobs.append(("V", lambda half=half: xc_quant(s, half), 1, None, ("cc", s) if half == 1 else None))
+            return jobs
+
+        def xh_jobs(s):
+            return [
+                ("X", lambda k=k: b_xh(s, k, "ss"), lambda k=k: b_xh_evac(s, k, sc_copy), ("q1", 0), ("xh", s) if k == 7 else None)
+                for k in range(8)
+            ]
+
+        def xw_jobs(s):
+            return [
+                ("W", lambda h8=h8: b_xw(s, h8, "ss"), lambda h8=h8: b_add(s, h8), ("xh", s), ("add", s) if h8 == 7 else None)
+                for h8 in range(8)
+            ]
+
+        queues = [
+            ic_jobs(1) + t_jobs(1),
+            i_jobs(0) + i_jobs(1) + xw_jobs(2) + t_jobs(2) + xw_jobs(3) + t_jobs(3),
+            xh_jobs(2) + xh_jobs(3),
+            ic_jobs(2) + ic_jobs(3),
+        ]
+        rank = {"T": 0, "V": 1, "X": 2, "W": 2, "G": 3}
+        flags = {("add", 1): -1, ("a", 0): -1, ("cc", 0): -1}
         NT = 32
+        due = {}
+
+        def later(c, what, arg):
+            due[c] = due.get(c, []) + [(what, arg)]
+
+        def todo(c, what):
+            return [a for (w, a) in due.get(c, []) if w == what]
+
+        pend = []
+        pos = [0, 0, 0, 0]
+        nxt = {"v1": 0, "pe1": 1, "left": NT}
         pe1(0)
-        done = {0: 0, 1: 0, 2: 0, 3: 0}
-        for n in range(NT + 8):
-            if n + 1 < NT:
-                pe1(n + 1)
-            if n < NT:
+        c = 0
+        while nxt["left"] > 0:
+            assert c < 200
+            n = nxt["v1"]
+            go = n < NT and ("a", n // 8) in flags
+            hid_jobs = todo(c, "pe2")
+            banks = (4 if go else 5) - len(hid_jobs)
+            vbud = 3 if go else 4
+            wbud = 2
+            take = []
+            for qi, qu in enumerate(queues):
+                top = 0
+                while pos[qi] < len(qu):
+                    typ, f1, f2, needs, sets = qu[pos[qi]]
+                    if rank[typ] < top:
+                        break
+                    if needs is not None:
+                        if needs[0] == "tile":
+                            if nxt["pe1"] <= needs[1] + 1:
+                                break
+                        elif needs not in flags or (flags[needs] == c and needs[0] != "q1" and needs[0] != "xh"):
+                            break
+                    if typ in ("T", "X", "W"):
+                        if banks <= 0 or (typ == "W" and wbud == 0):
+                            break
+                        banks -= 1
+                        if typ == "W":
+                            wbud -= 1
+                    if typ == "V":
+                        if vbud < f2:
+                            break
+                        vbud -= f2
+                    top = rank[typ]
+                    if sets is not None:
+                        flags[sets] = c
+                    take.append(qu[pos[qi]])
+                    pos[qi] += 1
+            pass
+            for f in pend:
+                f()
+            pend = []
+            for j in hid_jobs:
+                pe2(j)
+            for e in take:
+                if e[0] == "T":
+                    e[1]()
+            for j in hid_jobs:
+                s2c(j)
+            for e in take:
+                if e[0] == "T":
+                    e[2]()
+            if go:
                 v1(n)
-            if 0 <= n - 5 < NT:
-                gx(n - 5)
-            if n >= 2 and n % 2 == 0 and (n - 2) // 2 < NT // 2:
-                pe2((n - 2) // 2)
-                s2c((n - 2) // 2)
-            if n >= 5 and (n - 5) % 4 == 0 and (n - 5) // 4 < NT // 4:
-                qh((n - 5) // 4)
-            if 0 <= n - 6 < NT:
-                pe3(n - 6)
-            if 0 <= n - 7 < NT:
-                v3(n - 7)
-            if n < NT:
-                w = n // 8
-                upto = ((n % 8 + 1) * len(side[w]) + 7) // 8
-                run(side[w][done[w] : upto])
-                done[w] = upto
+                nxt["v1"] = n + 1
+                if n % 2 == 1:
+                    later(c + 1, "pe2", n // 2)
+                    if n % 4 == 3:
+                        later(c + 1, "qh", n // 4)
+                        for k in range(4):
+                            step = k if n < NT - 1 else 0
+                            later(c + step, "gx", n - 3 + k)
+                            later(c + 2 + step, "pe3", n - 3 + k)
+                            later(c + 3 + step, "v3", n - 3 + k)
+            m = nxt["pe1"]
+            if m < NT and m <= nxt["v1"] and ("cc", m // 8) in flags and flags["cc", m // 8] < c:
+                pe1(m)
+                nxt["pe1"] = m + 1
+            for a in todo(c, "v3"):
+                v3(a)
+                nxt["left"] -= 1
+            for a in todo(c, "pe3"):
+                pe3(a, ("pf", "pc", "pa", "ss")[a % 4] if a >= NT - 4 else "pf")
+            for a in todo(c, "qh"):
+                qh(a)
+            for e in take:
+                if e[0] == "V":
+                    e[1]()
+            for e in take:
+                if e[0] == "X":
+                    e[1]()
+                    e[2]()
+                if e[0] == "W":
+                    e[1]()
+                    pend.append(e[2])
+            for a in todo(c, "gx"):
+                gx(a)
+            for e in take:
+                if e[0] == "G":
+                    e[1]()
+            c += 1
+        assert all(pos[qi] == len(qu) for qi, qu in enumerate(queues))

@@ -26,11 +26,14 @@ def tile_mlpp_pa_kernel(tc, x, W_h, b_h, W_w, b_w, W_c, b_c, W_attn, b_attn, W_1
         two = ctx.enter_context(tc.tile_pool(name="two", bufs=2))
         three = ctx.enter_context(tc.tile_pool(name="three", bufs=3))
         ps1 = ctx.enter_context(tc.psum_pool(name="ps1", bufs=1))
-        ps5 = ctx.enter_context(tc.psum_pool(name="ps5", bufs=5))
+        ps5 = ctx.enter_context(tc.psum_pool(name="ps5", bufs=4))
+        ps2 = ctx.enter_context(tc.psum_pool(name="ps2", bufs=2))
 
         def bank(tag, dtype=F32, cols=C):
             if tag == "ss":
                 t = ps5.tile([P, cols], dtype, name="bk_ss", tag="ss")
+            elif tag == "pa":
+                t = ps2.tile([P, cols], dtype, name="bk_pa", tag="pa")
             else:
                 t = ps1.tile([P, cols], dtype, name="bk_" + tag, tag=tag)
             return t
@@ -52,7 +55,7 @@ def tile_mlpp_pa_kernel(tc, x, W_h, b_h, W_w, b_w, W_c, b_c, W_attn, b_attn, W_1
             for q in range(2):
                 for a8 in range(8):
                     nc.sync.dma_start(
-                        out=xbig[16 * a8 : 16 * a8 + 16, 8 * q : 8 * q + 8, :], in_=x2v[:, 8 * q : 8 * q + 8, a8, 0, :]
+                        out=xbig[a8 : P : 8, 8 * q : 8 * q + 8, :], in_=x2v[:, 8 * q : 8 * q + 8, a8, 0, :]
                     )
                 st["xs", 1, 0, q] = xbig[:, 8 * q : 8 * q + 8, :]
 
@@ -62,7 +65,7 @@ def tile_mlpp_pa_kernel(tc, x, W_h, b_h, W_w, b_w, W_c, b_c, W_attn, b_attn, W_1
                 nc.sync.dma_start(out=xs[:], in_=x1v[:, 8 * q : 8 * q + 8, dlo, :])
             else:
                 for a8 in range(8):
-                    nc.sync.dma_start(out=xs[16 * a8 : 16 * a8 + 16, :, :], in_=x2v[:, 8 * q : 8 * q + 8, a8, dlo, :])
+                    nc.sync.dma_start(out=xs[a8 : P : 8, :, :], in_=x2v[:, 8 * q : 8 * q + 8, a8, dlo, :])
             st["xs", which, dlo, q] = xs[:]
 
         wraw = two.tile([P, 8192], BF16, tag="a", align_bytes=64)
@@ -82,8 +85,8 @@ def tile_mlpp_pa_kernel(tc, x, W_h, b_h, W_w, b_w, W_c, b_c, W_attn, b_attn, W_1
         load_xs(0, 0, 0)
         load_xs(0, 0, 1)
         load_w(0, W_h)
-        load_x2_first()
         load_w(1, W_w)
+        load_x2_first()
 
         def weight_prep(i, eng_copy):
             eng_copy(out=wgv[:, i], in_=wrv[:, i].rearrange("p t n -> p n t"))
@@ -145,10 +148,7 @@ def tile_mlpp_pa_kernel(tc, x, W_h, b_h, W_w, b_w, W_c, b_c, W_attn, b_attn, W_1
             pt = st["pt", which, dlo, lp]
             for li in range(2):
                 half_bank = pt[:, li * 256 : (li + 1) * 256]
-                if which == 0:
-                    src = half_bank.rearrange("p (u y a) -> p y a u", u=2, y=16, a=8)
-                else:
-                    src = half_bank.rearrange("p (u a y) -> p y a u", u=2, y=16, a=8)
+                src = half_bank.rearrange("p (u y a) -> p y a u", u=2, y=16, a=8)
                 copies[li](out=grw[:, :, 2 * lp + li, :, :], in_=src)
 
         def in_quant(which, dlo, qn):
@@ -181,11 +181,14 @@ def tile_mlpp_pa_kernel(tc, x, W_h, b_h, W_w, b_w, W_c, b_c, W_attn, b_attn, W_1
 
         xn = []
 
-        def load_xn(k):
-            xnk = two.tile([P, 8192], BF16, name="xn%d" % k, tag="xn", align_bytes=64)
-            for j in range(2):
-                nc.sync.dma_start(out=xnk[:, j * 4096 : (j + 1) * 4096], in_=xnv[k][:, j * 4096 : (j + 1) * 4096])
-            xn.append(xnk)
+        def load_xn(k, dlo):
+            if dlo == 0:
+                xnk = two.tile([P, 8192], BF16, name="xn%d" % k, tag="xn", align_bytes=64)
+                xn.append(xnk)
+            nc.sync.dma_start(
+                out=xn[k][:].rearrange("p (a e c) -> p a e c", a=8, e=2, c=C)[:, :, dlo, :],
+                in_=xnv[k].rearrange("p (a e c) -> p a e c", a=8, e=2, c=C)[:, :, dlo, :],
+            )
 
         def xc_transpose(s, pr4, tag):
             dlo, hh = s // 2, s % 2
@@ -199,13 +202,12 @@ def tile_mlpp_pa_kernel(tc, x, W_h, b_h, W_w, b_w, W_c, b_c, W_attn, b_attn, W_1
             st["pxc", s, pr4] = pt
 
         def xc_evac(s, pr4, copy):
-            if pr4 % 2 == 0:
-                gc = one.tile([P, 2048], BF16, tag="gc", align_bytes=64)
-                st["gc", s, pr4 // 2] = gc
-            gcw = st["gc", s, pr4 // 2][:].bitcast(F32)
-            pr = pr4 % 2
+            if pr4 == 0:
+                gc = one.tile([P, 4096], BF16, tag="gc", align_bytes=64)
+                st["gc", s] = gc
+            gcw = st["gc", s][:].bitcast(F32)
             copy(
-                out=gcw[:, pr * C : (pr + 1) * C].rearrange("p (i r u) -> p i r u", i=2, r=P, u=2),
+                out=gcw[:, pr4 * C : (pr4 + 1) * C].rearrange("p (i r u) -> p i r u", i=2, r=P, u=2),
                 in_=st["pxc", s, pr4][:].rearrange("p (i u r) -> p i r u", i=2, u=2, r=P),
             )
 
@@ -218,7 +220,7 @@ def tile_mlpp_pa_kernel(tc, x, W_h, b_h, W_w, b_w, W_c, b_c, W_attn, b_attn, W_1
             nc.vector.quantize_mx(
                 out=cc[:, half * C : (half + 1) * C].bitcast(FP8X4),
                 scales=sc[:, half * C : (half + 1) * C],
-                in_=st["gc", s, half][:],
+                in_=st["gc", s][:, half * 2048 : (half + 1) * 2048],
             )
 
         def xc_steps(s, tags, copy):
@@ -349,17 +351,21 @@ def tile_mlpp_pa_kernel(tc, x, W_h, b_h, W_w, b_w, W_c, b_c, W_attn, b_attn, W_1
                 start=True,
                 stop=True,
             )
-            pa = bank("pa")
-            for k in range(2):
-                nc.tensor.matmul(
-                    out=pa[:],
-                    lhsT=wattn[:, k, hh * P : (hh + 1) * P],
-                    rhs=xn[k][:, d * C : (d + 1) * C],
-                    start=(k == 0),
-                    stop=(k == 1),
-                )
             st["pc", n] = pc
-            st["pa", n] = pa
+
+        def att(n, k):
+            s, dlo, hh, d8 = where(n)
+            d = 2 * d8 + dlo
+            if k == 0:
+                pa = bank("pa")
+                st["pa", n] = pa
+            nc.tensor.matmul(
+                out=st["pa", n][:],
+                lhsT=wattn[:, k, hh * P : (hh + 1) * P],
+                rhs=xn[k][:, d * C : (d + 1) * C],
+                start=(k == 0),
+                stop=(k == 1),
+            )
 
         def v1(n):
             s, dlo, hh, d8 = where(n)
@@ -384,7 +390,7 @@ def tile_mlpp_pa_kernel(tc, x, W_h, b_h, W_w, b_w, W_c, b_c, W_attn, b_attn, W_1
 
         def s2c(j):
             if j % 2 == 0:
-                ghid = two.tile([P, 2048], BF16, tag="ghid", align_bytes=64)
+                ghid = one.tile([P, 2048], BF16, tag="ghid", align_bytes=64)
                 st["ghid", j // 2] = ghid
             ghid = st["ghid", j // 2]
             pr = j % 2
@@ -434,13 +440,13 @@ def tile_mlpp_pa_kernel(tc, x, W_h, b_h, W_w, b_w, W_c, b_c, W_attn, b_attn, W_1
         both = (sc_copy, ve_copy)
         only_s = (sc_copy, sc_copy)
         rot = {"n": 0}
-        ring = ("ss", "ss", "ss", "ss", "ss", "pc", "pa", "pf")
+        ring = ("ss", "ss", "ss", "ss", "pa", "pa", "pc", "pf")
 
         def ptag():
             rot["n"] += 1
             return ring[(rot["n"] - 1) % len(ring)]
 
-        load_xn(0)
+        load_xn(0, 0)
         load_w(2, W_c)
         nc.sync.dma_start(out=wrv[:, 3, :, :], in_=W_1.rearrange("(t p) n -> p t n", p=P))
 
@@ -473,214 +479,148 @@ def tile_mlpp_pa_kernel(tc, x, W_h, b_h, W_w, b_w, W_c, b_c, W_attn, b_attn, W_1
 
         in_relayout(0, 0, 0)
         in_relayout(0, 0, 1)
-        load_xs(0, 1, 0)
-        load_xs(0, 1, 1)
+        weight_prep(1, sc_copy)
+        weight_prep(0, ve_copy)
+        weight_quant(0)
+        weight_quant(1)
         for lp in range(8):
             in_transpose(0, 0, lp, ptag())
-            if lp >= 1:
-                in_evac(0, 0, lp - 1, both)
-        in_evac(0, 0, 7, both)
-        weight_prep(0, ve_copy)
+            in_evac(0, 0, lp, both)
         in_quant(0, 0, 0)
-        weight_quant(0)
         in_quant(0, 0, 1)
-        weight_prep(1, sc_copy)
         in_relayout(1, 0, 0)
         in_relayout(1, 0, 1)
-        load_xn(1)
-        weight_quant(1)
-        for s in range(2):
-            for k in range(8):
-                b_xh(s, k, ptag())
-                b_xh_evac(s, k, both[(k // 2) % 2])
+        load_xn(1, 0)
+        load_xs(0, 1, 0)
+        load_xs(0, 1, 1)
+        load_xn(0, 1)
+        load_xn(1, 1)
+        for k in range(8):
+            b_xh(0, k, ptag())
+            b_xh_evac(0, k, both[(k // 2) % 2])
         for lp in range(8):
             in_transpose(1, 0, lp, ptag())
-            if lp >= 1:
-                in_evac(1, 0, lp - 1, both)
-        in_evac(1, 0, 7, both)
+            in_evac(1, 0, lp, both)
         in_quant(1, 0, 0)
-        in_quant(1, 0, 1)
+        for q4 in range(4):
+            xc_transpose(0, q4, ptag())
+        xc_evac(0, 0, sc_copy)
+        xc_evac(0, 1, sc_copy)
+        xc_quant(0, 0)
+        xc_evac(0, 2, sc_copy)
+        xc_evac(0, 3, sc_copy)
         weight_prep(2, sc_copy)
         weight_prep(3, sc_copy)
-
         for h8 in range(8):
             b_xw(0, h8, ptag())
-        for h8 in range(8):
             b_add(0, h8)
-            if h8 < 4:
-                b_xw(1, h8, ptag())
         weight_quant(2)
         weight_quant(3)
+        xc_quant(0, 1)
+        in_quant(1, 0, 1)
+        for k in range(8):
+            b_xh(1, k, ptag())
+            b_xh_evac(1, k, sc_copy)
         for gb in range(8):
             b_t(0, gb, ptag())
             b_t_evac(0, gb, sc_copy)
-            if gb < 4:
-                b_add(1, gb)
-        for d8 in range(8):
-            b_bias(0, d8)
-        for h8 in range(4, 8):
+        b_bias(0, 0)
+        for h8 in range(8):
             b_xw(1, h8, ptag())
             b_add(1, h8)
-        for f in xc_steps(0, ("ss",), sc_copy):
-            f()
 
-        def t_jobs(s):
-            jobs = [
-                ("T", lambda gb=gb: b_t(s, gb, "ss"), lambda gb=gb: b_t_evac(s, gb, sc_copy), ("add", s), None)
-                for gb in range(8)
-            ]
-            jobs.append(("G", lambda: [b_bias(s, d8) for d8 in range(8)], None, None, ("a", s)))
+        def tr_jobs(s):
+            jobs = [("T", lambda gb=gb: b_t(s, gb, "ss"), lambda gb=gb: b_t_evac(s, gb, sc_copy), []) for gb in range(8)]
             return jobs
 
-        def i_jobs(which):
-            jobs = [("V", lambda q=q: in_relayout(which, 1, q), 2, None, None) for q in range(2)]
-            if which == 0:
-                jobs.append(("G", lambda: (load_xs(1, 1, 0), load_xs(1, 1, 1)), None, None, None))
-            jobs += [
-                ("T", lambda lp=lp: in_transpose(which, 1, lp, "ss"), lambda lp=lp: in_evac(which, 1, lp, only_s), None, None)
+        def in_jobs(which):
+            jobs = [
+                ("T", lambda lp=lp: in_transpose(which, 1, lp, "ss"), lambda lp=lp: in_evac(which, 1, lp, only_s), [])
                 for lp in range(8)
             ]
-            jobs.append(("V", lambda: in_quant(which, 1, 0), 2, None, ("q0", which)))
-            jobs.append(("V", lambda: in_quant(which, 1, 1), 2, None, ("q1", which)))
+            jobs[7][3].extend([lambda: in_quant(which, 1, 0), lambda: in_quant(which, 1, 1)])
             return jobs
 
         def ic_jobs(s):
-            jobs = []
-            for half in range(2):
-                for pr in range(2):
-                    jobs.append(
-                        (
-                            "T",
-                            lambda q=2 * half + pr: xc_transpose(s, q, "ss"),
-                            lambda q=2 * half + pr: xc_evac(s, q, sc_copy),
-                            ("tile", 8 * s - 9),
-                            None,
-                        )
-                    )
-                jobs.append(("V", lambda half=half: xc_quant(s, half), 1, None, ("cc", s) if half == 1 else None))
+            jobs = [("T", lambda q=q: xc_transpose(s, q, "ss"), lambda q=q: xc_evac(s, q, sc_copy), []) for q in range(4)]
+            jobs[1][3].append(lambda: xc_quant(s, 0))
+            jobs[3][3].append(lambda: xc_quant(s, 1))
             return jobs
 
         def xh_jobs(s):
-            return [
-                ("X", lambda k=k: b_xh(s, k, "ss"), lambda k=k: b_xh_evac(s, k, sc_copy), ("q1", 0), ("xh", s) if k == 7 else None)
-                for k in range(8)
-            ]
+            return [("M", lambda k=k: b_xh(s, k, "ss"), lambda k=k: b_xh_evac(s, k, sc_copy), []) for k in range(8)]
 
         def xw_jobs(s):
-            return [
-                ("W", lambda h8=h8: b_xw(s, h8, "ss"), lambda h8=h8: b_add(s, h8), ("xh", s), ("add", s) if h8 == 7 else None)
-                for h8 in range(8)
-            ]
+            return [("W", lambda h8=h8: b_xw(s, h8, "ss"), lambda h8=h8: b_add(s, h8), []) for h8 in range(8)]
 
-        queues = [
-            ic_jobs(1) + t_jobs(1),
-            i_jobs(0) + i_jobs(1) + xw_jobs(2) + t_jobs(2) + xw_jobs(3) + t_jobs(3),
-            xh_jobs(2) + xh_jobs(3),
-            ic_jobs(2) + ic_jobs(3),
-        ]
-        rank = {"T": 0, "V": 1, "X": 2, "W": 2, "G": 3}
-        flags = {("add", 1): -1, ("a", 0): -1, ("cc", 0): -1}
+        def mix(a, b):
+            return [job for pair in zip(a, b) for job in pair]
+
+        first = ic_jobs(1)
+        first[0][3].extend([lambda: in_relayout(0, 1, 0), lambda: in_relayout(0, 1, 1)])
+        first[0][3].extend([lambda: load_xs(1, 1, 0), lambda: load_xs(1, 1, 1)])
+        second = in_jobs(0)
+        second[7][3].extend([lambda: in_relayout(1, 1, 0), lambda: in_relayout(1, 1, 1)])
+        side = first + mix(tr_jobs(1), second) + (
+            xh_jobs(2)[:4]
+            + mix(in_jobs(1)[:4], xh_jobs(2)[4:])
+            + in_jobs(1)[4:]
+            + xw_jobs(2)
+            + ic_jobs(2)
+            + tr_jobs(2)
+            + xh_jobs(3)
+            + xw_jobs(3)
+            + ic_jobs(3)
+            + tr_jobs(3)
+        )
+
         NT = 32
-        due = {}
-
-        def later(c, what, arg):
-            due[c] = due.get(c, []) + [(what, arg)]
-
-        def todo(c, what):
-            return [a for (w, a) in due.get(c, []) if w == what]
-
-        pend = []
-        pos = [0, 0, 0, 0]
-        nxt = {"v1": 0, "pe1": 1, "left": NT}
+        taken = 0
+        adds = []
+        att(0, 0)
+        att(0, 1)
         pe1(0)
-        c = 0
-        while nxt["left"] > 0:
-            assert c < 200
-            n = nxt["v1"]
-            go = n < NT and ("a", n // 8) in flags
-            hid_jobs = todo(c, "pe2")
-            banks = (4 if go else 5) - len(hid_jobs)
-            vbud = 3 if go else 4
-            wbud = 2
-            take = []
-            for qi, qu in enumerate(queues):
-                top = 0
-                while pos[qi] < len(qu):
-                    typ, f1, f2, needs, sets = qu[pos[qi]]
-                    if rank[typ] < top:
-                        break
-                    if needs is not None:
-                        if needs[0] == "tile":
-                            if nxt["pe1"] <= needs[1] + 1:
-                                break
-                        elif needs not in flags or (flags[needs] == c and needs[0] != "q1" and needs[0] != "xh"):
-                            break
-                    if typ in ("T", "X", "W"):
-                        if banks <= 0 or (typ == "W" and wbud == 0):
-                            break
-                        banks -= 1
-                        if typ == "W":
-                            wbud -= 1
-                    if typ == "V":
-                        if vbud < f2:
-                            break
-                        vbud -= f2
-                    top = rank[typ]
-                    if sets is not None:
-                        flags[sets] = c
-                    take.append(qu[pos[qi]])
-                    pos[qi] += 1
-            pass
-            for f in pend:
+        for c in range(NT + 7):
+            pair = (c - 2) // 2
+            hid_due = c % 2 == 0 and 0 <= pair < NT // 2
+            room = 4 - (1 if hid_due else 0)
+            jobs = side[taken : taken + room]
+            taken += len(jobs)
+            for f in adds:
                 f()
-            pend = []
-            for j in hid_jobs:
-                pe2(j)
-            for e in take:
-                if e[0] == "T":
-                    e[1]()
-            for j in hid_jobs:
-                s2c(j)
-            for e in take:
-                if e[0] == "T":
-                    e[2]()
-            if go:
-                v1(n)
-                nxt["v1"] = n + 1
-                if n % 2 == 1:
-                    later(c + 1, "pe2", n // 2)
-                    if n % 4 == 3:
-                        later(c + 1, "qh", n // 4)
-                        for k in range(4):
-                            step = k if n < NT - 1 else 0
-                            later(c + step, "gx", n - 3 + k)
-                            later(c + 2 + step, "pe3", n - 3 + k)
-                            later(c + 3 + step, "v3", n - 3 + k)
-            m = nxt["pe1"]
-            if m < NT and m <= nxt["v1"] and ("cc", m // 8) in flags and flags["cc", m // 8] < c:
-                pe1(m)
-                nxt["pe1"] = m + 1
-            for a in todo(c, "v3"):
-                v3(a)
-                nxt["left"] -= 1
-            for a in todo(c, "pe3"):
-                pe3(a, ("pf", "pc", "pa", "ss")[a % 4] if a >= NT - 4 else "pf")
-            for a in todo(c, "qh"):
-                qh(a)
-            for e in take:
-                if e[0] == "V":
-                    e[1]()
-            for e in take:
-                if e[0] == "X":
-                    e[1]()
-                    e[2]()
-                if e[0] == "W":
-                    e[1]()
-                    pend.append(e[2])
-            for a in todo(c, "gx"):
-                gx(a)
-            for e in take:
-                if e[0] == "G":
-                    e[1]()
-            c += 1
-        assert all(pos[qi] == len(qu) for qi, qu in enumerate(queues))
+            adds = []
+            runs = ([lambda: pe2(pair)] if hid_due else []) + [j[1] for j in jobs if j[0] == "T"]
+            for i in range(max(len(runs), 2)):
+                if i < len(runs):
+                    runs[i]()
+                if i < 2 and c + 1 < NT:
+                    att(c + 1, i)
+            if hid_due:
+                s2c(pair)
+            for j in jobs:
+                if j[0] == "T":
+                    j[2]()
+            if c < NT:
+                v1(c)
+            if c + 1 < NT:
+                pe1(c + 1)
+            if 0 <= c - 6 < NT:
+                v3(c - 6)
+            if 0 <= c - 5 < NT:
+                pe3(c - 5)
+            if c % 4 == 0 and 0 <= (c - 4) // 4 < NT // 4:
+                qh((c - 4) // 4)
+            for j in jobs:
+                if j[0] == "M":
+                    j[1]()
+                    j[2]()
+                if j[0] == "W":
+                    j[1]()
+                    adds.append(j[2])
+                for f in j[3]:
+                    f()
+            if c + 1 < NT:
+                b_bias((c + 1) // 8, (c + 1) % 8)
+            if 0 <= c - 4 < NT:
+                gx(c - 4)
+        assert taken == len(side)

@@ -13,6 +13,7 @@ MULT = mybir.AluOpType.mult
 
 P = 128
 C = 512
+REP = 2
 FLOPS = 4 * 2 * 4096 * 512 * 512 + 2 * 8192 * 256 * 256
 
 
@@ -342,7 +343,8 @@ def tile_mlpp_pa_kernel(tc, x, W_h, b_h, W_w, b_w, W_c, b_c, W_attn, b_attn, W_1
             cc, sc = st["cc", s]
             rc, rs = wslice(2, 0, C)
             pc = bank("pc")
-            nc.tensor.matmul_mx(
+            for rep in range(REP):
+              nc.tensor.matmul_mx(
                 out=pc[:],
                 lhsT=cc[:, d8 * P : (d8 + 1) * P].bitcast(FP8X4),
                 lhsT_scale=sc[:, d8 * P : (d8 + 1) * P],
@@ -417,7 +419,8 @@ def tile_mlpp_pa_kernel(tc, x, W_h, b_h, W_w, b_w, W_c, b_c, W_attn, b_attn, W_1
             j = n % 4
             rc, rs = wslice(3, 0, C)
             pf = bank(tag)
-            nc.tensor.matmul_mx(
+            for rep in range(REP):
+              nc.tensor.matmul_mx(
                 out=pf[:],
                 lhsT=chid[:, j * P : (j + 1) * P].bitcast(FP8X4),
                 lhsT_scale=shid[:, j * P : (j + 1) * P],
@@ -607,7 +610,7 @@ def tile_mlpp_pa_kernel(tc, x, W_h, b_h, W_w, b_w, W_c, b_c, W_attn, b_attn, W_1
             if 0 <= c - 6 < NT:
                 v3(c - 6)
             if 0 <= c - 5 < NT:
-                pe3(c - 5)
+                pe3(c - 5, "ss" if taken == len(side) else "pf")
             if c % 4 == 0 and 0 <= (c - 4) // 4 < NT // 4:
                 qh((c - 4) // 4)
             for j in jobs:

@@ -13,7 +13,6 @@ MULT = mybir.AluOpType.mult
 
 P = 128
 C = 512
-REP = 2
 FLOPS = 4 * 2 * 4096 * 512 * 512 + 2 * 8192 * 256 * 256
 
 
@@ -109,12 +108,10 @@ def tile_mlpp_pa_kernel(tc, x, W_h, b_h, W_w, b_w, W_c, b_c, W_attn, b_attn, W_1
         nc.scalar.dma_start(out=wattn[:], in_=W_attn.rearrange("(k p) n -> p k n", p=P))
         b1bc = consts.tile([P, C], BF16, tag="b1bc")
         nc.scalar.dma_start(out=b1bc[:], in_=b_1.partition_broadcast(P))
-        bcbc = consts.tile([P, C], BF16, tag="bcbc")
-        nc.scalar.dma_start(out=bcbc[:], in_=b_c.partition_broadcast(P))
-        tb = consts.tile([P, 32], BF16, tag="tb")
-        nc.vector.memset(tb[:], 0.0)
-        nc.scalar.dma_start(out=tb[0:16, :], in_=b_w.rearrange("(w g) -> w g", g=32))
-        nc.scalar.dma_start(out=tb[16:32, :], in_=b_h.rearrange("(h g) -> h g", g=32))
+        tb = consts.tile([P, C], BF16, tag="tb")
+        nc.scalar.dma_start(out=tb[0:16, 0:32], in_=b_w.rearrange("(w g) -> w g", g=32))
+        nc.scalar.dma_start(out=tb[16:32, 0:32], in_=b_h.rearrange("(h g) -> h g", g=32))
+        nc.scalar.dma_start(out=tb[32:33, :], in_=b_c.rearrange("(o c) -> o c", o=1))
         tba = consts.tile([P, P], BF16, tag="tba")
         nc.vector.memset(tba[:], 0.0)
         nc.scalar.dma_start(out=tba[0:2, :], in_=b_attn.rearrange("(k p) -> k p", p=P))
@@ -168,18 +165,6 @@ def tile_mlpp_pa_kernel(tc, x, W_h, b_h, W_w, b_w, W_c, b_c, W_attn, b_attn, W_1
                 in_=st["gr", which, dlo][:, qn * 4096 : (qn + 1) * 4096],
             )
 
-        def input_steps(which, dlo, tags, copies):
-            steps = []
-            steps.append(lambda: in_relayout(which, dlo, 0))
-            steps.append(lambda: in_relayout(which, dlo, 1))
-            steps.append(lambda: in_transpose(which, dlo, 0, tags[0]))
-            for lp in range(1, 8):
-                steps.append(lambda lp=lp: (in_transpose(which, dlo, lp, tags[lp % len(tags)]), in_evac(which, dlo, lp - 1, copies)))
-            steps.append(lambda: in_evac(which, dlo, 7, copies))
-            steps.append(lambda: in_quant(which, dlo, 0))
-            steps.append(lambda: in_quant(which, dlo, 1))
-            return steps
-
         xn = []
 
         def load_xn(k, dlo):
@@ -223,17 +208,6 @@ def tile_mlpp_pa_kernel(tc, x, W_h, b_h, W_w, b_w, W_c, b_c, W_attn, b_attn, W_1
                 scales=sc[:, half * C : (half + 1) * C],
                 in_=st["gc", s][:, half * 2048 : (half + 1) * 2048],
             )
-
-        def xc_steps(s, tags, copy):
-            steps = []
-            steps.append(lambda: xc_transpose(s, 0, tags[0]))
-            steps.append(lambda: (xc_transpose(s, 1, tags[1 % len(tags)]), xc_evac(s, 0, copy)))
-            steps.append(lambda: xc_evac(s, 1, copy))
-            steps.append(lambda: (xc_transpose(s, 2, tags[0]), xc_quant(s, 0)))
-            steps.append(lambda: (xc_transpose(s, 3, tags[1 % len(tags)]), xc_evac(s, 2, copy)))
-            steps.append(lambda: xc_evac(s, 3, copy))
-            steps.append(lambda: xc_quant(s, 1))
-            return steps
 
         def b_xh(s, k, tag):
             dlo, hh = s // 2, s % 2
@@ -296,7 +270,21 @@ def tile_mlpp_pa_kernel(tc, x, W_h, b_h, W_w, b_w, W_c, b_c, W_attn, b_attn, W_1
             pst = bank(tag)
             for gi in range(4):
                 g = 4 * gb + gi
-                nc.tensor.transpose(pst[:, gi * P : (gi + 1) * P], s2[:, g * P : (g + 1) * P], ident_f[:])
+                nc.tensor.matmul(
+                    out=pst[:, gi * P : (gi + 1) * P],
+                    lhsT=st["sel", s % 2][:].rearrange("p a w -> p (a w)"),
+                    rhs=rtab[:, g * P : (g + 1) * P],
+                    start=True,
+                    stop=False,
+                )
+                nc.tensor.matmul(
+                    out=pst[:, gi * P : (gi + 1) * P],
+                    lhsT=s2[:, g * P : (g + 1) * P],
+                    rhs=ident_f[:],
+                    is_transpose=True,
+                    start=False,
+                    stop=True,
+                )
             st["pst", s, gb] = pst
 
         def b_t_evac(s, gb, copy):
@@ -309,30 +297,6 @@ def tile_mlpp_pa_kernel(tc, x, W_h, b_h, W_w, b_w, W_c, b_c, W_attn, b_attn, W_1
                 in_=st["pst", s, gb][:].rearrange("p (g l a) -> p a l g", g=4, l=16, a=8),
             )
 
-        def b_bias(s, d8):
-            a = st["a", s]
-            nc.gpsimd.tensor_tensor(
-                out=a[:, d8 * C : (d8 + 1) * C], in0=a[:, d8 * C : (d8 + 1) * C], in1=bias_n[:, s % 2, :], op=ADD
-            )
-
-        def beta_steps(s, mtags, ttags, copies):
-            steps = []
-            nm, nt, ncp = len(mtags), len(ttags), len(copies)
-            steps.append(lambda: b_xh(s, 0, mtags[0]))
-            for k in range(1, 8):
-                steps.append(lambda k=k: (b_xh(s, k, mtags[k % nm]), b_xh_evac(s, k - 1, copies[((k - 1) // 2) % ncp])))
-            steps.append(lambda: (b_xw(s, 0, mtags[0]), b_xh_evac(s, 7, copies[3 % ncp])))
-            for h8 in range(1, 8):
-                steps.append(lambda h8=h8: (b_xw(s, h8, mtags[h8 % nm]), b_add(s, h8 - 1)))
-            steps.append(lambda: b_add(s, 7))
-            steps.append(lambda: b_t(s, 0, ttags[0]))
-            for gb in range(1, 8):
-                steps.append(lambda gb=gb: (b_t(s, gb, ttags[gb % nt]), b_t_evac(s, gb - 1, copies[((gb - 1) // 2) % ncp])))
-            steps.append(lambda: b_t_evac(s, 7, copies[3 % ncp]))
-            for d8 in range(8):
-                steps.append(lambda d8=d8: b_bias(s, d8))
-            return steps
-
         def where(n):
             s = n // 8
             return s, s // 2, s % 2, n % 8
@@ -343,8 +307,7 @@ def tile_mlpp_pa_kernel(tc, x, W_h, b_h, W_w, b_w, W_c, b_c, W_attn, b_attn, W_1
             cc, sc = st["cc", s]
             rc, rs = wslice(2, 0, C)
             pc = bank("pc")
-            for rep in range(REP):
-              nc.tensor.matmul_mx(
+            nc.tensor.matmul_mx(
                 out=pc[:],
                 lhsT=cc[:, d8 * P : (d8 + 1) * P].bitcast(FP8X4),
                 lhsT_scale=sc[:, d8 * P : (d8 + 1) * P],
@@ -419,8 +382,7 @@ def tile_mlpp_pa_kernel(tc, x, W_h, b_h, W_w, b_w, W_c, b_c, W_attn, b_attn, W_1
             j = n % 4
             rc, rs = wslice(3, 0, C)
             pf = bank(tag)
-            for rep in range(REP):
-              nc.tensor.matmul_mx(
+            nc.tensor.matmul_mx(
                 out=pf[:],
                 lhsT=chid[:, j * P : (j + 1) * P].bitcast(FP8X4),
                 lhsT_scale=shid[:, j * P : (j + 1) * P],
@@ -434,7 +396,7 @@ def tile_mlpp_pa_kernel(tc, x, W_h, b_h, W_w, b_w, W_c, b_c, W_attn, b_attn, W_1
         def v3(n):
             s, dlo, hh, d8 = where(n)
             d = 2 * d8 + dlo
-            o = three.tile([P, C], F32, tag="o")
+            o = two.tile([P, C], F32, tag="o")
             nc.vector.tensor_tensor(out=o[:], in0=st["pf", n][:], in1=st["xpb", n][:], op=ADD)
             nc.sync.dma_start(out=outv[hh][:, d, :], in_=o[:])
 
@@ -453,11 +415,23 @@ def tile_mlpp_pa_kernel(tc, x, W_h, b_h, W_w, b_w, W_c, b_c, W_attn, b_attn, W_1
         load_w(2, W_c)
         nc.sync.dma_start(out=wrv[:, 3, :, :], in_=W_1.rearrange("(t p) n -> p t n", p=P))
 
-        tbx = consts.tile([P, 16, 32], BF16, tag="tbx")
-        nc.vector.tensor_copy(out=tbx[:], in_=tb[:].unsqueeze(1).to_broadcast([P, 16, 32]))
+        rtab = consts.tile([P, 4096], BF16, tag="rtab")
+        nc.vector.memset(rtab[:], 0.0)
+        nc.vector.tensor_copy(
+            out=rtab[0:32, :].rearrange("p (g x) -> p g x", g=32, x=P),
+            in_=tb[0:32, 0:32].unsqueeze(2).to_broadcast([32, 32, P]),
+        )
+        nc.vector.tensor_copy(
+            out=rtab[32:33, :].rearrange("p (g l a) -> p g l a", g=32, l=16, a=8),
+            in_=tb[32:33, :].rearrange("p (l g) -> p g l", l=16, g=32).unsqueeze(3).to_broadcast([1, 32, 16, 8]),
+        )
         selw = consts.tile([P, 8, 16], BF16, tag="selw")
-        nc.vector.tensor_copy(out=selw[:], in_=ident_b[:, 0:16].unsqueeze(1).to_broadcast([P, 8, 16]))
-        bias_n = consts.tile([P, 2, C], F32, tag="bias_n")
+        nc.vector.tensor_tensor(
+            out=selw[:],
+            in0=ident_b[:, 0:16].unsqueeze(1).to_broadcast([P, 8, 16]),
+            in1=ident_b[:, 32:33].unsqueeze(1).to_broadcast([P, 8, 16]),
+            op=ADD,
+        )
         for hh in range(2):
             sel = consts.tile([P, 8, 16], BF16, name="sel%d" % hh, tag="sel%d" % hh)
             nc.vector.tensor_tensor(
@@ -466,15 +440,7 @@ def tile_mlpp_pa_kernel(tc, x, W_h, b_h, W_w, b_w, W_c, b_c, W_attn, b_attn, W_1
                 in1=ident_b[:, 16 + 8 * hh : 24 + 8 * hh].unsqueeze(2).to_broadcast([P, 8, 16]),
                 op=ADD,
             )
-            pb = bank(ptag())
-            nc.tensor.matmul(
-                out=pb[:],
-                lhsT=sel[:].rearrange("p a w -> p (a w)"),
-                rhs=tbx[:].rearrange("p l g -> p (l g)"),
-                start=True,
-                stop=True,
-            )
-            nc.vector.tensor_tensor(out=bias_n[:, hh, :], in0=pb[:], in1=bcbc[:], op=ADD)
+            st["sel", hh] = sel
         pta = bank(ptag(), BF16, P)
         nc.tensor.transpose(pta[:], tba[:], ident_b[:])
         ap1 = consts.tile([P, 2], F32, tag="ap1")
@@ -527,7 +493,6 @@ def tile_mlpp_pa_kernel(tc, x, W_h, b_h, W_w, b_w, W_c, b_c, W_attn, b_attn, W_1
         for gb in range(8):
             b_t(0, gb, ptag())
             b_t_evac(0, gb, sc_copy)
-        b_bias(0, 0)
         for h8 in range(8):
             b_xw(1, h8, ptag())
             b_add(1, h8)
@@ -622,8 +587,6 @@ def tile_mlpp_pa_kernel(tc, x, W_h, b_h, W_w, b_w, W_c, b_c, W_attn, b_attn, W_1
                     adds.append(j[2])
                 for f in j[3]:
                     f()
-            if c + 1 < NT:
-                b_bias((c + 1) // 8, (c + 1) % 8)
             if 0 <= c - 4 < NT:
                 gx(c - 4)
         assert taken == len(side)

@@ -338,10 +338,19 @@ def tile_mlpp_pa_kernel(tc, x, W_h, b_h, W_w, b_w, W_c, b_c, W_attn, b_attn, W_1
                 hidn = two.tile([P, 2, C], BF16, tag="hidn")
                 st["hidn", n // 2] = hidn
             hidn = st["hidn", n // 2]
-            bsum = two.tile([P, C], F32, tag="bsum")
+            bsum = one.tile([P, C], F32, tag="bsum")
             nc.vector.tensor_tensor(out=bsum[:], in0=st["pc", n][:], in1=st["a", s][:, d8 * C : (d8 + 1) * C], op=ADD)
+            st["bsum", n] = bsum
+
+        def v2(n):
+            hh = (n // 8) % 2
             nc.vector.scalar_tensor_tensor(
-                out=hidn[:, n % 2, :], in0=st["pa", n][:], scalar=ap1[:, hh : hh + 1], in1=bsum[:], op0=ADD, op1=MULT
+                out=st["hidn", n // 2][:, n % 2, :],
+                in0=st["pa", n][:],
+                scalar=ap1[:, hh : hh + 1],
+                in1=st["bsum", n][:],
+                op0=ADD,
+                op1=MULT,
             )
 
         def pe2(j):
@@ -396,7 +405,7 @@ def tile_mlpp_pa_kernel(tc, x, W_h, b_h, W_w, b_w, W_c, b_c, W_attn, b_attn, W_1
         def v3(n):
             s, dlo, hh, d8 = where(n)
             d = 2 * d8 + dlo
-            o = two.tile([P, C], F32, tag="o")
+            o = three.tile([P, C], F32, tag="o")
             nc.vector.tensor_tensor(out=o[:], in0=st["pf", n][:], in1=st["xpb", n][:], op=ADD)
             nc.sync.dma_start(out=outv[hh][:, d, :], in_=o[:])
 
@@ -574,8 +583,8 @@ def tile_mlpp_pa_kernel(tc, x, W_h, b_h, W_w, b_w, W_c, b_c, W_attn, b_attn, W_1
                 pe1(c + 1)
             if 0 <= c - 6 < NT:
                 v3(c - 6)
-            if 0 <= c - 5 < NT:
-                pe3(c - 5, "ss" if taken == len(side) else "pf")
+            if c < NT:
+                v2(c)
             if c % 4 == 0 and 0 <= (c - 4) // 4 < NT // 4:
                 qh((c - 4) // 4)
             for j in jobs:
@@ -587,6 +596,8 @@ def tile_mlpp_pa_kernel(tc, x, W_h, b_h, W_w, b_w, W_c, b_c, W_attn, b_attn, W_1
                     adds.append(j[2])
                 for f in j[3]:
                     f()
+            if 0 <= c - 5 < NT:
+                pe3(c - 5, "ss" if taken == len(side) else "pf")
             if 0 <= c - 4 < NT:
                 gx(c - 4)
         assert taken == len(side)

@@ -25,6 +25,7 @@ def tile_mlpp_pa_kernel(tc, x, W_h, b_h, W_w, b_w, W_c, b_c, W_attn, b_attn, W_1
         one = ctx.enter_context(tc.tile_pool(name="one", bufs=1))
         two = ctx.enter_context(tc.tile_pool(name="two", bufs=2))
         three = ctx.enter_context(tc.tile_pool(name="three", bufs=3))
+        five = ctx.enter_context(tc.tile_pool(name="five", bufs=5))
         ps1 = ctx.enter_context(tc.psum_pool(name="ps1", bufs=1))
         ps5 = ctx.enter_context(tc.psum_pool(name="ps5", bufs=4))
         ps2 = ctx.enter_context(tc.psum_pool(name="ps2", bufs=2))
@@ -68,10 +69,8 @@ def tile_mlpp_pa_kernel(tc, x, W_h, b_h, W_w, b_w, W_c, b_c, W_attn, b_attn, W_1
                     nc.sync.dma_start(out=xs[a8 : P : 8, :, :], in_=x2v[:, 8 * q : 8 * q + 8, a8, dlo, :])
             st["xs", which, dlo, q] = xs[:]
 
-        wraw = two.tile([P, 8192], BF16, tag="a", align_bytes=64)
+        wraw = two.tile([P, 8192], BF16, tag="s2", align_bytes=64)
         wrv = wraw[:].rearrange("p (i t n) -> p i t n", i=4, t=4, n=C)
-        wg = two.tile([P, 8192], BF16, tag="a", align_bytes=64)
-        wgv = wg[:].rearrange("p (i n t) -> p i n t", i=4, n=C, t=4)
         wcodes = consts.tile([P, 2048], U32, tag="wcodes", align_bytes=64)
         wscl = consts.tile([P, 2048], U8, tag="wscl", align_bytes=64)
 
@@ -84,18 +83,23 @@ def tile_mlpp_pa_kernel(tc, x, W_h, b_h, W_w, b_w, W_c, b_c, W_attn, b_attn, W_1
 
         load_xs(0, 0, 0)
         load_xs(0, 0, 1)
+        load_x2_first()
         load_w(0, W_h)
         load_w(1, W_w)
-        load_x2_first()
 
         def weight_prep(i, eng_copy):
-            eng_copy(out=wgv[:, i], in_=wrv[:, i].rearrange("p t n -> p n t"))
+            wg = one.tile([P, 2048], BF16, tag="ghid", align_bytes=64)
+            st["wg", i] = wg
+            eng_copy(
+                out=wg[:].rearrange("p (n i t) -> p n t i", n=P, i=4, t=4),
+                in_=wrv[:, i].rearrange("p t (n i) -> p n t i", n=P, i=4),
+            )
 
         def weight_quant(i):
             nc.vector.quantize_mx(
                 out=wcodes[:, i * C : (i + 1) * C].bitcast(FP8X4),
                 scales=wscl[:, i * C : (i + 1) * C],
-                in_=wg[:, i * 2048 : (i + 1) * 2048],
+                in_=st["wg", i][:],
             )
 
         def wslice(i, c0, n):
@@ -105,26 +109,30 @@ def tile_mlpp_pa_kernel(tc, x, W_h, b_h, W_w, b_w, W_c, b_c, W_attn, b_attn, W_1
             )
 
         wattn = consts.tile([P, 2, 256], BF16, tag="wattn")
-        nc.scalar.dma_start(out=wattn[:], in_=W_attn.rearrange("(k p) n -> p k n", p=P))
+        nc.sync.dma_start(out=wattn[:], in_=W_attn.rearrange("(k p) n -> p k n", p=P))
         b1bc = consts.tile([P, C], BF16, tag="b1bc")
-        nc.scalar.dma_start(out=b1bc[:], in_=b_1.partition_broadcast(P))
         tb = consts.tile([P, C], BF16, tag="tb")
-        nc.scalar.dma_start(out=tb[0:16, 0:32], in_=b_w.rearrange("(w g) -> w g", g=32))
-        nc.scalar.dma_start(out=tb[16:32, 0:32], in_=b_h.rearrange("(h g) -> h g", g=32))
-        nc.scalar.dma_start(out=tb[32:33, :], in_=b_c.rearrange("(o c) -> o c", o=1))
+        nc.sync.dma_start(out=tb[0:16, 0:32], in_=b_w.rearrange("(w g) -> w g", g=32))
+        nc.sync.dma_start(out=tb[16:32, 0:32], in_=b_h.rearrange("(h g) -> h g", g=32))
+        nc.sync.dma_start(out=tb[32:33, :], in_=b_c.rearrange("(o c) -> o c", o=1))
         tba = consts.tile([P, P], BF16, tag="tba")
         nc.vector.memset(tba[:], 0.0)
-        nc.scalar.dma_start(out=tba[0:2, :], in_=b_attn.rearrange("(k p) -> k p", p=P))
+        nc.sync.dma_start(out=tba[0:2, :], in_=b_attn.rearrange("(k p) -> k p", p=P))
 
-        def in_relayout(which, dlo, q):
-            if q == 0:
-                rl = one.tile([P, 8192], BF16, tag="rl")
+        def in_relayout(which, dlo, q, eng_copy, piece=0, pieces=1):
+            if q == 0 and piece == 0:
+                if which == 1 and dlo == 0:
+                    rl = two.tile([P, 8192], BF16, tag="a", align_bytes=64)
+                else:
+                    rl = one.tile([P, 8192], BF16, tag="rl")
                 st["rl", which, dlo] = rl
             rl = st["rl", which, dlo]
             rl4 = rl[:].rearrange("p (l y g) -> p l y g", l=16, y=16, g=32)
             xs = st["xs", which, dlo, q]
-            nc.vector.tensor_copy(
-                out=rl4[:, :, 8 * q : 8 * q + 8, :], in_=xs.rearrange("p y (l g) -> p l y g", l=16, g=32)
+            ls = slice(16 // pieces * piece, 16 // pieces * (piece + 1))
+            eng_copy(
+                out=rl4[:, ls, 8 * q : 8 * q + 8, :],
+                in_=xs.rearrange("p y (l g) -> p l y g", l=16, g=32)[:, ls, :, :],
             )
 
         def in_transpose(which, dlo, lp, tag):
@@ -137,9 +145,12 @@ def tile_mlpp_pa_kernel(tc, x, W_h, b_h, W_w, b_w, W_c, b_c, W_attn, b_attn, W_1
                     nc.tensor.transpose(pt[:, s0 : s0 + P], rlw[:, w0 : w0 + P], ident_f[:])
             st["pt", which, dlo, lp] = pt
 
-        def in_evac(which, dlo, lp, copies):
+        def in_evac(which, dlo, lp, copy):
             if lp == 0:
-                gr = one.tile([P, 8192], BF16, tag="gr", align_bytes=64)
+                if which == 1 and dlo == 0:
+                    gr = two.tile([P, 8192], BF16, tag="a", align_bytes=64)
+                else:
+                    gr = one.tile([P, 8192], BF16, tag="gr", align_bytes=64)
                 st["gr", which, dlo] = gr
             gr = st["gr", which, dlo]
             grw = gr[:].bitcast(F32).rearrange("p (y l a u) -> p y l a u", y=16, l=16, a=8, u=2)
@@ -147,7 +158,7 @@ def tile_mlpp_pa_kernel(tc, x, W_h, b_h, W_w, b_w, W_c, b_c, W_attn, b_attn, W_1
             for li in range(2):
                 half_bank = pt[:, li * 256 : (li + 1) * 256]
                 src = half_bank.rearrange("p (u y a) -> p y a u", u=2, y=16, a=8)
-                copies[li](out=grw[:, :, 2 * lp + li, :, :], in_=src)
+                copy(out=grw[:, :, 2 * lp + li, :, :], in_=src)
 
         def in_quant(which, dlo, qn):
             if qn == 0:
@@ -172,7 +183,7 @@ def tile_mlpp_pa_kernel(tc, x, W_h, b_h, W_w, b_w, W_c, b_c, W_attn, b_attn, W_1
                 xnk = two.tile([P, 8192], BF16, name="xn%d" % k, tag="xn", align_bytes=64)
                 xn.append(xnk)
             nc.sync.dma_start(
-                out=xn[k][:].rearrange("p (a e c) -> p a e c", a=8, e=2, c=C)[:, :, dlo, :],
+                out=xn[k][:, dlo * 4096 : (dlo + 1) * 4096].rearrange("p (a c) -> p a c", a=8, c=C),
                 in_=xnv[k].rearrange("p (a e c) -> p a e c", a=8, e=2, c=C)[:, :, dlo, :],
             )
 
@@ -181,10 +192,10 @@ def tile_mlpp_pa_kernel(tc, x, W_h, b_h, W_w, b_w, W_c, b_c, W_attn, b_attn, W_1
             xw32 = xn[hh][:].bitcast(F32)
             pt = bank(tag)
             for i in range(2):
-                d = 2 * (pr4 * 2 + i) + dlo
+                w0 = (8 * dlo + pr4 * 2 + i) * 256
                 for u in range(2):
                     s0 = (2 * i + u) * P
-                    nc.tensor.transpose(pt[:, s0 : s0 + P], xw32[:, d * 256 + u * P : d * 256 + (u + 1) * P], ident_f[:])
+                    nc.tensor.transpose(pt[:, s0 : s0 + P], xw32[:, w0 + u * P : w0 + (u + 1) * P], ident_f[:])
             st["pxc", s, pr4] = pt
 
         def xc_evac(s, pr4, copy):
@@ -268,22 +279,22 @@ def tile_mlpp_pa_kernel(tc, x, W_h, b_h, W_w, b_w, W_c, b_c, W_attn, b_attn, W_1
         def b_t(s, gb, tag):
             s2 = st["s2", s]
             pst = bank(tag)
+            nc.tensor.matmul(
+                out=pst[:],
+                lhsT=st["sel", s % 2][:].rearrange("p a w -> p (a w)"),
+                rhs=rtab[:, gb * 64 : (gb + 1) * 64].unsqueeze(2).to_broadcast([P, 64, 8]),
+                start=True,
+                stop=False,
+            )
             for gi in range(4):
                 g = 4 * gb + gi
-                nc.tensor.matmul(
-                    out=pst[:, gi * P : (gi + 1) * P],
-                    lhsT=st["sel", s % 2][:].rearrange("p a w -> p (a w)"),
-                    rhs=rtab[:, g * P : (g + 1) * P],
-                    start=True,
-                    stop=False,
-                )
                 nc.tensor.matmul(
                     out=pst[:, gi * P : (gi + 1) * P],
                     lhsT=s2[:, g * P : (g + 1) * P],
                     rhs=ident_f[:],
                     is_transpose=True,
                     start=False,
-                    stop=True,
+                    stop=(gi == 3),
                 )
             st["pst", s, gb] = pst
 
@@ -303,7 +314,6 @@ def tile_mlpp_pa_kernel(tc, x, W_h, b_h, W_w, b_w, W_c, b_c, W_attn, b_attn, W_1
 
         def pe1(n):
             s, dlo, hh, d8 = where(n)
-            d = 2 * d8 + dlo
             cc, sc = st["cc", s]
             rc, rs = wslice(2, 0, C)
             pc = bank("pc")
@@ -320,14 +330,13 @@ def tile_mlpp_pa_kernel(tc, x, W_h, b_h, W_w, b_w, W_c, b_c, W_attn, b_attn, W_1
 
         def att(n, k):
             s, dlo, hh, d8 = where(n)
-            d = 2 * d8 + dlo
             if k == 0:
                 pa = bank("pa")
                 st["pa", n] = pa
             nc.tensor.matmul(
                 out=st["pa", n][:],
                 lhsT=wattn[:, k, hh * P : (hh + 1) * P],
-                rhs=xn[k][:, d * C : (d + 1) * C],
+                rhs=xn[k][:, (8 * dlo + d8) * C : (8 * dlo + d8 + 1) * C],
                 start=(k == 0),
                 stop=(k == 1),
             )
@@ -335,7 +344,7 @@ def tile_mlpp_pa_kernel(tc, x, W_h, b_h, W_w, b_w, W_c, b_c, W_attn, b_attn, W_1
         def v1(n):
             s, dlo, hh, d8 = where(n)
             if n % 2 == 0:
-                hidn = two.tile([P, 2, C], BF16, tag="hidn")
+                hidn = two.tile([P, 2 * C], BF16, tag="hidn")
                 st["hidn", n // 2] = hidn
             hidn = st["hidn", n // 2]
             bsum = one.tile([P, C], F32, tag="bsum")
@@ -345,7 +354,7 @@ def tile_mlpp_pa_kernel(tc, x, W_h, b_h, W_w, b_w, W_c, b_c, W_attn, b_attn, W_1
         def v2(n):
             hh = (n // 8) % 2
             nc.vector.scalar_tensor_tensor(
-                out=st["hidn", n // 2][:, n % 2, :],
+                out=st["hidn", n // 2][:, (n % 2) * C : (n % 2 + 1) * C],
                 in0=st["pa", n][:],
                 scalar=ap1[:, hh : hh + 1],
                 in1=st["bsum", n][:],
@@ -354,12 +363,10 @@ def tile_mlpp_pa_kernel(tc, x, W_h, b_h, W_w, b_w, W_c, b_c, W_attn, b_attn, W_1
             )
 
         def pe2(j):
-            hidn = st["hidn", j]
-            pht = bank("ss", BF16, 1024)
-            for i in range(2):
-                for t in range(4):
-                    s0 = (4 * i + t) * P
-                    nc.tensor.transpose(pht[:, s0 : s0 + P], hidn[:, i, t * P : (t + 1) * P], ident_b[:])
+            hidw = st["hidn", j][:].bitcast(F32)
+            pht = bank("ss")
+            for q in range(4):
+                nc.tensor.transpose(pht[:, q * P : (q + 1) * P], hidw[:, q * P : (q + 1) * P], ident_f[:])
             st["pht", j] = pht
 
         def s2c(j):
@@ -369,8 +376,8 @@ def tile_mlpp_pa_kernel(tc, x, W_h, b_h, W_w, b_w, W_c, b_c, W_attn, b_attn, W_1
             ghid = st["ghid", j // 2]
             pr = j % 2
             nc.scalar.copy(
-                out=ghid[:, pr * 1024 : (pr + 1) * 1024].rearrange("p (i r t) -> p i r t", i=2, r=P, t=4),
-                in_=st["pht", j][:].rearrange("p (i t r) -> p i r t", i=2, t=4, r=P),
+                out=ghid[:].bitcast(F32)[:, pr * C : (pr + 1) * C].rearrange("p (i r u) -> p i r u", i=2, r=P, u=2),
+                in_=st["pht", j][:].rearrange("p (i u r) -> p i r u", i=2, u=2, r=P),
             )
 
         def qh(m):
@@ -381,9 +388,9 @@ def tile_mlpp_pa_kernel(tc, x, W_h, b_h, W_w, b_w, W_c, b_c, W_attn, b_attn, W_1
 
         def gx(n):
             s, dlo, hh, d8 = where(n)
-            d = 2 * d8 + dlo
-            xpb = three.tile([P, C], F32, tag="xpb")
-            nc.gpsimd.tensor_tensor(out=xpb[:], in0=xn[hh][:, d * C : (d + 1) * C], in1=b1bc[:], op=ADD)
+            e0 = (8 * dlo + d8) * C
+            xpb = five.tile([P, C], F32, tag="xpb")
+            nc.gpsimd.tensor_tensor(out=xpb[:], in0=xn[hh][:, e0 : e0 + C], in1=b1bc[:], op=ADD)
             st["xpb", n] = xpb
 
         def pe3(n, tag="pf"):
@@ -411,8 +418,6 @@ def tile_mlpp_pa_kernel(tc, x, W_h, b_h, W_w, b_w, W_c, b_c, W_attn, b_attn, W_1
 
         sc_copy = nc.scalar.copy
         ve_copy = nc.vector.tensor_copy
-        both = (sc_copy, ve_copy)
-        only_s = (sc_copy, sc_copy)
         rot = {"n": 0}
         ring = ("ss", "ss", "ss", "ss", "pa", "pa", "pc", "pf")
 
@@ -420,20 +425,8 @@ def tile_mlpp_pa_kernel(tc, x, W_h, b_h, W_w, b_w, W_c, b_c, W_attn, b_attn, W_1
             rot["n"] += 1
             return ring[(rot["n"] - 1) % len(ring)]
 
-        load_xn(0, 0)
-        load_w(2, W_c)
-        nc.sync.dma_start(out=wrv[:, 3, :, :], in_=W_1.rearrange("(t p) n -> p t n", p=P))
-
-        rtab = consts.tile([P, 4096], BF16, tag="rtab")
+        rtab = consts.tile([P, C], BF16, tag="rtab")
         nc.vector.memset(rtab[:], 0.0)
-        nc.vector.tensor_copy(
-            out=rtab[0:32, :].rearrange("p (g x) -> p g x", g=32, x=P),
-            in_=tb[0:32, 0:32].unsqueeze(2).to_broadcast([32, 32, P]),
-        )
-        nc.vector.tensor_copy(
-            out=rtab[32:33, :].rearrange("p (g l a) -> p g l a", g=32, l=16, a=8),
-            in_=tb[32:33, :].rearrange("p (l g) -> p g l", l=16, g=32).unsqueeze(3).to_broadcast([1, 32, 16, 8]),
-        )
         selw = consts.tile([P, 8, 16], BF16, tag="selw")
         nc.vector.tensor_tensor(
             out=selw[:],
@@ -450,133 +443,167 @@ def tile_mlpp_pa_kernel(tc, x, W_h, b_h, W_w, b_w, W_c, b_c, W_attn, b_attn, W_1
                 op=ADD,
             )
             st["sel", hh] = sel
-        pta = bank(ptag(), BF16, P)
-        nc.tensor.transpose(pta[:], tba[:], ident_b[:])
-        ap1 = consts.tile([P, 2], F32, tag="ap1")
-        nc.vector.tensor_scalar_add(out=ap1[:], in0=pta[:, 0:2], scalar1=1.0)
+        warm = consts.tile([P, 8], BF16, tag="warm")
+        nc.scalar.copy(out=warm[:], in_=ident_b[:, 0:8])
+        load_xn(0, 0)
+        load_w(2, W_c)
+        load_w(3, W_1)
 
-        in_relayout(0, 0, 0)
-        in_relayout(0, 0, 1)
-        weight_prep(1, sc_copy)
-        weight_prep(0, ve_copy)
-        weight_quant(0)
-        weight_quant(1)
+        in_relayout(0, 0, 0, ve_copy)
+        in_relayout(0, 0, 1, ve_copy)
         for lp in range(8):
             in_transpose(0, 0, lp, ptag())
-            in_evac(0, 0, lp, both)
+            in_evac(0, 0, lp, sc_copy)
+        in_relayout(1, 0, 0, ve_copy)
+        in_relayout(1, 0, 1, ve_copy)
+        weight_prep(0, ve_copy)
+        weight_quant(0)
+        weight_prep(1, ve_copy)
+        weight_quant(1)
         in_quant(0, 0, 0)
         in_quant(0, 0, 1)
-        in_relayout(1, 0, 0)
-        in_relayout(1, 0, 1)
         load_xn(1, 0)
         load_xs(0, 1, 0)
         load_xs(0, 1, 1)
         load_xn(0, 1)
         load_xn(1, 1)
-        for k in range(8):
-            b_xh(0, k, ptag())
-            b_xh_evac(0, k, both[(k // 2) % 2])
+        b1bc = consts.tile([P, C], BF16, tag="b1bc")
+        nc.sync.dma_start(out=b1bc[:], in_=b_1.partition_broadcast(P))
+        xh0 = (0, 1, 4, 5, 2, 3, 6, 7)
         for lp in range(8):
             in_transpose(1, 0, lp, ptag())
-            in_evac(1, 0, lp, both)
+            in_evac(1, 0, lp, sc_copy)
+            if lp >= 4:
+                b_xh(0, xh0[lp - 4], ptag())
+                b_xh_evac(0, xh0[lp - 4], ve_copy)
         in_quant(1, 0, 0)
+        for k in xh0[4:]:
+            b_xh(0, k, ptag())
+            b_xh_evac(0, k, sc_copy)
         for q4 in range(4):
             xc_transpose(0, q4, ptag())
-        xc_evac(0, 0, sc_copy)
-        xc_evac(0, 1, sc_copy)
-        xc_quant(0, 0)
-        xc_evac(0, 2, sc_copy)
-        xc_evac(0, 3, sc_copy)
+            xc_evac(0, q4, sc_copy)
         weight_prep(2, sc_copy)
+        weight_quant(2)
         weight_prep(3, sc_copy)
+        nc.vector.tensor_copy(
+            out=rtab[0:32, :].rearrange("p (g l) -> p g l", g=32, l=16),
+            in_=tb[0:32, 0:32].unsqueeze(2).to_broadcast([32, 32, 16]),
+        )
+        nc.vector.tensor_copy(
+            out=rtab[32:33, :].rearrange("p (g l) -> p g l", g=32, l=16),
+            in_=tb[32:33, :].rearrange("p (l g) -> p g l", l=16, g=32),
+        )
         for h8 in range(8):
             b_xw(0, h8, ptag())
             b_add(0, h8)
-        weight_quant(2)
-        weight_quant(3)
+            b_xh(1, h8, ptag())
+            b_xh_evac(1, h8, sc_copy)
+            if h8 == 3:
+                weight_quant(3)
+        pta = bank(ptag(), BF16, P)
+        nc.tensor.transpose(pta[:], tba[:], ident_b[:])
+        ap1 = consts.tile([P, 2], F32, tag="ap1")
+        nc.vector.tensor_scalar_add(out=ap1[:], in0=pta[:, 0:2], scalar1=1.0)
+        xc_quant(0, 0)
         xc_quant(0, 1)
-        in_quant(1, 0, 1)
-        for k in range(8):
-            b_xh(1, k, ptag())
-            b_xh_evac(1, k, sc_copy)
         for gb in range(8):
             b_t(0, gb, ptag())
-            b_t_evac(0, gb, sc_copy)
-        for h8 in range(8):
-            b_xw(1, h8, ptag())
-            b_add(1, h8)
+            b_t_evac(0, gb, ve_copy if gb % 2 else sc_copy)
+            if gb == 3:
+                in_quant(1, 0, 1)
 
         def tr_jobs(s):
-            jobs = [("T", lambda gb=gb: b_t(s, gb, "ss"), lambda gb=gb: b_t_evac(s, gb, sc_copy), []) for gb in range(8)]
-            return jobs
+            return [("T", lambda gb=gb: b_t(s, gb, "ss"), lambda gb=gb: b_t_evac(s, gb, sc_copy), [], s) for gb in range(8)]
 
         def in_jobs(which):
             jobs = [
-                ("T", lambda lp=lp: in_transpose(which, 1, lp, "ss"), lambda lp=lp: in_evac(which, 1, lp, only_s), [])
+                ("T", lambda lp=lp: in_transpose(which, 1, lp, "ss"), lambda lp=lp: in_evac(which, 1, lp, sc_copy), [], -1)
                 for lp in range(8)
             ]
             jobs[7][3].extend([lambda: in_quant(which, 1, 0), lambda: in_quant(which, 1, 1)])
             return jobs
 
         def ic_jobs(s):
-            jobs = [("T", lambda q=q: xc_transpose(s, q, "ss"), lambda q=q: xc_evac(s, q, sc_copy), []) for q in range(4)]
+            jobs = [("T", lambda q=q: xc_transpose(s, q, "ss"), lambda q=q: xc_evac(s, q, sc_copy), [], -1) for q in range(4)]
             jobs[1][3].append(lambda: xc_quant(s, 0))
             jobs[3][3].append(lambda: xc_quant(s, 1))
             return jobs
 
         def xh_jobs(s):
-            return [("M", lambda k=k: b_xh(s, k, "ss"), lambda k=k: b_xh_evac(s, k, sc_copy), []) for k in range(8)]
+            return [("M", lambda k=k: b_xh(s, k, "ss"), lambda k=k: b_xh_evac(s, k, sc_copy), [], s) for k in range(8)]
 
         def xw_jobs(s):
-            return [("W", lambda h8=h8: b_xw(s, h8, "ss"), lambda h8=h8: b_add(s, h8), []) for h8 in range(8)]
+            return [("W", lambda h8=h8: b_xw(s, h8, "ss"), lambda h8=h8: b_add(s, h8), [], s) for h8 in range(8)]
 
         def mix(a, b):
-            return [job for pair in zip(a, b) for job in pair]
+            keyed = [((i + 0.5) / len(l), l[i]) for l in (a, b) for i in range(len(l))]
+            return [job for key, job in sorted(keyed, key=lambda kj: kj[0])]
 
-        first = ic_jobs(1)
-        first[0][3].extend([lambda: in_relayout(0, 1, 0), lambda: in_relayout(0, 1, 1)])
-        first[0][3].extend([lambda: load_xs(1, 1, 0), lambda: load_xs(1, 1, 1)])
-        second = in_jobs(0)
-        second[7][3].extend([lambda: in_relayout(1, 1, 0), lambda: in_relayout(1, 1, 1)])
-        side = first + mix(tr_jobs(1), second) + (
-            xh_jobs(2)[:4]
-            + mix(in_jobs(1)[:4], xh_jobs(2)[4:])
-            + in_jobs(1)[4:]
-            + xw_jobs(2)
-            + ic_jobs(2)
+        def gp_copy(out, in_):
+            nc.gpsimd.tensor_scalar(out=out, in0=in_, scalar1=1.0, scalar2=0.0, op0=MULT, op1=ADD)
+
+        def relayout_pieces(which, eng_copy):
+            return [lambda q=q, j=j: in_relayout(which, 1, q, eng_copy, j, 4) for q in range(2) for j in range(4)]
+
+        c1 = ic_jobs(1)
+        i0 = in_jobs(0)
+        i1 = in_jobs(1)
+        rel0 = relayout_pieces(0, gp_copy)
+        for f in rel0:
+            f()
+        load_xs(1, 1, 0)
+        load_xs(1, 1, 1)
+        rel1 = relayout_pieces(1, ve_copy)
+        i0[7][3].extend(rel1)
+        side = (
+            mix(xw_jobs(1), i0)
+            + mix(tr_jobs(1), c1 + i1[:4])
+            + mix(i1[4:], xh_jobs(2))
+            + mix(xw_jobs(2), ic_jobs(2))
             + tr_jobs(2)
-            + xh_jobs(3)
+            + mix(xh_jobs(3), ic_jobs(3))
             + xw_jobs(3)
-            + ic_jobs(3)
             + tr_jobs(3)
         )
 
         NT = 32
         taken = 0
         adds = []
+        pend = []
+
+        def flush(n):
+            while len(pend) > n:
+                pend.pop(0)()
+
+        def fill(job):
+            flush(3)
+            job[1]()
+            pend.append(job[2])
+
         att(0, 0)
         att(0, 1)
         pe1(0)
         for c in range(NT + 7):
             pair = (c - 2) // 2
             hid_due = c % 2 == 0 and 0 <= pair < NT // 2
-            room = 4 - (1 if hid_due else 0)
-            jobs = side[taken : taken + room]
-            taken += len(jobs)
-            for f in adds:
-                f()
-            adds = []
-            runs = ([lambda: pe2(pair)] if hid_due else []) + [j[1] for j in jobs if j[0] == "T"]
+            room = (5 if c < 16 else 4) - (1 if hid_due else 0)
+            jobs = []
+            while taken < len(side) and len(jobs) < room:
+                job = side[taken]
+                if any(j[0] == "W" and j[4] == job[4] for j in jobs) and job[0] == "T":
+                    break
+                jobs.append(job)
+                taken += 1
+            flush(0)
+            runs = [("T", lambda: pe2(pair), lambda: s2c(pair), [], -1)] if hid_due else []
+            runs = runs + [j for j in jobs if j[0] == "T"]
             for i in range(max(len(runs), 2)):
                 if i < len(runs):
-                    runs[i]()
+                    fill(runs[i])
                 if i < 2 and c + 1 < NT:
                     att(c + 1, i)
-            if hid_due:
-                s2c(pair)
-            for j in jobs:
-                if j[0] == "T":
-                    j[2]()
+            flush(0)
             if c < NT:
                 v1(c)
             if c + 1 < NT:
@@ -588,14 +615,16 @@ def tile_mlpp_pa_kernel(tc, x, W_h, b_h, W_w, b_w, W_c, b_c, W_attn, b_attn, W_1
             if c % 4 == 0 and 0 <= (c - 4) // 4 < NT // 4:
                 qh((c - 4) // 4)
             for j in jobs:
+                if j[0] == "T":
+                    for f in j[3]:
+                        f()
+            for j in jobs:
                 if j[0] == "M":
-                    j[1]()
-                    j[2]()
+                    fill(j)
+            flush(0)
+            for j in jobs:
                 if j[0] == "W":
-                    j[1]()
-                    adds.append(j[2])
-                for f in j[3]:
-                    f()
+                    fill(j)
             if 0 <= c - 5 < NT:
                 pe3(c - 5, "ss" if taken == len(side) else "pf")
             if 0 <= c - 4 < NT:

@@ -457,11 +457,11 @@ def tile_mlpp_pa_kernel(tc, x, W_h, b_h, W_w, b_w, W_c, b_c, W_attn, b_attn, W_1
         in_relayout(1, 0, 0, ve_copy)
         in_relayout(1, 0, 1, ve_copy)
         weight_prep(0, ve_copy)
+        in_quant(0, 0, 0)
         weight_quant(0)
+        in_quant(0, 0, 1)
         weight_prep(1, ve_copy)
         weight_quant(1)
-        in_quant(0, 0, 0)
-        in_quant(0, 0, 1)
         load_xn(1, 0)
         load_xs(0, 1, 0)
         load_xs(0, 1, 1)
@@ -480,12 +480,6 @@ def tile_mlpp_pa_kernel(tc, x, W_h, b_h, W_w, b_w, W_c, b_c, W_attn, b_attn, W_1
         for k in xh0[4:]:
             b_xh(0, k, ptag())
             b_xh_evac(0, k, sc_copy)
-        for q4 in range(4):
-            xc_transpose(0, q4, ptag())
-            xc_evac(0, q4, sc_copy)
-        weight_prep(2, sc_copy)
-        weight_quant(2)
-        weight_prep(3, sc_copy)
         nc.vector.tensor_copy(
             out=rtab[0:32, :].rearrange("p (g l) -> p g l", g=32, l=16),
             in_=tb[0:32, 0:32].unsqueeze(2).to_broadcast([32, 32, 16]),
@@ -497,28 +491,37 @@ def tile_mlpp_pa_kernel(tc, x, W_h, b_h, W_w, b_w, W_c, b_c, W_attn, b_attn, W_1
         for h8 in range(8):
             b_xw(0, h8, ptag())
             b_add(0, h8)
-            b_xh(1, h8, ptag())
-            b_xh_evac(1, h8, sc_copy)
-            if h8 == 3:
-                weight_quant(3)
+            if h8 % 2 == 1:
+                xc_transpose(0, h8 // 2, ptag())
+                xc_evac(0, h8 // 2, sc_copy)
+        weight_prep(2, sc_copy)
+        weight_quant(2)
+        xc_quant(0, 0)
+        weight_prep(3, sc_copy)
+        weight_quant(3)
+        xc_quant(0, 1)
         pta = bank(ptag(), BF16, P)
         nc.tensor.transpose(pta[:], tba[:], ident_b[:])
         ap1 = consts.tile([P, 2], F32, tag="ap1")
         nc.vector.tensor_scalar_add(out=ap1[:], in0=pta[:, 0:2], scalar1=1.0)
-        xc_quant(0, 0)
-        xc_quant(0, 1)
         for gb in range(8):
             b_t(0, gb, ptag())
             b_t_evac(0, gb, ve_copy if gb % 2 else sc_copy)
-            if gb == 3:
-                in_quant(1, 0, 1)
+            b_xh(1, gb, ptag())
+            b_xh_evac(1, gb, sc_copy if gb % 2 else ve_copy)
+        in_quant(1, 0, 1)
 
         def tr_jobs(s):
             return [("T", lambda gb=gb: b_t(s, gb, "ss"), lambda gb=gb: b_t_evac(s, gb, sc_copy), [], s) for gb in range(8)]
 
+        def in_fill(which, lp):
+            in_transpose(which, 1, lp, "ss")
+            if which == 1 and lp in (0, 2, 4):
+                relayout(1, lp // 2 + 1, (ve_copy, sc_copy))
+
         def in_jobs(which):
             jobs = [
-                ("T", lambda lp=lp: in_transpose(which, 1, lp, "ss"), lambda lp=lp: in_evac(which, 1, lp, sc_copy), [], -1)
+                ("T", lambda lp=lp: in_fill(which, lp), lambda lp=lp: in_evac(which, 1, lp, sc_copy), [], -1)
                 for lp in range(8)
             ]
             jobs[7][3].extend([lambda: in_quant(which, 1, 0), lambda: in_quant(which, 1, 1)])
@@ -543,28 +546,25 @@ def tile_mlpp_pa_kernel(tc, x, W_h, b_h, W_w, b_w, W_c, b_c, W_attn, b_attn, W_1
         def gp_copy(out, in_):
             nc.gpsimd.tensor_scalar(out=out, in0=in_, scalar1=1.0, scalar2=0.0, op0=MULT, op1=ADD)
 
-        def relayout_pieces(which, eng_copy):
-            return [lambda q=q, j=j: in_relayout(which, 1, q, eng_copy, j, 4) for q in range(2) for j in range(4)]
+        def relayout(which, j, copies):
+            for q in range(2):
+                in_relayout(which, 1, q, copies[q], j, 4)
 
         c1 = ic_jobs(1)
         i0 = in_jobs(0)
         i1 = in_jobs(1)
-        rel0 = relayout_pieces(0, gp_copy)
-        for f in rel0:
-            f()
+        for j in range(4):
+            relayout(0, j, (gp_copy, gp_copy))
         load_xs(1, 1, 0)
         load_xs(1, 1, 1)
-        rel1 = relayout_pieces(1, ve_copy)
-        i0[7][3].extend(rel1)
+        i0[7][3].append(lambda: relayout(1, 0, (ve_copy, sc_copy)))
         side = (
             mix(xw_jobs(1), i0)
-            + mix(tr_jobs(1), c1 + i1[:4])
-            + mix(i1[4:], xh_jobs(2))
-            + mix(xw_jobs(2), ic_jobs(2))
-            + tr_jobs(2)
-            + mix(xh_jobs(3), ic_jobs(3))
-            + xw_jobs(3)
-            + tr_jobs(3)
+            + mix(tr_jobs(1), c1 + i1)
+            + xh_jobs(2)
+            + mix(xw_jobs(2), ic_jobs(2) + xh_jobs(3))
+            + mix(tr_jobs(2), xw_jobs(3))
+            + mix(tr_jobs(3), ic_jobs(3))
         )
 
         NT = 32
@@ -587,7 +587,7 @@ def tile_mlpp_pa_kernel(tc, x, W_h, b_h, W_w, b_w, W_c, b_c, W_attn, b_attn, W_1
         for c in range(NT + 7):
             pair = (c - 2) // 2
             hid_due = c % 2 == 0 and 0 <= pair < NT // 2
-            room = (5 if c < 16 else 4) - (1 if hid_due else 0)
+            room = 5
             jobs = []
             while taken < len(side) and len(jobs) < room:
                 job = side[taken]

@@ -390,7 +390,13 @@ def tile_mlpp_pa_kernel(tc, x, W_h, b_h, W_w, b_w, W_c, b_c, W_attn, b_attn, W_1
             s, dlo, hh, d8 = where(n)
             e0 = (8 * dlo + d8) * C
             xpb = five.tile([P, C], F32, tag="xpb")
-            nc.gpsimd.tensor_tensor(out=xpb[:], in0=xn[hh][:, e0 : e0 + C], in1=b1bc[:], op=ADD)
+            for c0 in (0, 256):
+                nc.gpsimd.tensor_tensor(
+                    out=xpb[:, c0 : c0 + 256],
+                    in0=xn[hh][:, e0 + c0 : e0 + c0 + 256],
+                    in1=b1bc[:, c0 : c0 + 256],
+                    op=ADD,
+                )
             st["xpb", n] = xpb
 
         def pe3(n, tag="pf"):

@@ -25,7 +25,8 @@ def tile_mlpp_pa_kernel(tc, x, W_h, b_h, W_w, b_w, W_c, b_c, W_attn, b_attn, W_1
         one = ctx.enter_context(tc.tile_pool(name="one", bufs=1))
         two = ctx.enter_context(tc.tile_pool(name="two", bufs=2))
         three = ctx.enter_context(tc.tile_pool(name="three", bufs=3))
-        five = ctx.enter_context(tc.tile_pool(name="five", bufs=5))
+        outp = ctx.enter_context(tc.tile_pool(name="outp", bufs=6))
+        five = ctx.enter_context(tc.tile_pool(name="five", bufs=4))
         ps1 = ctx.enter_context(tc.psum_pool(name="ps1", bufs=1))
         ps5 = ctx.enter_context(tc.psum_pool(name="ps5", bufs=4))
         ps2 = ctx.enter_context(tc.psum_pool(name="ps2", bufs=2))
@@ -88,7 +89,10 @@ def tile_mlpp_pa_kernel(tc, x, W_h, b_h, W_w, b_w, W_c, b_c, W_attn, b_attn, W_1
         load_w(1, W_w)
 
         def weight_prep(i, eng_copy):
-            wg = one.tile([P, 2048], BF16, tag="ghid", align_bytes=64)
+            if i % 2 == 0:
+                wg = one.tile([P, 2048], BF16, tag="ghid", align_bytes=64)
+            else:
+                wg = two.tile([P, 2048], BF16, tag="cc", align_bytes=64)
             st["wg", i] = wg
             eng_copy(
                 out=wg[:].rearrange("p (n i t) -> p n t i", n=P, i=4, t=4),
@@ -135,15 +139,17 @@ def tile_mlpp_pa_kernel(tc, x, W_h, b_h, W_w, b_w, W_c, b_c, W_attn, b_attn, W_1
                 in_=xs.rearrange("p y (l g) -> p l y g", l=16, g=32)[:, ls, :, :],
             )
 
-        def in_transpose(which, dlo, lp, tag):
+        def in_transpose(which, dlo, lp, tag, halves=(0, 1)):
             rlw = st["rl", which, dlo][:].bitcast(F32)
-            pt = bank(tag)
+            if 0 in halves:
+                pt = bank(tag)
+                st["pt", which, dlo, lp] = pt
+            pt = st["pt", which, dlo, lp]
             for li in range(2):
-                for u in range(2):
+                for u in halves:
                     w0 = (2 * lp + li) * 256 + u * P
                     s0 = (2 * li + u) * P
                     nc.tensor.transpose(pt[:, s0 : s0 + P], rlw[:, w0 : w0 + P], ident_f[:])
-            st["pt", which, dlo, lp] = pt
 
         def in_evac(which, dlo, lp, copy):
             if lp == 0:
@@ -418,7 +424,7 @@ def tile_mlpp_pa_kernel(tc, x, W_h, b_h, W_w, b_w, W_c, b_c, W_attn, b_attn, W_1
         def v3(n):
             s, dlo, hh, d8 = where(n)
             d = 2 * d8 + dlo
-            o = three.tile([P, C], F32, tag="o")
+            o = outp.tile([P, C], F32, tag="o")
             nc.vector.tensor_tensor(out=o[:], in0=st["pf", n][:], in1=st["xpb", n][:], op=ADD)
             nc.sync.dma_start(out=outv[hh][:, d, :], in_=o[:])
 
@@ -430,6 +436,10 @@ def tile_mlpp_pa_kernel(tc, x, W_h, b_h, W_w, b_w, W_c, b_c, W_attn, b_attn, W_1
         def ptag():
             rot["n"] += 1
             return ring[(rot["n"] - 1) % len(ring)]
+
+        def relayout(which, j, copies, pieces):
+            for q in range(2):
+                in_relayout(which, 1, q, copies[q], j, pieces)
 
         rtab = consts.tile([P, C], BF16, tag="rtab")
         nc.vector.memset(rtab[:], 0.0)
@@ -456,32 +466,36 @@ def tile_mlpp_pa_kernel(tc, x, W_h, b_h, W_w, b_w, W_c, b_c, W_attn, b_attn, W_1
         load_w(3, W_1)
 
         in_relayout(0, 0, 0, ve_copy)
+        for lp in range(8):
+            in_transpose(0, 0, lp, ptag(), (0,))
         in_relayout(0, 0, 1, ve_copy)
         for lp in range(8):
-            in_transpose(0, 0, lp, ptag())
-            in_evac(0, 0, lp, sc_copy)
+            in_transpose(0, 0, lp, None, (1,))
+            in_evac(0, 0, lp, ve_copy if lp in () else sc_copy)
         in_relayout(1, 0, 0, ve_copy)
+        for lp in range(8):
+            in_transpose(1, 0, lp, ptag(), (0,))
         in_relayout(1, 0, 1, ve_copy)
         weight_prep(0, ve_copy)
         in_quant(0, 0, 0)
         weight_quant(0)
         in_quant(0, 0, 1)
+        for lp in range(8):
+            in_transpose(1, 0, lp, None, (1,))
+            in_evac(1, 0, lp, ve_copy if lp in (2, 5,) else sc_copy)
         weight_prep(1, ve_copy)
         weight_quant(1)
-        load_xn(1, 0)
         load_xs(0, 1, 0)
         load_xs(0, 1, 1)
+        load_xn(1, 0)
         load_xn(0, 1)
         load_xn(1, 1)
         b1bc = consts.tile([P, C], BF16, tag="b1bc")
         nc.sync.dma_start(out=b1bc[:], in_=b_1.partition_broadcast(P))
         xh0 = (0, 1, 4, 5, 2, 3, 6, 7)
-        for lp in range(8):
-            in_transpose(1, 0, lp, ptag())
-            in_evac(1, 0, lp, sc_copy)
-            if lp >= 4:
-                b_xh(0, xh0[lp - 4], ptag())
-                b_xh_evac(0, xh0[lp - 4], ve_copy)
+        for k in xh0[:4]:
+            b_xh(0, k, ptag())
+            b_xh_evac(0, k, sc_copy)
         in_quant(1, 0, 0)
         for k in xh0[4:]:
             b_xh(0, k, ptag())
@@ -497,25 +511,35 @@ def tile_mlpp_pa_kernel(tc, x, W_h, b_h, W_w, b_w, W_c, b_c, W_attn, b_attn, W_1
         for h8 in range(8):
             b_xw(0, h8, ptag())
             b_add(0, h8)
-            if h8 % 2 == 1:
-                xc_transpose(0, h8 // 2, ptag())
-                xc_evac(0, h8 // 2, sc_copy)
-        weight_prep(2, sc_copy)
+            if h8 == 0:
+                weight_prep(2, sc_copy)
+                weight_prep(3, sc_copy)
+            if h8 in (3, 7):
+                for q4 in (h8 // 2 - 1, h8 // 2):
+                    xc_transpose(0, q4, ptag())
+                    xc_evac(0, q4, sc_copy)
         weight_quant(2)
-        xc_quant(0, 0)
-        weight_prep(3, sc_copy)
-        weight_quant(3)
-        xc_quant(0, 1)
         pta = bank(ptag(), BF16, P)
         nc.tensor.transpose(pta[:], tba[:], ident_b[:])
         ap1 = consts.tile([P, 2], F32, tag="ap1")
         nc.vector.tensor_scalar_add(out=ap1[:], in0=pta[:, 0:2], scalar1=1.0)
-        for gb in range(8):
-            b_t(0, gb, ptag())
-            b_t_evac(0, gb, ve_copy if gb % 2 else sc_copy)
-            b_xh(1, gb, ptag())
-            b_xh_evac(1, gb, sc_copy if gb % 2 else ve_copy)
-        in_quant(1, 0, 1)
+        for g0 in range(0, 8, 2):
+            for gb in range(g0, g0 + 2):
+                b_t(0, gb, ptag())
+                b_t_evac(0, gb, sc_copy)
+            for gb in range(g0, g0 + 2):
+                b_xh(1, gb, ptag())
+                b_xh_evac(1, gb, ve_copy)
+                if gb == 0:
+                    xc_quant(0, 0)
+                if gb == 1:
+                    in_quant(1, 0, 1)
+                if gb == 3:
+                    xc_quant(0, 1)
+                if gb == 5:
+                    weight_quant(3)
+                if gb % 2 == 0:
+                    relayout(0, gb // 2, (sc_copy, sc_copy), 4)
 
         def tr_jobs(s):
             return [("T", lambda gb=gb: b_t(s, gb, "ss"), lambda gb=gb: b_t_evac(s, gb, sc_copy), [], s) for gb in range(8)]
@@ -523,7 +547,7 @@ def tile_mlpp_pa_kernel(tc, x, W_h, b_h, W_w, b_w, W_c, b_c, W_attn, b_attn, W_1
         def in_fill(which, lp):
             in_transpose(which, 1, lp, "ss")
             if which == 1 and lp in (0, 2, 4):
-                relayout(1, lp // 2 + 1, (ve_copy, sc_copy))
+                relayout(1, lp // 2 + 1, (ve_copy, sc_copy), 4)
 
         def in_jobs(which):
             jobs = [
@@ -549,21 +573,12 @@ def tile_mlpp_pa_kernel(tc, x, W_h, b_h, W_w, b_w, W_c, b_c, W_attn, b_attn, W_1
             keyed = [((i + 0.5) / len(l), l[i]) for l in (a, b) for i in range(len(l))]
             return [job for key, job in sorted(keyed, key=lambda kj: kj[0])]
 
-        def gp_copy(out, in_):
-            nc.gpsimd.tensor_scalar(out=out, in0=in_, scalar1=1.0, scalar2=0.0, op0=MULT, op1=ADD)
-
-        def relayout(which, j, copies):
-            for q in range(2):
-                in_relayout(which, 1, q, copies[q], j, 4)
-
         c1 = ic_jobs(1)
         i0 = in_jobs(0)
         i1 = in_jobs(1)
-        for j in range(4):
-            relayout(0, j, (gp_copy, gp_copy))
         load_xs(1, 1, 0)
         load_xs(1, 1, 1)
-        i0[7][3].append(lambda: relayout(1, 0, (ve_copy, sc_copy)))
+        i0[7][3].append(lambda: relayout(1, 0, (ve_copy, sc_copy), 4))
         side = (
             mix(xw_jobs(1), i0)
             + mix(tr_jobs(1), c1 + i1)
@@ -602,6 +617,8 @@ def tile_mlpp_pa_kernel(tc, x, W_h, b_h, W_w, b_w, W_c, b_c, W_attn, b_attn, W_1
                 jobs.append(job)
                 taken += 1
             flush(0)
+            if c < NT:
+                v1(c)
             runs = [("T", lambda: pe2(pair), lambda: s2c(pair), [], -1)] if hid_due else []
             runs = runs + [j for j in jobs if j[0] == "T"]
             for i in range(max(len(runs), 2)):
@@ -610,10 +627,6 @@ def tile_mlpp_pa_kernel(tc, x, W_h, b_h, W_w, b_w, W_c, b_c, W_attn, b_attn, W_1
                 if i < 2 and c + 1 < NT:
                     att(c + 1, i)
             flush(0)
-            if c < NT:
-                v1(c)
-            if c + 1 < NT:
-                pe1(c + 1)
             if 0 <= c - 6 < NT:
                 v3(c - 6)
             if c < NT:
@@ -627,6 +640,8 @@ def tile_mlpp_pa_kernel(tc, x, W_h, b_h, W_w, b_w, W_c, b_c, W_attn, b_attn, W_1
             for j in jobs:
                 if j[0] == "M":
                     fill(j)
+            if c + 1 < NT:
+                pe1(c + 1)
             flush(0)
             for j in jobs:
                 if j[0] == "W":

@@ -131,11 +131,11 @@ def tile_mlpp_pa_kernel(tc, x, W_h, b_h, W_w, b_w, W_c, b_c, W_attn, b_attn, W_1
                     rl = one.tile([P, 8192], BF16, tag="rl")
                 st["rl", which, dlo] = rl
             rl = st["rl", which, dlo]
-            rl4 = rl[:].rearrange("p (l y g) -> p l y g", l=16, y=16, g=32)
+            rl4 = rl[:, q * 4096 : (q + 1) * 4096].rearrange("p (l y g) -> p l y g", l=16, y=8, g=32)
             xs = st["xs", which, dlo, q]
             ls = slice(16 // pieces * piece, 16 // pieces * (piece + 1))
             eng_copy(
-                out=rl4[:, ls, 8 * q : 8 * q + 8, :],
+                out=rl4[:, ls, :, :],
                 in_=xs.rearrange("p y (l g) -> p l y g", l=16, g=32)[:, ls, :, :],
             )
 
@@ -147,7 +147,7 @@ def tile_mlpp_pa_kernel(tc, x, W_h, b_h, W_w, b_w, W_c, b_c, W_attn, b_attn, W_1
             pt = st["pt", which, dlo, lp]
             for li in range(2):
                 for u in halves:
-                    w0 = (2 * lp + li) * 256 + u * P
+                    w0 = u * 2048 + (2 * lp + li) * P
                     s0 = (2 * li + u) * P
                     nc.tensor.transpose(pt[:, s0 : s0 + P], rlw[:, w0 : w0 + P], ident_f[:])
 
@@ -353,7 +353,7 @@ def tile_mlpp_pa_kernel(tc, x, W_h, b_h, W_w, b_w, W_c, b_c, W_attn, b_attn, W_1
                 hidn = two.tile([P, 2 * C], BF16, tag="hidn")
                 st["hidn", n // 2] = hidn
             hidn = st["hidn", n // 2]
-            bsum = one.tile([P, C], F32, tag="bsum")
+            bsum = two.tile([P, C], F32, tag="bsum")
             nc.vector.tensor_tensor(out=bsum[:], in0=st["pc", n][:], in1=st["a", s][:, d8 * C : (d8 + 1) * C], op=ADD)
             st["bsum", n] = bsum
 
@@ -471,7 +471,7 @@ def tile_mlpp_pa_kernel(tc, x, W_h, b_h, W_w, b_w, W_c, b_c, W_attn, b_attn, W_1
         in_relayout(0, 0, 1, ve_copy)
         for lp in range(8):
             in_transpose(0, 0, lp, None, (1,))
-            in_evac(0, 0, lp, ve_copy if lp in () else sc_copy)
+            in_evac(0, 0, lp, sc_copy)
         in_relayout(1, 0, 0, ve_copy)
         for lp in range(8):
             in_transpose(1, 0, lp, ptag(), (0,))
@@ -482,7 +482,7 @@ def tile_mlpp_pa_kernel(tc, x, W_h, b_h, W_w, b_w, W_c, b_c, W_attn, b_attn, W_1
         in_quant(0, 0, 1)
         for lp in range(8):
             in_transpose(1, 0, lp, None, (1,))
-            in_evac(1, 0, lp, ve_copy if lp in (2, 5,) else sc_copy)
+            in_evac(1, 0, lp, sc_copy)
         weight_prep(1, ve_copy)
         weight_quant(1)
         load_xs(0, 1, 0)
@@ -493,13 +493,11 @@ def tile_mlpp_pa_kernel(tc, x, W_h, b_h, W_w, b_w, W_c, b_c, W_attn, b_attn, W_1
         b1bc = consts.tile([P, C], BF16, tag="b1bc")
         nc.sync.dma_start(out=b1bc[:], in_=b_1.partition_broadcast(P))
         xh0 = (0, 1, 4, 5, 2, 3, 6, 7)
-        for k in xh0[:4]:
-            b_xh(0, k, ptag())
-            b_xh_evac(0, k, sc_copy)
-        in_quant(1, 0, 0)
-        for k in xh0[4:]:
-            b_xh(0, k, ptag())
-            b_xh_evac(0, k, sc_copy)
+        for i in range(8):
+            b_xh(0, xh0[i], ptag())
+            b_xh_evac(0, xh0[i], ve_copy if i < 2 else sc_copy)
+            if i == 1:
+                in_quant(1, 0, 0)
         nc.vector.tensor_copy(
             out=rtab[0:32, :].rearrange("p (g l) -> p g l", g=32, l=16),
             in_=tb[0:32, 0:32].unsqueeze(2).to_broadcast([32, 32, 16]),

@@ -288,7 +288,7 @@ def tile_mlpp_pa_kernel(tc, x, W_h, b_h, W_w, b_w, W_c, b_c, W_attn, b_attn, W_1
             nc.tensor.matmul(
                 out=pst[:],
                 lhsT=st["sel", s % 2][:].rearrange("p a w -> p (a w)"),
-                rhs=rtab[:, gb * 64 : (gb + 1) * 64].unsqueeze(2).to_broadcast([P, 64, 8]),
+                rhs=rtab[:, gb * 64 : (gb + 1) * 64, :].unsqueeze(2).to_broadcast([P, 64, 4, 2]),
                 start=True,
                 stop=False,
             )
@@ -441,8 +441,9 @@ def tile_mlpp_pa_kernel(tc, x, W_h, b_h, W_w, b_w, W_c, b_c, W_attn, b_attn, W_1
             for q in range(2):
                 in_relayout(which, 1, q, copies[q], j, pieces)
 
-        rtab = consts.tile([P, C], BF16, tag="rtab")
+        rtab = consts.tile([P, C, 2], BF16, tag="rtab")
         nc.vector.memset(rtab[:], 0.0)
+        rtab4 = rtab[:].rearrange("p (g l) b -> p g l b", g=32, l=16)
         selw = consts.tile([P, 8, 16], BF16, tag="selw")
         nc.vector.tensor_tensor(
             out=selw[:],
@@ -499,12 +500,12 @@ def tile_mlpp_pa_kernel(tc, x, W_h, b_h, W_w, b_w, W_c, b_c, W_attn, b_attn, W_1
             if i == 1:
                 in_quant(1, 0, 0)
         nc.vector.tensor_copy(
-            out=rtab[0:32, :].rearrange("p (g l) -> p g l", g=32, l=16),
-            in_=tb[0:32, 0:32].unsqueeze(2).to_broadcast([32, 32, 16]),
+            out=rtab4[0:32, :, :, :],
+            in_=tb[0:32, 0:32].unsqueeze(2).unsqueeze(3).to_broadcast([32, 32, 16, 2]),
         )
         nc.vector.tensor_copy(
-            out=rtab[32:33, :].rearrange("p (g l) -> p g l", g=32, l=16),
-            in_=tb[32:33, :].rearrange("p (l g) -> p g l", l=16, g=32),
+            out=rtab4[32:33, :, :, :],
+            in_=tb[32:33, :].rearrange("p (l g) -> p g l", l=16, g=32).unsqueeze(3).to_broadcast([1, 32, 16, 2]),
         )
         for h8 in range(8):
             b_xw(0, h8, ptag())
@@ -615,6 +616,8 @@ def tile_mlpp_pa_kernel(tc, x, W_h, b_h, W_w, b_w, W_c, b_c, W_attn, b_attn, W_1
                 jobs.append(job)
                 taken += 1
             flush(0)
+            if c % 4 == 1 and 0 <= (c - 5) // 4 < NT // 4:
+                qh((c - 5) // 4)
             if c < NT:
                 v1(c)
             runs = [("T", lambda: pe2(pair), lambda: s2c(pair), [], -1)] if hid_due else []
@@ -629,8 +632,6 @@ def tile_mlpp_pa_kernel(tc, x, W_h, b_h, W_w, b_w, W_c, b_c, W_attn, b_attn, W_1
                 v3(c - 6)
             if c < NT:
                 v2(c)
-            if c % 4 == 0 and 0 <= (c - 4) // 4 < NT // 4:
-                qh((c - 4) // 4)
             for j in jobs:
                 if j[0] == "T":
                     for f in j[3]:
@@ -638,12 +639,12 @@ def tile_mlpp_pa_kernel(tc, x, W_h, b_h, W_w, b_w, W_c, b_c, W_attn, b_attn, W_1
             for j in jobs:
                 if j[0] == "M":
                     fill(j)
-            if c + 1 < NT:
-                pe1(c + 1)
             flush(0)
             for j in jobs:
                 if j[0] == "W":
                     fill(j)
+            if c + 1 < NT:
+                pe1(c + 1)
             if 0 <= c - 5 < NT:
                 pe3(c - 5, "ss" if taken == len(side) else "pf")
             if 0 <= c - 4 < NT:

@@ -64,7 +64,8 @@ def tile_mlpp_pa_kernel(tc, x, W_h, b_h, W_w, b_w, W_c, b_c, W_attn, b_attn, W_1
         def load_xs(which, dlo, q):
             xs = xsp.tile([P, 8, C], BF16, tag="xs")
             if which == 0:
-                nc.sync.dma_start(out=xs[:], in_=x1v[:, 8 * q : 8 * q + 8, dlo, :])
+                for y in range(0, 8, 4):
+                    nc.sync.dma_start(out=xs[:, y : y + 4, :], in_=x1v[:, 8 * q + y : 8 * q + y + 4, dlo, :])
             else:
                 for a8 in range(8):
                     nc.sync.dma_start(out=xs[a8 : P : 8, :, :], in_=x2v[:, 8 * q : 8 * q + 8, a8, dlo, :])
@@ -113,18 +114,18 @@ def tile_mlpp_pa_kernel(tc, x, W_h, b_h, W_w, b_w, W_c, b_c, W_attn, b_attn, W_1
             )
 
         wattn = consts.tile([P, 2, 256], BF16, tag="wattn")
-        nc.sync.dma_start(out=wattn[:], in_=W_attn.rearrange("(k p) n -> p k n", p=P))
+        nc.gpsimd.dma_start(out=wattn[:], in_=W_attn.rearrange("(k p) n -> p k n", p=P))
         b1bc = consts.tile([P, C], BF16, tag="b1bc")
         tb = consts.tile([P, C], BF16, tag="tb")
-        nc.sync.dma_start(out=tb[0:16, 0:32], in_=b_w.rearrange("(w g) -> w g", g=32))
-        nc.sync.dma_start(out=tb[16:32, 0:32], in_=b_h.rearrange("(h g) -> h g", g=32))
-        nc.sync.dma_start(out=tb[32:33, :], in_=b_c.rearrange("(o c) -> o c", o=1))
+        nc.gpsimd.dma_start(out=tb[0:16, 0:32], in_=b_w.rearrange("(w g) -> w g", g=32))
+        nc.gpsimd.dma_start(out=tb[16:32, 0:32], in_=b_h.rearrange("(h g) -> h g", g=32))
+        nc.gpsimd.dma_start(out=tb[32:33, :], in_=b_c.rearrange("(o c) -> o c", o=1))
         tba = consts.tile([P, P], BF16, tag="tba")
         nc.vector.memset(tba[:], 0.0)
-        nc.sync.dma_start(out=tba[0:2, :], in_=b_attn.rearrange("(k p) -> k p", p=P))
+        nc.gpsimd.dma_start(out=tba[0:2, :], in_=b_attn.rearrange("(k p) -> k p", p=P))
 
-        def in_relayout(which, dlo, q, eng_copy, piece=0, pieces=1):
-            if q == 0 and piece == 0:
+        def in_relayout(which, dlo, q, eng_copy, piece=0, pieces=1, ys=slice(0, 8)):
+            if ("rl", which, dlo) not in st:
                 if which == 1 and dlo == 0:
                     rl = two.tile([P, 8192], BF16, tag="a", align_bytes=64)
                 else:
@@ -135,8 +136,8 @@ def tile_mlpp_pa_kernel(tc, x, W_h, b_h, W_w, b_w, W_c, b_c, W_attn, b_attn, W_1
             xs = st["xs", which, dlo, q]
             ls = slice(16 // pieces * piece, 16 // pieces * (piece + 1))
             eng_copy(
-                out=rl4[:, ls, :, :],
-                in_=xs.rearrange("p y (l g) -> p l y g", l=16, g=32)[:, ls, :, :],
+                out=rl4[:, ls, ys, :],
+                in_=xs.rearrange("p y (l g) -> p l y g", l=16, g=32)[:, ls, ys, :],
             )
 
         def in_transpose(which, dlo, lp, tag, halves=(0, 1)):
@@ -466,10 +467,20 @@ def tile_mlpp_pa_kernel(tc, x, W_h, b_h, W_w, b_w, W_c, b_c, W_attn, b_attn, W_1
         load_w(2, W_c)
         load_w(3, W_1)
 
-        in_relayout(0, 0, 0, ve_copy)
+        in_relayout(0, 0, 0, ve_copy, ys=slice(0, 4))
+        in_relayout(0, 0, 0, ve_copy, ys=slice(4, 8))
         for lp in range(8):
             in_transpose(0, 0, lp, ptag(), (0,))
-        in_relayout(0, 0, 1, ve_copy)
+        in_relayout(0, 0, 1, ve_copy, ys=slice(0, 4))
+        in_relayout(0, 0, 1, ve_copy, ys=slice(4, 8))
+        nc.vector.tensor_copy(
+            out=rtab4[0:32, :, :, :],
+            in_=tb[0:32, 0:32].unsqueeze(2).unsqueeze(3).to_broadcast([32, 32, 16, 2]),
+        )
+        nc.vector.tensor_copy(
+            out=rtab4[32:33, :, :, :],
+            in_=tb[32:33, :].rearrange("p (l g) -> p g l", l=16, g=32).unsqueeze(3).to_broadcast([1, 32, 16, 2]),
+        )
         for lp in range(8):
             in_transpose(0, 0, lp, None, (1,))
             in_evac(0, 0, lp, sc_copy)
@@ -499,14 +510,6 @@ def tile_mlpp_pa_kernel(tc, x, W_h, b_h, W_w, b_w, W_c, b_c, W_attn, b_attn, W_1
             b_xh_evac(0, xh0[i], ve_copy if i < 2 else sc_copy)
             if i == 1:
                 in_quant(1, 0, 0)
-        nc.vector.tensor_copy(
-            out=rtab4[0:32, :, :, :],
-            in_=tb[0:32, 0:32].unsqueeze(2).unsqueeze(3).to_broadcast([32, 32, 16, 2]),
-        )
-        nc.vector.tensor_copy(
-            out=rtab4[32:33, :, :, :],
-            in_=tb[32:33, :].rearrange("p (l g) -> p g l", l=16, g=32).unsqueeze(3).to_broadcast([1, 32, 16, 2]),
-        )
         for h8 in range(8):
             b_xw(0, h8, ptag())
             b_add(0, h8)
@@ -530,12 +533,12 @@ def tile_mlpp_pa_kernel(tc, x, W_h, b_h, W_w, b_w, W_c, b_c, W_attn, b_attn, W_1
                 b_xh(1, gb, ptag())
                 b_xh_evac(1, gb, ve_copy)
                 if gb == 0:
-                    xc_quant(0, 0)
-                if gb == 1:
                     in_quant(1, 0, 1)
-                if gb == 3:
+                if gb == 1:
+                    xc_quant(0, 0)
+                if gb == 2:
                     xc_quant(0, 1)
-                if gb == 5:
+                if gb == 3:
                     weight_quant(3)
                 if gb % 2 == 0:
                     relayout(0, gb // 2, (sc_copy, sc_copy), 4)
@@ -578,14 +581,7 @@ def tile_mlpp_pa_kernel(tc, x, W_h, b_h, W_w, b_w, W_c, b_c, W_attn, b_attn, W_1
         load_xs(1, 1, 0)
         load_xs(1, 1, 1)
         i0[7][3].append(lambda: relayout(1, 0, (ve_copy, sc_copy), 4))
-        side = (
-            mix(xw_jobs(1), i0)
-            + mix(tr_jobs(1), c1 + i1)
-            + xh_jobs(2)
-            + mix(xw_jobs(2), ic_jobs(2) + xh_jobs(3))
-            + mix(tr_jobs(2), xw_jobs(3))
-            + mix(tr_jobs(3), ic_jobs(3))
-        )
+        side = (mix(xw_jobs(1), i0) + mix(tr_jobs(1), c1 + i1) + xh_jobs(2) + mix(xw_jobs(2), mix(ic_jobs(2), xh_jobs(3))) + mix(xw_jobs(3), tr_jobs(2)) + mix(tr_jobs(3), ic_jobs(3)))
 
         NT = 32
         taken = 0

@@ -91,7 +91,7 @@ def tile_mlpp_pa_kernel(tc, x, W_h, b_h, W_w, b_w, W_c, b_c, W_attn, b_attn, W_1
 
         def weight_prep(i, eng_copy):
             if i % 2 == 0:
-                wg = one.tile([P, 2048], BF16, tag="ghid", align_bytes=64)
+                wg = two.tile([P, 2048], BF16, tag="ghid", align_bytes=64)
             else:
                 wg = two.tile([P, 2048], BF16, tag="cc", align_bytes=64)
             st["wg", i] = wg
@@ -377,21 +377,18 @@ def tile_mlpp_pa_kernel(tc, x, W_h, b_h, W_w, b_w, W_c, b_c, W_attn, b_attn, W_1
             st["pht", j] = pht
 
         def s2c(j):
-            if j % 2 == 0:
-                ghid = one.tile([P, 2048], BF16, tag="ghid", align_bytes=64)
-                st["ghid", j // 2] = ghid
-            ghid = st["ghid", j // 2]
-            pr = j % 2
+            ghid = two.tile([P, 1024], BF16, tag="ghid", align_bytes=64)
+            st["ghid", j] = ghid
             nc.scalar.copy(
-                out=ghid[:].bitcast(F32)[:, pr * C : (pr + 1) * C].rearrange("p (i r u) -> p i r u", i=2, r=P, u=2),
+                out=ghid[:].bitcast(F32).rearrange("p (i r u) -> p i r u", i=2, r=P, u=2),
                 in_=st["pht", j][:].rearrange("p (i u r) -> p i r u", i=2, u=2, r=P),
             )
 
-        def qh(m):
-            chid = two.tile([P, C], U32, tag="chid", align_bytes=64)
-            shid = two.tile([P, C], U8, tag="shid", align_bytes=64)
-            nc.vector.quantize_mx(out=chid[:].bitcast(FP8X4), scales=shid[:], in_=st["ghid", m][:])
-            st["chid", m] = (chid, shid)
+        def qh(j):
+            chid = two.tile([P, 2 * P], U32, tag="chid", align_bytes=64)
+            shid = two.tile([P, 2 * P], U8, tag="shid", align_bytes=64)
+            nc.vector.quantize_mx(out=chid[:].bitcast(FP8X4), scales=shid[:], in_=st["ghid", j][:])
+            st["chid", j] = (chid, shid)
 
         def gx(n):
             s, dlo, hh, d8 = where(n)
@@ -407,8 +404,8 @@ def tile_mlpp_pa_kernel(tc, x, W_h, b_h, W_w, b_w, W_c, b_c, W_attn, b_attn, W_1
             st["xpb", n] = xpb
 
         def pe3(n, tag="pf"):
-            chid, shid = st["chid", n // 4]
-            j = n % 4
+            chid, shid = st["chid", n // 2]
+            j = n % 2
             rc, rs = wslice(3, 0, C)
             pf = bank(tag)
             nc.tensor.matmul_mx(
@@ -528,10 +525,10 @@ def tile_mlpp_pa_kernel(tc, x, W_h, b_h, W_w, b_w, W_c, b_c, W_attn, b_attn, W_1
         for g0 in range(0, 8, 2):
             for gb in range(g0, g0 + 2):
                 b_t(0, gb, ptag())
-                b_t_evac(0, gb, sc_copy)
+                b_t_evac(0, gb, sc_copy if gb % 2 else ve_copy)
             for gb in range(g0, g0 + 2):
                 b_xh(1, gb, ptag())
-                b_xh_evac(1, gb, ve_copy)
+                b_xh_evac(1, gb, ve_copy if gb % 2 else sc_copy)
                 if gb == 0:
                     in_quant(1, 0, 1)
                 if gb == 1:
@@ -581,7 +578,7 @@ def tile_mlpp_pa_kernel(tc, x, W_h, b_h, W_w, b_w, W_c, b_c, W_attn, b_attn, W_1
         load_xs(1, 1, 0)
         load_xs(1, 1, 1)
         i0[7][3].append(lambda: relayout(1, 0, (ve_copy, sc_copy), 4))
-        side = (mix(xw_jobs(1), i0) + mix(tr_jobs(1), c1 + i1) + xh_jobs(2) + mix(xw_jobs(2), mix(ic_jobs(2), xh_jobs(3))) + mix(xw_jobs(3), tr_jobs(2)) + mix(tr_jobs(3), ic_jobs(3)))
+        side = (mix(xw_jobs(1), i0) + mix(tr_jobs(1), c1 + i1) + xh_jobs(2) + mix(xw_jobs(2), ic_jobs(2) + xh_jobs(3)) + mix(xw_jobs(3), tr_jobs(2)) + mix(tr_jobs(3), ic_jobs(3)))
 
         NT = 32
         taken = 0
@@ -600,7 +597,7 @@ def tile_mlpp_pa_kernel(tc, x, W_h, b_h, W_w, b_w, W_c, b_c, W_attn, b_attn, W_1
         att(0, 0)
         att(0, 1)
         pe1(0)
-        for c in range(NT + 7):
+        for c in range(NT + 5):
             pair = (c - 2) // 2
             hid_due = c % 2 == 0 and 0 <= pair < NT // 2
             room = 5
@@ -612,8 +609,6 @@ def tile_mlpp_pa_kernel(tc, x, W_h, b_h, W_w, b_w, W_c, b_c, W_attn, b_attn, W_1
                 jobs.append(job)
                 taken += 1
             flush(0)
-            if c % 4 == 1 and 0 <= (c - 5) // 4 < NT // 4:
-                qh((c - 5) // 4)
             if c < NT:
                 v1(c)
             runs = [("T", lambda: pe2(pair), lambda: s2c(pair), [], -1)] if hid_due else []
@@ -624,8 +619,10 @@ def tile_mlpp_pa_kernel(tc, x, W_h, b_h, W_w, b_w, W_c, b_c, W_attn, b_attn, W_1
                 if i < 2 and c + 1 < NT:
                     att(c + 1, i)
             flush(0)
-            if 0 <= c - 6 < NT:
-                v3(c - 6)
+            if 0 <= c - 4 < NT:
+                v3(c - 4)
+            if c % 2 == 1 and 0 <= (c - 3) // 2 < NT // 2:
+                qh((c - 3) // 2)
             if c < NT:
                 v2(c)
             for j in jobs:
@@ -641,8 +638,8 @@ def tile_mlpp_pa_kernel(tc, x, W_h, b_h, W_w, b_w, W_c, b_c, W_attn, b_attn, W_1
                     fill(j)
             if c + 1 < NT:
                 pe1(c + 1)
-            if 0 <= c - 5 < NT:
-                pe3(c - 5, "ss" if taken == len(side) else "pf")
-            if 0 <= c - 4 < NT:
-                gx(c - 4)
+            if 0 <= c - 3 < NT:
+                pe3(c - 3, "ss" if taken == len(side) else "pf")
+            if 0 <= c - 2 < NT:
+                gx(c - 2)
         assert taken == len(side)

from contextlib import ExitStack

import concourse.mybir as mybir
from concourse.masks import make_identity

F32 = mybir.dt.float32
BF16 = mybir.dt.bfloat16
U32 = mybir.dt.uint32
U8 = mybir.dt.uint8
FP8X4 = mybir.dt.float8_e4m3fn_x4
ADD = mybir.AluOpType.add
MULT = mybir.AluOpType.mult

P = 128
C = 512
FLOPS = 4 * 2 * 4096 * 512 * 512 + 2 * 8192 * 256 * 256


def tile_mlpp_pa_kernel(tc, x, W_h, b_h, W_w, b_w, W_c, b_c, W_attn, b_attn, W_1, b_1, out):
    nc = tc.nc
    with ExitStack() as ctx:
        ctx.enter_context(tc.manual_schedule())
        consts = ctx.enter_context(tc.tile_pool(name="consts", bufs=1))
        xsp = ctx.enter_context(tc.tile_pool(name="xsp", bufs=2))
        one = ctx.enter_context(tc.tile_pool(name="one", bufs=1))
        two = ctx.enter_context(tc.tile_pool(name="two", bufs=2))
        three = ctx.enter_context(tc.tile_pool(name="three", bufs=3))
        outp = ctx.enter_context(tc.tile_pool(name="outp", bufs=6))
        five = ctx.enter_context(tc.tile_pool(name="five", bufs=4))
        ps1 = ctx.enter_context(tc.psum_pool(name="ps1", bufs=1))
        ps5 = ctx.enter_context(tc.psum_pool(name="ps5", bufs=4))
        ps2 = ctx.enter_context(tc.psum_pool(name="ps2", bufs=2))

        def bank(tag, dtype=F32, cols=C):
            if tag == "ss":
                t = ps5.tile([P, cols], dtype, name="bk_ss", tag="ss")
            elif tag == "pa":
                t = ps2.tile([P, cols], dtype, name="bk_pa", tag="pa")
            else:
                t = ps1.tile([P, cols], dtype, name="bk_" + tag, tag=tag)
            return t

        xnv = x.rearrange("b (k h) w d c -> k (b h w) (d c)", k=2)
        x1v = x.rearrange("b h w (a e) c -> (b w a) h e c", e=2)
        x2v = x.rearrange("b h w (a e) c -> (b h) w a e c", e=2)
        outv = out.rearrange("b (k h) w d c -> k (b h w) d c", k=2)

        st = {}

        ident_f = consts.tile([P, P], F32, tag="ident_f")
        make_identity(nc, ident_f[:])
        ident_b = consts.tile([P, P], BF16, tag="ident_b")
        make_identity(nc, ident_b[:])

        def load_x2_first():
            xbig = two.tile([P, 16, C], BF16, tag="xn", align_bytes=64)
            for q in range(2):
                for a8 in range(8):
                    nc.sync.dma_start(
                        out=xbig[a8 : P : 8, 8 * q : 8 * q + 8, :], in_=x2v[:, 8 * q : 8 * q + 8, a8, 0, :]
                    )
                st["xs", 1, 0, q] = xbig[:, 8 * q : 8 * q + 8, :]

        def load_xs(which, dlo, q):
            xs = xsp.tile([P, 8, C], BF16, tag="xs")
            if which == 0:
                for y in range(0, 8, 4):
                    nc.sync.dma_start(out=xs[:, y : y + 4, :], in_=x1v[:, 8 * q + y : 8 * q + y + 4, dlo, :])
            else:
                for a8 in range(8):
                    nc.sync.dma_start(out=xs[a8 : P : 8, :, :], in_=x2v[:, 8 * q : 8 * q + 8, a8, dlo, :])
            st["xs", which, dlo, q] = xs[:]

        wraw = two.tile([P, 8192], BF16, tag="s2", align_bytes=64)
        wrv = wraw[:].rearrange("p (i t n) -> p i t n", i=4, t=4, n=C)
        wcodes = consts.tile([P, 2048], U32, tag="wcodes", align_bytes=64)
        wscl = consts.tile([P, 2048], U8, tag="wscl", align_bytes=64)

        def load_w(i, w_ap):
            for u in range(2):
                nc.sync.dma_start(
                    out=wrv[:, i, 2 * u : 2 * u + 2, :],
                    in_=w_ap[256 * u : 256 * u + 256, :].rearrange("(q e) n -> q e n", e=2),
                )

        load_xs(0, 0, 0)
        load_xs(0, 0, 1)
        load_x2_first()
        load_w(0, W_h)
        load_w(1, W_w)

        def weight_prep(i, eng_copy):
            if i % 2 == 0:
                wg = two.tile([P, 2048], BF16, tag="ghid", align_bytes=64)
            else:
                wg = two.tile([P, 2048], BF16, tag="cc", align_bytes=64)
            st["wg", i] = wg
            eng_copy(
                out=wg[:].rearrange("p (n i t) -> p n t i", n=P, i=4, t=4),
                in_=wrv[:, i].rearrange("p t (n i) -> p n t i", n=P, i=4),
            )

        def weight_quant(i):
            nc.vector.quantize_mx(
                out=wcodes[:, i * C : (i + 1) * C].bitcast(FP8X4),
                scales=wscl[:, i * C : (i + 1) * C],
                in_=st["wg", i][:],
            )

        def wslice(i, c0, n):
            return (
                wcodes[:, i * C + c0 : i * C + c0 + n].bitcast(FP8X4),
                wscl[:, i * C + c0 : i * C + c0 + n],
            )

        wattn = consts.tile([P, 2, 256], BF16, tag="wattn")
        nc.gpsimd.dma_start(out=wattn[:], in_=W_attn.rearrange("(k p) n -> p k n", p=P))
        b1bc = consts.tile([P, C], BF16, tag="b1bc")
        tb = consts.tile([P, C], BF16, tag="tb")
        nc.gpsimd.dma_start(out=tb[0:16, 0:32], in_=b_w.rearrange("(w g) -> w g", g=32))
        nc.gpsimd.dma_start(out=tb[16:32, 0:32], in_=b_h.rearrange("(h g) -> h g", g=32))
        nc.gpsimd.dma_start(out=tb[32:33, :], in_=b_c.rearrange("(o c) -> o c", o=1))
        tba = consts.tile([P, P], BF16, tag="tba")
        nc.vector.memset(tba[:], 0.0)
        nc.gpsimd.dma_start(out=tba[0:2, :], in_=b_attn.rearrange("(k p) -> k p", p=P))

        def in_relayout(which, dlo, q, eng_copy, piece=0, pieces=1, ys=slice(0, 8)):
            if ("rl", which, dlo) not in st:
                if which == 1 and dlo == 0:
                    rl = two.tile([P, 8192], BF16, tag="a", align_bytes=64)
                else:
                    rl = one.tile([P, 8192], BF16, tag="rl")
                st["rl", which, dlo] = rl
            rl = st["rl", which, dlo]
            rl4 = rl[:, q * 4096 : (q + 1) * 4096].rearrange("p (l y g) -> p l y g", l=16, y=8, g=32)
            xs = st["xs", which, dlo, q]
            ls = slice(16 // pieces * piece, 16 // pieces * (piece + 1))
            eng_copy(
                out=rl4[:, ls, ys, :],
                in_=xs.rearrange("p y (l g) -> p l y g", l=16, g=32)[:, ls, ys, :],
            )

        def in_transpose(which, dlo, lp, tag, halves=(0, 1)):
            rlw = st["rl", which, dlo][:].bitcast(F32)
            if 0 in halves:
                pt = bank(tag)
                st["pt", which, dlo, lp] = pt
            pt = st["pt", which, dlo, lp]
            for li in range(2):
                for u in halves:
                    w0 = u * 2048 + (2 * lp + li) * P
                    s0 = (2 * li + u) * P
                    nc.tensor.transpose(pt[:, s0 : s0 + P], rlw[:, w0 : w0 + P], ident_f[:])

        def in_evac(which, dlo, lp, copy):
            if lp == 0:
                if which == 1 and dlo == 0:
                    gr = two.tile([P, 8192], BF16, tag="a", align_bytes=64)
                else:
                    gr = one.tile([P, 8192], BF16, tag="gr", align_bytes=64)
                st["gr", which, dlo] = gr
            gr = st["gr", which, dlo]
            grw = gr[:].bitcast(F32).rearrange("p (y l a u) -> p y l a u", y=16, l=16, a=8, u=2)
            pt = st["pt", which, dlo, lp]
            for li in range(2):
                half_bank = pt[:, li * 256 : (li + 1) * 256]
                src = half_bank.rearrange("p (u y a) -> p y a u", u=2, y=16, a=8)
                copy(out=grw[:, :, 2 * lp + li, :, :], in_=src)

        def in_quant(which, dlo, qn):
            if qn == 0:
                if which == 0:
                    codes = one.tile([P, 2048], U32, tag="ch", align_bytes=64)
                    scl = one.tile([P, 2048], U8, tag="sh", align_bytes=64)
                else:
                    codes = one.tile([P, 2048], U32, tag="cw", align_bytes=64)
                    scl = one.tile([P, 2048], U8, tag="sw", align_bytes=64)
                st["codes", which, dlo] = (codes, scl)
            codes, scl = st["codes", which, dlo]
            nc.vector.quantize_mx(
                out=codes[:, qn * 1024 : (qn + 1) * 1024].bitcast(FP8X4),
                scales=scl[:, qn * 1024 : (qn + 1) * 1024],
                in_=st["gr", which, dlo][:, qn * 4096 : (qn + 1) * 4096],
            )

        xn = []

        def load_xn(k, dlo):
            if dlo == 0:
                xnk = two.tile([P, 8192], BF16, name="xn%d" % k, tag="xn", align_bytes=64)
                xn.append(xnk)
            nc.sync.dma_start(
                out=xn[k][:, dlo * 4096 : (dlo + 1) * 4096].rearrange("p (a c) -> p a c", a=8, c=C),
                in_=xnv[k].rearrange("p (a e c) -> p a e c", a=8, e=2, c=C)[:, :, dlo, :],
            )

        def xc_transpose(s, pr4, tag):
            dlo, hh = s // 2, s % 2
            xw32 = xn[hh][:].bitcast(F32)
            pt = bank(tag)
            for i in range(2):
                w0 = (8 * dlo + pr4 * 2 + i) * 256
                for u in range(2):
                    s0 = (2 * i + u) * P
                    nc.tensor.transpose(pt[:, s0 : s0 + P], xw32[:, w0 + u * P : w0 + (u + 1) * P], ident_f[:])
            st["pxc", s, pr4] = pt

        def xc_evac(s, pr4, copy):
            if pr4 == 0:
                gc = one.tile([P, 4096], BF16, tag="gc", align_bytes=64)
                st["gc", s] = gc
            gcw = st["gc", s][:].bitcast(F32)
            copy(
                out=gcw[:, pr4 * C : (pr4 + 1) * C].rearrange("p (i r u) -> p i r u", i=2, r=P, u=2),
                in_=st["pxc", s, pr4][:].rearrange("p (i u r) -> p i r u", i=2, u=2, r=P),
            )

        def xc_quant(s, half):
            if half == 0:
                cc = two.tile([P, 1024], U32, tag="cc", align_bytes=64)
                sc = two.tile([P, 1024], U8, tag="sc", align_bytes=64)
                st["cc", s] = (cc, sc)
            cc, sc = st["cc", s]
            nc.vector.quantize_mx(
                out=cc[:, half * C : (half + 1) * C].bitcast(FP8X4),
                scales=sc[:, half * C : (half + 1) * C],
                in_=st["gc", s][:, half * 2048 : (half + 1) * 2048],
            )

        def b_xh(s, k, tag):
            dlo, hh = s // 2, s % 2
            ch, sh = st["codes", 0, dlo]
            hb, wb = k // 4, k % 4
            rc, rs = wslice(0, hh * 256 + hb * P, P)
            ph = bank(tag)
            for wi in range(4):
                w = 4 * wb + wi
                nc.tensor.matmul_mx(
                    out=ph[:, wi * P : (wi + 1) * P],
                    lhsT=ch[:, w * P : (w + 1) * P].bitcast(FP8X4),
                    lhsT_scale=sh[:, w * P : (w + 1) * P],
                    rhs=rc,
                    rhs_scale=rs,
                    start=True,
                    stop=True,
                )
            st["ph", s, k] = ph

        def b_xh_evac(s, k, copy):
            if k == 0:
                s2 = two.tile([P, 4096], F32, tag="s2", align_bytes=64)
                st["s2", s] = s2
            s2v = st["s2", s][:].rearrange("p (g h w) -> p g h w", g=32, h=8, w=16)
            hb, wb = k // 4, k % 4
            copy(
                out=s2v[:, :, 4 * hb : 4 * hb + 4, 4 * wb : 4 * wb + 4],
                in_=st["ph", s, k][:].rearrange("p (w h g) -> p g h w", w=4, h=4, g=32),
            )

        def b_xw(s, h8, tag):
            dlo, hh = s // 2, s % 2
            cw, sw = st["codes", 1, dlo]
            rc, rs = wslice(1, 0, C)
            h = 8 * hh + h8
            pw = bank(tag)
            nc.tensor.matmul_mx(
                out=pw[:],
                lhsT=cw[:, h * P : (h + 1) * P].bitcast(FP8X4),
                lhsT_scale=sw[:, h * P : (h + 1) * P],
                rhs=rc,
                rhs_scale=rs,
                start=True,
                stop=True,
            )
            st["pw", s, h8] = pw

        def b_add(s, h8):
            s2v = st["s2", s][:].rearrange("p (g h w) -> p g h w", g=32, h=8, w=16)
            nc.vector.tensor_tensor(
                out=s2v[:, :, h8, :],
                in0=st["pw", s, h8][:].rearrange("p (w g) -> p g w", w=16, g=32),
                in1=s2v[:, :, h8, :],
                op=ADD,
            )

        def b_t(s, gb, tag):
            s2 = st["s2", s]
            pst = bank(tag)
            nc.tensor.matmul(
                out=pst[:],
                lhsT=st["sel", s % 2][:].rearrange("p a w -> p (a w)"),
                rhs=rtab[:, gb * 64 : (gb + 1) * 64, :].unsqueeze(2).to_broadcast([P, 64, 4, 2]),
                start=True,
                stop=False,
            )
            for gi in range(4):
                g = 4 * gb + gi
                nc.tensor.matmul(
                    out=pst[:, gi * P : (gi + 1) * P],
                    lhsT=s2[:, g * P : (g + 1) * P],
                    rhs=ident_f[:],
                    is_transpose=True,
                    start=False,
                    stop=(gi == 3),
                )
            st["pst", s, gb] = pst

        def b_t_evac(s, gb, copy):
            if gb == 0:
                a = two.tile([P, 4096], F32, tag="a", align_bytes=64)
                st["a", s] = a
            av = st["a", s][:].rearrange("p (a l g) -> p a l g", a=8, l=16, g=32)
            copy(
                out=av[:, :, :, 4 * gb : 4 * gb + 4],
                in_=st["pst", s, gb][:].rearrange("p (g l a) -> p a l g", g=4, l=16, a=8),
            )

        def where(n):
            s = n // 8
            return s, s // 2, s % 2, n % 8

        def pe1(n):
            s, dlo, hh, d8 = where(n)
            cc, sc = st["cc", s]
            rc, rs = wslice(2, 0, C)
            pc = bank("pc")
            nc.tensor.matmul_mx(
                out=pc[:],
                lhsT=cc[:, d8 * P : (d8 + 1) * P].bitcast(FP8X4),
                lhsT_scale=sc[:, d8 * P : (d8 + 1) * P],
                rhs=rc,
                rhs_scale=rs,
                start=True,
                stop=True,
            )
            st["pc", n] = pc

        def att(n, k):
            s, dlo, hh, d8 = where(n)
            if k == 0:
                pa = bank("pa")
                st["pa", n] = pa
            nc.tensor.matmul(
                out=st["pa", n][:],
                lhsT=wattn[:, k, hh * P : (hh + 1) * P],
                rhs=xn[k][:, (8 * dlo + d8) * C : (8 * dlo + d8 + 1) * C],
                start=(k == 0),
                stop=(k == 1),
            )

        def v1(n):
            s, dlo, hh, d8 = where(n)
            if n % 2 == 0:
                hidn = two.tile([P, 2 * C], BF16, tag="hidn")
                st["hidn", n // 2] = hidn
            hidn = st["hidn", n // 2]
            bsum = two.tile([P, C], F32, tag="bsum")
            nc.vector.tensor_tensor(out=bsum[:], in0=st["pc", n][:], in1=st["a", s][:, d8 * C : (d8 + 1) * C], op=ADD)
            st["bsum", n] = bsum

        def v2(n):
            hh = (n // 8) % 2
            nc.vector.scalar_tensor_tensor(
                out=st["hidn", n // 2][:, (n % 2) * C : (n % 2 + 1) * C],
                in0=st["pa", n][:],
                scalar=ap1[:, hh : hh + 1],
                in1=st["bsum", n][:],
                op0=ADD,
                op1=MULT,
            )

        def pe2(j):
            hidw = st["hidn", j][:].bitcast(F32)
            pht = bank("ss")
            for q in range(4):
                nc.tensor.transpose(pht[:, q * P : (q + 1) * P], hidw[:, q * P : (q + 1) * P], ident_f[:])
            st["pht", j] = pht

        def s2c(j):
            ghid = two.tile([P, 1024], BF16, tag="ghid", align_bytes=64)
            st["ghid", j] = ghid
            nc.scalar.copy(
                out=ghid[:].bitcast(F32).rearrange("p (i r u) -> p i r u", i=2, r=P, u=2),
                in_=st["pht", j][:].rearrange("p (i u r) -> p i r u", i=2, u=2, r=P),
            )

        def qh(j):
            chid = two.tile([P, 2 * P], U32, tag="chid", align_bytes=64)
            shid = two.tile([P, 2 * P], U8, tag="shid", align_bytes=64)
            nc.vector.quantize_mx(out=chid[:].bitcast(FP8X4), scales=shid[:], in_=st["ghid", j][:])
            st["chid", j] = (chid, shid)

        def gx(n):
            s, dlo, hh, d8 = where(n)
            e0 = (8 * dlo + d8) * C
            xpb = five.tile([P, C], F32, tag="xpb")
            for c0 in (0, 256):
                nc.gpsimd.tensor_tensor(
                    out=xpb[:, c0 : c0 + 256],
                    in0=xn[hh][:, e0 + c0 : e0 + c0 + 256],
                    in1=b1bc[:, c0 : c0 + 256],
                    op=ADD,
                )
            st["xpb", n] = xpb

        def pe3(n, tag="pf"):
            chid, shid = st["chid", n // 2]
            j = n % 2
            rc, rs = wslice(3, 0, C)
            pf = bank(tag)
            nc.tensor.matmul_mx(
                out=pf[:],
                lhsT=chid[:, j * P : (j + 1) * P].bitcast(FP8X4),
                lhsT_scale=shid[:, j * P : (j + 1) * P],
                rhs=rc,
                rhs_scale=rs,
                start=True,
                stop=True,
            )
            st["pf", n] = pf

        def v3(n):
            s, dlo, hh, d8 = where(n)
            d = 2 * d8 + dlo
            o = outp.tile([P, C], F32, tag="o")
            nc.vector.tensor_tensor(out=o[:], in0=st["pf", n][:], in1=st["xpb", n][:], op=ADD)
            nc.sync.dma_start(out=outv[hh][:, d, :], in_=o[:])

        sc_copy = nc.scalar.copy
        ve_copy = nc.vector.tensor_copy
        rot = {"n": 0}
        ring = ("ss", "ss", "ss", "ss", "pa", "pa", "pc", "pf")

        def ptag():
            rot["n"] += 1
            return ring[(rot["n"] - 1) % len(ring)]

        def relayout(which, j, copies, pieces):
            for q in range(2):
                in_relayout(which, 1, q, copies[q], j, pieces)

        rtab = consts.tile([P, C, 2], BF16, tag="rtab")
        nc.vector.memset(rtab[:], 0.0)
        rtab4 = rtab[:].rearrange("p (g l) b -> p g l b", g=32, l=16)
        selw = consts.tile([P, 8, 16], BF16, tag="selw")
        nc.vector.tensor_tensor(
            out=selw[:],
            in0=ident_b[:, 0:16].unsqueeze(1).to_broadcast([P, 8, 16]),
            in1=ident_b[:, 32:33].unsqueeze(1).to_broadcast([P, 8, 16]),
            op=ADD,
        )
        for hh in range(2):
            sel = consts.tile([P, 8, 16], BF16, name="sel%d" % hh, tag="sel%d" % hh)
            nc.vector.tensor_tensor(
                out=sel[:],
                in0=selw[:],
                in1=ident_b[:, 16 + 8 * hh : 24 + 8 * hh].unsqueeze(2).to_broadcast([P, 8, 16]),
                op=ADD,
            )
            st["sel", hh] = sel
        warm = consts.tile([P, 8], BF16, tag="warm")
        nc.scalar.copy(out=warm[:], in_=ident_b[:, 0:8])
        load_xn(0, 0)
        load_w(2, W_c)
        load_w(3, W_1)

        in_relayout(0, 0, 0, ve_copy, ys=slice(0, 4))
        in_relayout(0, 0, 0, ve_copy, ys=slice(4, 8))
        for lp in range(8):
            in_transpose(0, 0, lp, ptag(), (0,))
        in_relayout(0, 0, 1, ve_copy, ys=slice(0, 4))
        in_relayout(0, 0, 1, ve_copy, ys=slice(4, 8))
        nc.vector.tensor_copy(
            out=rtab4[0:32, :, :, :],
            in_=tb[0:32, 0:32].unsqueeze(2).unsqueeze(3).to_broadcast([32, 32, 16, 2]),
        )
        nc.vector.tensor_copy(
            out=rtab4[32:33, :, :, :],
            in_=tb[32:33, :].rearrange("p (l g) -> p g l", l=16, g=32).unsqueeze(3).to_broadcast([1, 32, 16, 2]),
        )
        for lp in range(8):
            in_transpose(0, 0, lp, None, (1,))
            in_evac(0, 0, lp, sc_copy)
        in_relayout(1, 0, 0, ve_copy)
        for lp in range(8):
            in_transpose(1, 0, lp, ptag(), (0,))
        in_relayout(1, 0, 1, ve_copy)
        weight_prep(0, ve_copy)
        in_quant(0, 0, 0)
        weight_quant(0)
        in_quant(0, 0, 1)
        for lp in range(8):
            in_transpose(1, 0, lp, None, (1,))
            in_evac(1, 0, lp, sc_copy)
        weight_prep(1, ve_copy)
        weight_quant(1)
        load_xs(0, 1, 0)
        load_xs(0, 1, 1)
        load_xn(1, 0)
        load_xn(0, 1)
        load_xn(1, 1)
        b1bc = consts.tile([P, C], BF16, tag="b1bc")
        nc.sync.dma_start(out=b1bc[:], in_=b_1.partition_broadcast(P))
        xh0 = (0, 1, 4, 5, 2, 3, 6, 7)
        for i in range(8):
            b_xh(0, xh0[i], ptag())
            b_xh_evac(0, xh0[i], ve_copy if i < 2 else sc_copy)
            if i == 1:
                in_quant(1, 0, 0)
        for h8 in range(8):
            b_xw(0, h8, ptag())
            b_add(0, h8)
            if h8 == 0:
                weight_prep(2, sc_copy)
                weight_prep(3, sc_copy)
            if h8 in (3, 7):
                for q4 in (h8 // 2 - 1, h8 // 2):
                    xc_transpose(0, q4, ptag())
                    xc_evac(0, q4, sc_copy)
        weight_quant(2)
        pta = bank(ptag(), BF16, P)
        nc.tensor.transpose(pta[:], tba[:], ident_b[:])
        ap1 = consts.tile([P, 2], F32, tag="ap1")
        nc.vector.tensor_scalar_add(out=ap1[:], in0=pta[:, 0:2], scalar1=1.0)
        for g0 in range(0, 8, 2):
            for gb in range(g0, g0 + 2):
                b_t(0, gb, ptag())
                b_t_evac(0, gb, sc_copy if gb % 2 else ve_copy)
            for gb in range(g0, g0 + 2):
                b_xh(1, gb, ptag())
                b_xh_evac(1, gb, ve_copy if gb % 2 else sc_copy)
                if gb == 0:
                    in_quant(1, 0, 1)
                if gb == 1:
                    xc_quant(0, 0)
                if gb == 2:
                    xc_quant(0, 1)
                if gb == 3:
                    weight_quant(3)
                if gb % 2 == 0:
                    relayout(0, gb // 2, (sc_copy, sc_copy), 4)

        def tr_jobs(s):
            return [("T", lambda gb=gb: b_t(s, gb, "ss"), lambda gb=gb: b_t_evac(s, gb, sc_copy), [], s) for gb in range(8)]

        def in_fill(which, lp):
            in_transpose(which, 1, lp, "ss")
            if which == 1 and lp in (0, 2, 4):
                relayout(1, lp // 2 + 1, (ve_copy, sc_copy), 4)

        def in_jobs(which):
            jobs = [
                ("T", lambda lp=lp: in_fill(which, lp), lambda lp=lp: in_evac(which, 1, lp, sc_copy), [], -1)
                for lp in range(8)
            ]
            jobs[7][3].extend([lambda: in_quant(which, 1, 0), lambda: in_quant(which, 1, 1)])
            return jobs

        def ic_jobs(s):
            jobs = [("T", lambda q=q: xc_transpose(s, q, "ss"), lambda q=q: xc_evac(s, q, sc_copy), [], -1) for q in range(4)]
            jobs[1][3].append(lambda: xc_quant(s, 0))
            jobs[3][3].append(lambda: xc_quant(s, 1))
            return jobs

        def xh_jobs(s):
            return [("M", lambda k=k: b_xh(s, k, "ss"), lambda k=k: b_xh_evac(s, k, sc_copy), [], s) for k in range(8)]

        def xw_jobs(s):
            return [("W", lambda h8=h8: b_xw(s, h8, "ss"), lambda h8=h8: b_add(s, h8), [], s) for h8 in range(8)]

        def mix(a, b):
            keyed = [((i + 0.5) / len(l), l[i]) for l in (a, b) for i in range(len(l))]
            return [job for key, job in sorted(keyed, key=lambda kj: kj[0])]

        c1 = ic_jobs(1)
        i0 = in_jobs(0)
        i1 = in_jobs(1)
        load_xs(1, 1, 0)
        load_xs(1, 1, 1)
        i0[7][3].append(lambda: relayout(1, 0, (ve_copy, sc_copy), 4))
        side = (mix(xw_jobs(1), i0) + mix(tr_jobs(1), c1 + i1) + xh_jobs(2) + mix(xw_jobs(2), ic_jobs(2) + xh_jobs(3)) + mix(xw_jobs(3), tr_jobs(2)) + mix(tr_jobs(3), ic_jobs(3)))

        NT = 32
        taken = 0
        adds = []
        pend = []

        def flush(n):
            while len(pend) > n:
                pend.pop(0)()

        def fill(job):
            flush(3)
            job[1]()
            pend.append(job[2])

        att(0, 0)
        att(0, 1)
        pe1(0)
        for c in range(NT + 5):
            pair = (c - 2) // 2
            hid_due = c % 2 == 0 and 0 <= pair < NT // 2
            room = 5
            jobs = []
            while taken < len(side) and len(jobs) < room:
                job = side[taken]
                if any(j[0] == "W" and j[4] == job[4] for j in jobs) and job[0] == "T":
                    break
                jobs.append(job)
                taken += 1
            flush(0)
            if c < NT:
                v1(c)
            runs = [("T", lambda: pe2(pair), lambda: s2c(pair), [], -1)] if hid_due else []
            runs = runs + [j for j in jobs if j[0] == "T"]
            for i in range(max(len(runs), 2)):
                if i < len(runs):
                    fill(runs[i])
                if i < 2 and c + 1 < NT:
                    att(c + 1, i)
            flush(0)
            if 0 <= c - 4 < NT:
                v3(c - 4)
            if c % 2 == 1 and 0 <= (c - 3) // 2 < NT // 2:
                qh((c - 3) // 2)
            if c < NT:
                v2(c)
            for j in jobs:
                if j[0] == "T":
                    for f in j[3]:
                        f()
            for j in jobs:
                if j[0] == "M":
                    fill(j)
            flush(0)
            for j in jobs:
                if j[0] == "W":
                    fill(j)
            if c + 1 < NT:
                pe1(c + 1)
            if 0 <= c - 3 < NT:
                pe3(c - 3, "ss" if taken == len(side) else "pf")
            if 0 <= c - 2 < NT:
                gx(c - 2)
        assert taken == len(side)
